import numpy as np
import ml_dtypes


def mxq(x, axis, fmt="e4m3"):
    dtype, down = {"e4m3": (ml_dtypes.float8_e4m3fn, 7), "e5m2": (ml_dtypes.float8_e5m2, 14)}[fmt]
    v = np.moveaxis(np.asarray(x, np.float32).astype(ml_dtypes.bfloat16).astype(np.float64), axis, -1)
    blocks = v.reshape(v.shape[:-1] + (-1, 32))
    amax = np.abs(blocks).max(-1, keepdims=True)
    byte = np.maximum(np.where(amax > 0, np.frexp(amax)[1] - 1 + 127, 0) - down, 1)
    scale = np.exp2(byte - 127.0)
    codes = (blocks / scale).astype(np.float32).astype(dtype).astype(np.float64)
    return np.moveaxis((codes * scale).reshape(v.shape), -1, axis)


WIDE = False


def mx_kscale(k):
    if not WIDE:
        return np.ones(k)
    levels = np.array([10, -10, 5, -5, 0])
    a = np.random.permutation(np.resize(levels, k // 512 * 4)).reshape(k // 512, 4)
    idx = np.arange(k)
    return np.exp2(a[idx // 512, idx % 128 // 32])


BF16 = ml_dtypes.bfloat16


def bf(x):
    return np.asarray(x, np.float32).astype(BF16)


def f64(x):
    return np.asarray(x).astype(np.float64)


B, N, D, H, G, P, F = 4, 1024, 512, 16, 4, 2, 512
LN_EPS = 1e-5


def erf(v):
    a = np.minimum(np.abs(v), 6.0)
    t = a.copy()
    tot = a.copy()
    n = 0.0
    while not np.all(t <= 1e-18 * tot):
        n += 1.0
        t = t * (2.0 * a * a / (2.0 * n + 1.0))
        tot = tot + t
    return np.sign(v) * (2.0 / np.sqrt(np.pi)) * np.exp(-a * a) * tot


def gelu(v):
    return 0.5 * v * (1.0 + erf(v / np.sqrt(2.0)))


def layernorm(x, g, b):
    m = x.mean(-1, keepdims=True)
    v = ((x - m) ** 2).mean(-1, keepdims=True)
    return (x - m) / np.sqrt(v + LN_EPS) * g + b


def setup_inputs():
    s = mx_kscale(D)
    return {"attended": bf(np.random.standard_normal((B, N, D)) * 0.35 * s),
            "hidden": bf(np.random.standard_normal((B, N, D))),
            "Wo": bf(np.random.standard_normal((D, D)) * 2.0 / np.sqrt(D) / s),
            "bo": bf(np.random.standard_normal(D) * 0.1),
            "ln2_g": bf(1.0 + 0.1 * np.random.standard_normal(D)),
            "ln2_b": bf(np.random.standard_normal(D) * 0.1),
            "W_ff1": bf(np.random.standard_normal((F, D)) / np.sqrt(D)),
            "b_ff1": bf(np.random.standard_normal(F) * 0.2)}


def reference(attended, hidden, Wo, bo, ln2_g, ln2_b, W_ff1, b_ff1):
    h = f64(hidden) + (mxq(f64(attended), 2, "e4m3") @ mxq(f64(Wo), 1, "e4m3").T) + f64(bo)
    n2 = layernorm(h, f64(ln2_g), f64(ln2_b))
    u = (mxq(n2, 2, "e4m3") @ mxq(f64(W_ff1), 1, "e4m3").T) + f64(b_ff1)
    return h, gelu(u)

@@ -1,0 +1,363 @@
+from contextlib import ExitStack
+
+import concourse.mybir as mybir
+from concourse.masks import make_identity
+
+F32 = mybir.dt.float32
+BF16 = mybir.dt.bfloat16
+U32 = mybir.dt.uint32
+U8 = mybir.dt.uint8
+FP8X4 = mybir.dt.float8_e4m3fn_x4
+ALU = mybir.AluOpType
+ACT = mybir.ActivationFunctionType
+
+P = 128
+D = 512
+TOKENS = 4096
+TILES = TOKENS // P
+GT = 4
+GROUPS = TILES // GT
+GW = GT * D
+LN_EPS = 1e-5
+
+FLOPS = 2 * 2 * TOKENS * D * D
+
+
+def tile_supervisedrefiner_pb_t_kernel(
+    tc, attended, hidden, Wo, bo, ln2_g, ln2_b, W_ff1, b_ff1, out_0, out_1
+):
+    nc = tc.nc
+    att_v = attended.flatten_outer_dims().rearrange("(p t) d -> p (t d)", t=TILES)
+    hid_v = hidden.flatten_outer_dims().rearrange("(p t) d -> p (t d)", t=TILES)
+    o0_v = out_0.flatten_outer_dims().rearrange("(p t) d -> p (t d)", t=TILES)
+    o1_v = out_1.flatten_outer_dims().rearrange("(p t) d -> p (t d)", t=TILES)
+
+    with ExitStack() as ctx:
+        ctx.enter_context(tc.manual_schedule())
+        const = ctx.enter_context(tc.tile_pool(name="const", bufs=1))
+        loads = ctx.enter_context(tc.tile_pool(name="loads", bufs=GROUPS))
+        work = ctx.enter_context(tc.tile_pool(name="work", bufs=2))
+        mm = ctx.enter_context(tc.psum_pool(name="mm", bufs=4))
+        xt = ctx.enter_context(tc.psum_pool(name="xt", bufs=1))
+
+        wo_raw = const.tile([P, GW], BF16, name="wo_raw")
+        nc.sync.dma_start(
+            out=wo_raw[:].rearrange("p (r k) -> p r k", k=D),
+            in_=Wo.rearrange("(r p) k -> p r k", p=P),
+        )
+        att_sb = []
+        hid_sb = []
+        w2_raw = const.tile([P, GW], BF16, name="w2_raw")
+        for g in range(GROUPS):
+            a_t = loads.tile([P, GW], BF16, name="att_sb", tag="att")
+            nc.sync.dma_start(out=a_t[:], in_=att_v[:, g * GW : (g + 1) * GW])
+            att_sb.append(a_t)
+            if g == 1:
+                nc.sync.dma_start(
+                    out=w2_raw[:].rearrange("p (r k) -> p r k", k=D),
+                    in_=W_ff1.rearrange("(r p) k -> p r k", p=P),
+                )
+            h_t = loads.tile([P, GW], BF16, name="hid_sb", tag="hid")
+            nc.sync.dma_start(out=h_t[:], in_=hid_v[:, g * GW : (g + 1) * GW])
+            hid_sb.append(h_t)
+
+        rows = const.tile([P, 2 * D], BF16, name="rows")
+        nc.vector.memset(rows[:], 0.0)
+        nc.scalar.dma_start(out=rows[0:1, 0:D], in_=bo.unsqueeze(0))
+        nc.scalar.dma_start(out=rows[0:1, D : 2 * D], in_=b_ff1.unsqueeze(0))
+        lnrows = const.tile([P, P], BF16, name="lnrows")
+        nc.vector.memset(lnrows[:], 0.0)
+        nc.scalar.dma_start(out=lnrows[0:4, :], in_=ln2_g.rearrange("(j c) -> j c", c=P))
+        nc.scalar.dma_start(out=lnrows[4:8, :], in_=ln2_b.rearrange("(j c) -> j c", c=P))
+        zero1 = const.tile([P, 1], F32, name="zero1")
+        nc.vector.memset(zero1[:], 0.0)
+        warm = const.tile([P, 1], F32, name="warm")
+        nc.scalar.activation(out=warm[:], in_=zero1[:], func=ACT.Gelu)
+
+        ident32 = const.tile([P, P], F32, name="ident32")
+        make_identity(nc, ident32[:])
+        ident16 = const.tile([P, P], BF16, name="ident16")
+        make_identity(nc, ident16[:])
+        ones16 = const.tile([P, P], BF16, name="ones16")
+        nc.vector.memset(ones16[:], 1.0)
+        neghalf = const.tile([P, GT], F32, name="neghalf")
+        nc.vector.memset(neghalf[:], -0.5)
+
+        bo_bc = const.tile([P, D], BF16, name="bo_bc")
+        bff_bc = const.tile([P, D], F32, name="bff_bc")
+        gb8 = const.tile([P, 8], F32, name="gb8")
+        bo_ps = mm.tile([P, D], F32, name="bo_ps", tag="mm")
+        nc.tensor.matmul(out=bo_ps[:], lhsT=ones16[:], rhs=rows[:, 0:D], start=True, stop=True)
+        nc.vector.tensor_copy(out=bo_bc[:], in_=bo_ps[:])
+        bff_ps = mm.tile([P, D], F32, name="bff_ps", tag="mm")
+        nc.tensor.matmul(out=bff_ps[:], lhsT=ones16[:], rhs=rows[:, D : 2 * D], start=True, stop=True)
+        ln_ps = mm.tile([P, P], BF16, name="ln_ps", tag="mm")
+        nc.tensor.transpose(ln_ps[:], lnrows[:], ident16[:])
+        nc.vector.tensor_copy(out=bff_bc[:], in_=bff_ps[:])
+        nc.vector.tensor_copy(out=gb8[:], in_=ln_ps[:, 0:8])
+
+        st = {}
+        for g in range(GROUPS):
+            st[g] = {}
+
+        def words_to_psum(src, banks):
+            src32 = src[:].bitcast(F32)
+            out = []
+            for h in range(2):
+                ps = xt.tile([P, 2, 2 * P], F32, name="at_ps", tag="xtp%d" % banks[h])
+                for i2 in range(2):
+                    for u in range(2):
+                        c0 = 256 * (2 * h + i2) + P * u
+                        nc.tensor.transpose(
+                            ps[:, u, P * i2 : P * i2 + P], src32[:, c0 : c0 + P], ident32[:]
+                        )
+                out.append(ps)
+            return out
+
+        def words_out(banks_ps, engines):
+            grouped = work.tile([P, GW], BF16, name="agr", tag="agr", align_bytes=64)
+            g32 = grouped[:].bitcast(F32).rearrange("p (r u) -> p r u", u=2)
+            for h in range(2):
+                src_ap = banks_ps[h][:].rearrange("p u r -> p r u")
+                dst_ap = g32[:, 256 * h : 256 * h + 256, :]
+                if engines[h] == "s":
+                    nc.scalar.copy(out=dst_ap, in_=src_ap)
+                else:
+                    nc.vector.tensor_copy(out=dst_ap, in_=src_ap)
+            return grouped
+
+        def ta(g, banks):
+            st[g]["at_ps"] = words_to_psum(att_sb[g], banks)
+
+        def p1(g, engines):
+            st[g]["agr"] = words_out(st[g]["at_ps"], engines)
+
+        def q1(g):
+            acod = work.tile([P, D], U32, name="acod", tag="acod", bufs=3, align_bytes=64)
+            ascl = work.tile([P, D], U8, name="ascl", tag="ascl", bufs=3, align_bytes=64)
+            nc.vector.quantize_mx(out=acod[:].bitcast(FP8X4), scales=ascl[:], in_=st[g]["agr"][:])
+            st[g]["acod"] = acod
+            st[g]["ascl"] = ascl
+
+        def hbg(g, i):
+            if i == 0:
+                st[g]["hh"] = work.tile([P, GW], F32, name="hh", tag="hh", bufs=4)
+            sl = slice(D * i, D * i + D)
+            nc.gpsimd.tensor_tensor(
+                out=st[g]["hh"][:, sl], in0=hid_sb[g][:, sl], in1=bo_bc[:], op=ALU.add
+            )
+
+        def m1_c(g, i):
+            if i == 0:
+                st[g]["hsum"] = work.tile([P, GT], F32, name="hsum", tag="hsum", bufs=3)
+            hh = st[g]["hh"]
+            sl = slice(D * i, D * i + D)
+            cs = slice(P * i, P * i + P)
+            s1 = mm.tile([P, D], F32, name="s1", tag="mm")
+            nc.tensor.matmul_mx(
+                out=s1[:],
+                lhsT=st[g]["acod"][:, cs].bitcast(FP8X4),
+                lhsT_scale=st[g]["ascl"][:, cs],
+                rhs=wo_cod[:].bitcast(FP8X4),
+                rhs_scale=wo_scl[:],
+                start=True,
+                stop=True,
+            )
+            nc.vector.scalar_tensor_tensor(
+                out=hh[:, sl],
+                in0=s1[:],
+                scalar=1.0,
+                in1=hh[:, sl],
+                op0=ALU.mult,
+                op1=ALU.add,
+                accum_out=st[g]["hsum"][:, i : i + 1],
+            )
+
+        def nm_sq(g):
+            hh = st[g]["hh"]
+            negmean = work.tile([P, GT], F32, name="negmean", tag="negmean", bufs=3)
+            nc.scalar.mul(out=negmean[:], in_=st[g]["hsum"][:], mul=-1.0 / D)
+            ssq = work.tile([P, GT], F32, name="ssq", tag="ssq", bufs=3)
+            for i in range(GT):
+                sl = slice(D * i, D * i + D)
+                junk = work.tile([P, D], BF16, name="junk", tag="junk")
+                nc.scalar.activation(
+                    out=junk[:],
+                    in_=hh[:, sl],
+                    func=ACT.Square,
+                    bias=negmean[:, i : i + 1],
+                    scale=1.0,
+                    accum_out=ssq[:, i : i + 1],
+                )
+            st[g]["negmean"] = negmean
+            st[g]["ssq"] = ssq
+
+        def ve(g):
+            veps = work.tile([P, GT], F32, name="veps", tag="veps", bufs=3)
+            nc.vector.tensor_scalar(
+                out=veps[:],
+                in0=st[g]["ssq"][:],
+                scalar1=1.0 / D,
+                scalar2=LN_EPS,
+                op0=ALU.mult,
+                op1=ALU.add,
+            )
+            st[g]["veps"] = veps
+
+        def powg(g):
+            rstd = work.tile([P, GT], F32, name="rstd", tag="rstd", bufs=3)
+            nc.gpsimd.tensor_tensor(out=rstd[:], in0=st[g]["veps"][:], in1=neghalf[:], op=ALU.pow)
+            st[g]["rstd"] = rstd
+
+        def xh_tx(g):
+            hh = st[g]["hh"]
+            xh = work.tile([P, GW], F32, name="xh", tag="xh")
+            xtp = [xt.tile([P, D], F32, name="xtp%d" % j, tag="xtp%d" % j) for j in range(4)]
+            for i in range(GT):
+                sl = slice(D * i, D * i + D)
+                nc.vector.tensor_scalar(
+                    out=xh[:, sl],
+                    in0=hh[:, sl],
+                    scalar1=st[g]["negmean"][:, i : i + 1],
+                    scalar2=st[g]["rstd"][:, i : i + 1],
+                    op0=ALU.add,
+                    op1=ALU.mult,
+                )
+                for j in range(4):
+                    c0 = D * i + P * j
+                    nc.tensor.transpose(xtp[j][:, P * i : P * i + P], xh[:, c0 : c0 + P], ident32[:])
+            st[g]["xtp"] = xtp
+
+        def gbs(g):
+            n_t = work.tile([P, 4, D], BF16, name="n_t", tag="n_t")
+            for j in range(4):
+                nc.scalar.activation(
+                    out=n_t[:, j, :],
+                    in_=st[g]["xtp"][j][:],
+                    func=ACT.Identity,
+                    scale=gb8[:, j : j + 1],
+                    bias=gb8[:, 4 + j : 5 + j],
+                )
+            st[g]["n_t"] = n_t
+
+        def rg_q2(g):
+            ngr = work.tile([P, GW], BF16, name="ngr", tag="ngr", align_bytes=64)
+            nc.vector.tensor_copy(
+                out=ngr[:].rearrange("p (c i t) -> p c t i", i=4, t=4),
+                in_=st[g]["n_t"][:].rearrange("p t (c i) -> p c t i", i=4),
+            )
+            ncod = work.tile([P, D], U32, name="ncod", tag="ncod", align_bytes=64)
+            nscl = work.tile([P, D], U8, name="nscl", tag="nscl", align_bytes=64)
+            nc.vector.quantize_mx(out=ncod[:].bitcast(FP8X4), scales=nscl[:], in_=ngr[:])
+            st[g]["ncod"] = ncod
+            st[g]["nscl"] = nscl
+
+        def m2_hb(g, i):
+            if i == 0:
+                st[g]["aa"] = work.tile([P, GW], F32, name="aa", tag="aa", bufs=3)
+            sl = slice(D * i, D * i + D)
+            cs = slice(P * i, P * i + P)
+            s2 = mm.tile([P, D], F32, name="s2", tag="mm")
+            nc.tensor.matmul_mx(
+                out=s2[:],
+                lhsT=st[g]["ncod"][:, cs].bitcast(FP8X4),
+                lhsT_scale=st[g]["nscl"][:, cs],
+                rhs=w2_cod[:].bitcast(FP8X4),
+                rhs_scale=w2_scl[:],
+                start=True,
+                stop=True,
+            )
+            nc.vector.tensor_tensor(out=st[g]["aa"][:, sl], in0=s2[:], in1=bff_bc[:], op=ALU.add)
+
+        def ge(g, i):
+            sl = slice(D * i, D * i + D)
+            nc.scalar.activation(out=st[g]["aa"][:, sl], in_=st[g]["aa"][:, sl], func=ACT.Gelu)
+
+        wo_cod = const.tile([P, D], U32, name="wo_cod", align_bytes=64)
+        wo_scl = const.tile([P, D], U8, name="wo_scl", align_bytes=64)
+        w2_cod = const.tile([P, D], U32, name="w2_cod", align_bytes=64)
+        w2_scl = const.tile([P, D], U8, name="w2_scl", align_bytes=64)
+
+        wo_ps = words_to_psum(wo_raw, (0, 1))
+        ta(0, (2, 3))
+        wo_gr = words_out(wo_ps, "sv")
+        p1(0, "sv")
+        nc.vector.quantize_mx(out=wo_cod[:].bitcast(FP8X4), scales=wo_scl[:], in_=wo_gr[:])
+        q1(0)
+        for i in range(GT):
+            hbg(0, i)
+        w2_ps = []
+
+        def w2_start():
+            for h in range(2):
+                ps = xt.tile([P, 4, 2 * P], BF16, name="w2_ps", tag="xtp%d" % (2 + h))
+                for r2 in range(2):
+                    for j in range(4):
+                        c0 = D * (2 * h + r2) + P * j
+                        nc.tensor.transpose(
+                            ps[:, j, P * r2 : P * r2 + P], w2_raw[:, c0 : c0 + P], ident16[:]
+                        )
+                w2_ps.append(ps)
+
+        def w2_finish():
+            w2_gr = const.tile([P, GW], BF16, name="w2_gr", align_bytes=64)
+            w2_g3 = w2_gr[:].rearrange("p (f j) -> p f j", j=4)
+            for h in range(2):
+                nc.vector.tensor_copy(
+                    out=w2_g3[:, 256 * h : 256 * h + 256, :],
+                    in_=w2_ps[h][:].rearrange("p j f -> p f j"),
+                )
+            nc.vector.quantize_mx(out=w2_cod[:].bitcast(FP8X4), scales=w2_scl[:], in_=w2_gr[:])
+
+        for k in range(-1, GROUPS):
+            b = k + 1
+            c = k
+            has_b = b < GROUPS
+            has_c = c >= 0
+            if k + 2 < GROUPS:
+                for i in range(3):
+                    hbg(k + 2, i)
+            if has_b:
+                for i in range(GT):
+                    m1_c(b, i)
+            if k == -1:
+                ta(1, (0, 1))
+                p1(1, "ss")
+                w2_start()
+            if has_c:
+                gbs(c)
+            if has_b:
+                nc.sync.dma_start(out=o0_v[:, b * GW : (b + 1) * GW], in_=st[b]["hh"][:])
+                nm_sq(b)
+            if has_c:
+                rg_q2(c)
+            if k + 3 < GROUPS:
+                ta(k + 3, (0, 1))
+            if k + 2 < GROUPS:
+                q1(k + 2)
+            if k == -1:
+                w2_finish()
+            if has_c:
+                m2_hb(c, 0)
+            if has_b:
+                ve(b)
+                powg(b)
+            if k + 2 < GROUPS:
+                hbg(k + 2, 3)
+            if has_c:
+                for i in range(1, GT):
+                    m2_hb(c, i)
+            if k + 3 < GROUPS:
+                p1(k + 3, "ss")
+            if has_c:
+                for i in range(GT):
+                    ge(c, i)
+                    if c == GROUPS - 1:
+                        nc.sync.dma_start(
+                            out=o1_v[:, c * GW + D * i : c * GW + D * i + D],
+                            in_=st[c]["aa"][:, D * i : D * i + D],
+                        )
+                if c < GROUPS - 1:
+                    nc.sync.dma_start(out=o1_v[:, c * GW : (c + 1) * GW], in_=st[c]["aa"][:])
+            if has_b:
+                xh_tx(b)

@@ -37,7 +37,7 @@ def tile_supervisedrefiner_pb_t_kernel(
         const = ctx.enter_context(tc.tile_pool(name="const", bufs=1))
         loads = ctx.enter_context(tc.tile_pool(name="loads", bufs=GROUPS))
         work = ctx.enter_context(tc.tile_pool(name="work", bufs=2))
-        mm = ctx.enter_context(tc.psum_pool(name="mm", bufs=4))
+        mm = ctx.enter_context(tc.psum_pool(name="mm", bufs=1))
         xt = ctx.enter_context(tc.psum_pool(name="xt", bufs=1))
 
         wo_raw = const.tile([P, GW], BF16, name="wo_raw")
@@ -86,12 +86,12 @@ def tile_supervisedrefiner_pb_t_kernel(
         bo_bc = const.tile([P, D], BF16, name="bo_bc")
         bff_bc = const.tile([P, D], F32, name="bff_bc")
         gb8 = const.tile([P, 8], F32, name="gb8")
-        bo_ps = mm.tile([P, D], F32, name="bo_ps", tag="mm")
+        bo_ps = mm.tile([P, D], F32, name="bo_ps", tag="mm0")
         nc.tensor.matmul(out=bo_ps[:], lhsT=ones16[:], rhs=rows[:, 0:D], start=True, stop=True)
         nc.vector.tensor_copy(out=bo_bc[:], in_=bo_ps[:])
-        bff_ps = mm.tile([P, D], F32, name="bff_ps", tag="mm")
+        bff_ps = mm.tile([P, D], F32, name="bff_ps", tag="mm1")
         nc.tensor.matmul(out=bff_ps[:], lhsT=ones16[:], rhs=rows[:, D : 2 * D], start=True, stop=True)
-        ln_ps = mm.tile([P, P], BF16, name="ln_ps", tag="mm")
+        ln_ps = mm.tile([P, P], BF16, name="ln_ps", tag="mm2")
         nc.tensor.transpose(ln_ps[:], lnrows[:], ident16[:])
         nc.vector.tensor_copy(out=bff_bc[:], in_=bff_ps[:])
         nc.vector.tensor_copy(out=gb8[:], in_=ln_ps[:, 0:8])
@@ -139,47 +139,55 @@ def tile_supervisedrefiner_pb_t_kernel(
             st[g]["acod"] = acod
             st[g]["ascl"] = ascl
 
-        def hbg(g, i):
-            if i == 0:
-                st[g]["hh"] = work.tile([P, GW], F32, name="hh", tag="hh", bufs=4)
-            sl = slice(D * i, D * i + D)
-            nc.gpsimd.tensor_tensor(
-                out=st[g]["hh"][:, sl], in0=hid_sb[g][:, sl], in1=bo_bc[:], op=ALU.add
-            )
+        def hbg(g):
+            hh = work.tile([P, GW], F32, name="hh", tag="hh", bufs=3)
+            for i in range(GT):
+                sl = slice(D * i, D * i + D)
+                nc.gpsimd.tensor_tensor(out=hh[:, sl], in0=hid_sb[g][:, sl], in1=bo_bc[:], op=ALU.add)
+            st[g]["hh"] = hh
 
-        def m1_c(g, i):
-            if i == 0:
-                st[g]["hsum"] = work.tile([P, GT], F32, name="hsum", tag="hsum", bufs=3)
+        def m1(g):
+            st[g]["s1"] = []
+            for i in range(GT):
+                cs = slice(P * i, P * i + P)
+                s1 = mm.tile([P, D], F32, name="s1", tag="mm%d" % i)
+                nc.tensor.matmul_mx(
+                    out=s1[:],
+                    lhsT=st[g]["acod"][:, cs].bitcast(FP8X4),
+                    lhsT_scale=st[g]["ascl"][:, cs],
+                    rhs=wo_cod[:].bitcast(FP8X4),
+                    rhs_scale=wo_scl[:],
+                    start=True,
+                    stop=True,
+                )
+                st[g]["s1"].append(s1)
+
+        def c4(g):
             hh = st[g]["hh"]
-            sl = slice(D * i, D * i + D)
-            cs = slice(P * i, P * i + P)
-            s1 = mm.tile([P, D], F32, name="s1", tag="mm")
-            nc.tensor.matmul_mx(
-                out=s1[:],
-                lhsT=st[g]["acod"][:, cs].bitcast(FP8X4),
-                lhsT_scale=st[g]["ascl"][:, cs],
-                rhs=wo_cod[:].bitcast(FP8X4),
-                rhs_scale=wo_scl[:],
-                start=True,
-                stop=True,
-            )
-            nc.vector.scalar_tensor_tensor(
-                out=hh[:, sl],
-                in0=s1[:],
-                scalar=1.0,
-                in1=hh[:, sl],
-                op0=ALU.mult,
-                op1=ALU.add,
-                accum_out=st[g]["hsum"][:, i : i + 1],
-            )
+            hsum = work.tile([P, GT], F32, name="hsum", tag="hsum", bufs=3)
+            for i in range(GT):
+                sl = slice(D * i, D * i + D)
+                nc.vector.scalar_tensor_tensor(
+                    out=hh[:, sl],
+                    in0=st[g]["s1"][i][:],
+                    scalar=1.0,
+                    in1=hh[:, sl],
+                    op0=ALU.mult,
+                    op1=ALU.add,
+                    accum_out=hsum[:, i : i + 1],
+                )
+            st[g]["hsum"] = hsum
+            nc.sync.dma_start(out=o0_v[:, g * GW : (g + 1) * GW], in_=hh[:])
 
-        def nm_sq(g):
+        def sq4(g):
             hh = st[g]["hh"]
             negmean = work.tile([P, GT], F32, name="negmean", tag="negmean", bufs=3)
-            nc.scalar.mul(out=negmean[:], in_=st[g]["hsum"][:], mul=-1.0 / D)
             ssq = work.tile([P, GT], F32, name="ssq", tag="ssq", bufs=3)
             for i in range(GT):
                 sl = slice(D * i, D * i + D)
+                nc.scalar.mul(
+                    out=negmean[:, i : i + 1], in_=st[g]["hsum"][:, i : i + 1], mul=-1.0 / D
+                )
                 junk = work.tile([P, D], BF16, name="junk", tag="junk")
                 nc.scalar.activation(
                     out=junk[:],
@@ -192,9 +200,9 @@ def tile_supervisedrefiner_pb_t_kernel(
             st[g]["negmean"] = negmean
             st[g]["ssq"] = ssq
 
-        def ve(g):
+        def powg(g):
             veps = work.tile([P, GT], F32, name="veps", tag="veps", bufs=3)
-            nc.vector.tensor_scalar(
+            nc.gpsimd.tensor_scalar(
                 out=veps[:],
                 in0=st[g]["ssq"][:],
                 scalar1=1.0 / D,
@@ -202,11 +210,8 @@ def tile_supervisedrefiner_pb_t_kernel(
                 op0=ALU.mult,
                 op1=ALU.add,
             )
-            st[g]["veps"] = veps
-
-        def powg(g):
             rstd = work.tile([P, GT], F32, name="rstd", tag="rstd", bufs=3)
-            nc.gpsimd.tensor_tensor(out=rstd[:], in0=st[g]["veps"][:], in1=neghalf[:], op=ALU.pow)
+            nc.gpsimd.tensor_tensor(out=rstd[:], in0=veps[:], in1=neghalf[:], op=ALU.pow)
             st[g]["rstd"] = rstd
 
         def xh_tx(g):
@@ -252,31 +257,44 @@ def tile_supervisedrefiner_pb_t_kernel(
             st[g]["ncod"] = ncod
             st[g]["nscl"] = nscl
 
-        def m2_hb(g, i):
-            if i == 0:
-                st[g]["aa"] = work.tile([P, GW], F32, name="aa", tag="aa", bufs=3)
-            sl = slice(D * i, D * i + D)
-            cs = slice(P * i, P * i + P)
-            s2 = mm.tile([P, D], F32, name="s2", tag="mm")
-            nc.tensor.matmul_mx(
-                out=s2[:],
-                lhsT=st[g]["ncod"][:, cs].bitcast(FP8X4),
-                lhsT_scale=st[g]["nscl"][:, cs],
-                rhs=w2_cod[:].bitcast(FP8X4),
-                rhs_scale=w2_scl[:],
-                start=True,
-                stop=True,
-            )
-            nc.vector.tensor_tensor(out=st[g]["aa"][:, sl], in0=s2[:], in1=bff_bc[:], op=ALU.add)
+        def m2(g):
+            st[g]["s2"] = []
+            for i in range(GT):
+                cs = slice(P * i, P * i + P)
+                s2 = mm.tile([P, D], F32, name="s2", tag="mm%d" % i)
+                nc.tensor.matmul_mx(
+                    out=s2[:],
+                    lhsT=st[g]["ncod"][:, cs].bitcast(FP8X4),
+                    lhsT_scale=st[g]["nscl"][:, cs],
+                    rhs=w2_cod[:].bitcast(FP8X4),
+                    rhs_scale=w2_scl[:],
+                    start=True,
+                    stop=True,
+                )
+                st[g]["s2"].append(s2)
 
-        def ge(g, i):
-            sl = slice(D * i, D * i + D)
-            nc.scalar.activation(out=st[g]["aa"][:, sl], in_=st[g]["aa"][:, sl], func=ACT.Gelu)
+        def hb4(g):
+            aa = work.tile([P, GW], F32, name="aa", tag="aa", bufs=3)
+            for i in range(GT):
+                sl = slice(D * i, D * i + D)
+                nc.vector.tensor_tensor(out=aa[:, sl], in0=st[g]["s2"][i][:], in1=bff_bc[:], op=ALU.add)
+            st[g]["aa"] = aa
+
+        def ge4(g):
+            aa = st[g]["aa"]
+            for i in range(GT):
+                sl = slice(D * i, D * i + D)
+                nc.scalar.activation(out=aa[:, sl], in_=aa[:, sl], func=ACT.Gelu)
+                if g == GROUPS - 1:
+                    nc.sync.dma_start(out=o1_v[:, g * GW + D * i : g * GW + D * i + D], in_=aa[:, sl])
+            if g < GROUPS - 1:
+                nc.sync.dma_start(out=o1_v[:, g * GW : (g + 1) * GW], in_=aa[:])
 
         wo_cod = const.tile([P, D], U32, name="wo_cod", align_bytes=64)
         wo_scl = const.tile([P, D], U8, name="wo_scl", align_bytes=64)
         w2_cod = const.tile([P, D], U32, name="w2_cod", align_bytes=64)
         w2_scl = const.tile([P, D], U8, name="w2_scl", align_bytes=64)
+        w2_gr = const.tile([P, GW], BF16, name="w2_gr", align_bytes=64)
 
         wo_ps = words_to_psum(wo_raw, (0, 1))
         ta(0, (2, 3))
@@ -284,80 +302,61 @@ def tile_supervisedrefiner_pb_t_kernel(
         p1(0, "sv")
         nc.vector.quantize_mx(out=wo_cod[:].bitcast(FP8X4), scales=wo_scl[:], in_=wo_gr[:])
         q1(0)
-        for i in range(GT):
-            hbg(0, i)
-        w2_ps = []
+        hbg(0)
+        hbg(1)
+        m1(0)
 
-        def w2_start():
-            for h in range(2):
-                ps = xt.tile([P, 4, 2 * P], BF16, name="w2_ps", tag="xtp%d" % (2 + h))
-                for r2 in range(2):
-                    for j in range(4):
-                        c0 = D * (2 * h + r2) + P * j
-                        nc.tensor.transpose(
-                            ps[:, j, P * r2 : P * r2 + P], w2_raw[:, c0 : c0 + P], ident16[:]
-                        )
-                w2_ps.append(ps)
+        def has(g):
+            return 0 <= g < GROUPS
 
-        def w2_finish():
-            w2_gr = const.tile([P, GW], BF16, name="w2_gr", align_bytes=64)
-            w2_g3 = w2_gr[:].rearrange("p (f j) -> p f j", j=4)
-            for h in range(2):
-                nc.vector.tensor_copy(
-                    out=w2_g3[:, 256 * h : 256 * h + 256, :],
-                    in_=w2_ps[h][:].rearrange("p j f -> p f j"),
-                )
-            nc.vector.quantize_mx(out=w2_cod[:].bitcast(FP8X4), scales=w2_scl[:], in_=w2_gr[:])
-
-        for k in range(-1, GROUPS):
-            b = k + 1
-            c = k
-            has_b = b < GROUPS
-            has_c = c >= 0
-            if k + 2 < GROUPS:
-                for i in range(3):
-                    hbg(k + 2, i)
-            if has_b:
-                for i in range(GT):
-                    m1_c(b, i)
-            if k == -1:
-                ta(1, (0, 1))
-                p1(1, "ss")
-                w2_start()
-            if has_c:
-                gbs(c)
-            if has_b:
-                nc.sync.dma_start(out=o0_v[:, b * GW : (b + 1) * GW], in_=st[b]["hh"][:])
-                nm_sq(b)
-            if has_c:
-                rg_q2(c)
-            if k + 3 < GROUPS:
-                ta(k + 3, (0, 1))
-            if k + 2 < GROUPS:
-                q1(k + 2)
-            if k == -1:
-                w2_finish()
-            if has_c:
-                m2_hb(c, 0)
-            if has_b:
-                ve(b)
-                powg(b)
-            if k + 2 < GROUPS:
-                hbg(k + 2, 3)
-            if has_c:
-                for i in range(1, GT):
-                    m2_hb(c, i)
-            if k + 3 < GROUPS:
-                p1(k + 3, "ss")
-            if has_c:
-                for i in range(GT):
-                    ge(c, i)
-                    if c == GROUPS - 1:
-                        nc.sync.dma_start(
-                            out=o1_v[:, c * GW + D * i : c * GW + D * i + D],
-                            in_=st[c]["aa"][:, D * i : D * i + D],
-                        )
-                if c < GROUPS - 1:
-                    nc.sync.dma_start(out=o1_v[:, c * GW : (c + 1) * GW], in_=st[c]["aa"][:])
-            if has_b:
-                xh_tx(b)
+        for p in range(GROUPS + 3):
+            x, w, y, z, e = p, p + 1, p - 1, p - 2, p - 3
+            if has(x):
+                c4(x)
+            if has(z):
+                gbs(z)
+            if has(w):
+                ta(w, (0, 1))
+                p1(w, "ss")
+            if p == 0:
+                w2_ps = []
+                for h in range(2):
+                    ps = xt.tile([P, 4, 2 * P], BF16, name="w2_ps", tag="xtp%d" % (2 + h))
+                    for r2 in range(2):
+                        for j in range(4):
+                            c0 = D * (2 * h + r2) + P * j
+                            nc.tensor.transpose(
+                                ps[:, j, P * r2 : P * r2 + P], w2_raw[:, c0 : c0 + P], ident16[:]
+                            )
+                    w2_ps.append(ps)
+            if has(z):
+                rg_q2(z)
+            if has(w):
+                q1(w)
+            if p == 1:
+                nc.vector.quantize_mx(out=w2_cod[:].bitcast(FP8X4), scales=w2_scl[:], in_=w2_gr[:])
+            if has(z):
+                m2(z)
+            if not has(z) and has(x + 1):
+                m1(x + 1)
+            if has(y):
+                xh_tx(y)
+            if has(x):
+                sq4(x)
+            if p == 0:
+                w2_g3 = w2_gr[:].rearrange("p (f j) -> p f j", j=4)
+                for h in range(2):
+                    nc.scalar.copy(
+                        out=w2_g3[:, 256 * h : 256 * h + 256, :],
+                        in_=w2_ps[h][:].rearrange("p j f -> p f j"),
+                    )
+            if has(e):
+                ge4(e)
+            if has(z):
+                hb4(z)
+            if has(z) and has(x + 1):
+                m1(x + 1)
+            if has(x):
+                powg(x)
+            if has(p + 2):
+                hbg(p + 2)

@@ -22,6 +22,11 @@ LN_EPS = 1e-5
 
 FLOPS = 2 * 2 * TOKENS * D * D
 
+HB_ON_V = (2, 3)
+XH_ON_S = ()
+HH_BUFS = 4
+XH_BUFS = 3
+
 
 def tile_supervisedrefiner_pb_t_kernel(
     tc, attended, hidden, Wo, bo, ln2_g, ln2_b, W_ff1, b_ff1, out_0, out_1
@@ -33,7 +38,6 @@ def tile_supervisedrefiner_pb_t_kernel(
     o1_v = out_1.flatten_outer_dims().rearrange("(p t) d -> p (t d)", t=TILES)
 
     with ExitStack() as ctx:
-        ctx.enter_context(tc.manual_schedule())
         const = ctx.enter_context(tc.tile_pool(name="const", bufs=1))
         loads = ctx.enter_context(tc.tile_pool(name="loads", bufs=GROUPS))
         work = ctx.enter_context(tc.tile_pool(name="work", bufs=2))
@@ -140,10 +144,11 @@ def tile_supervisedrefiner_pb_t_kernel(
             st[g]["ascl"] = ascl
 
         def hbg(g):
-            hh = work.tile([P, GW], F32, name="hh", tag="hh", bufs=3)
+            hh = work.tile([P, GW], F32, name="hh", tag="hh", bufs=HH_BUFS)
             for i in range(GT):
                 sl = slice(D * i, D * i + D)
-                nc.gpsimd.tensor_tensor(out=hh[:, sl], in0=hid_sb[g][:, sl], in1=bo_bc[:], op=ALU.add)
+                eng = nc.vector if i in HB_ON_V else nc.gpsimd
+                eng.tensor_tensor(out=hh[:, sl], in0=hid_sb[g][:, sl], in1=bo_bc[:], op=ALU.add)
             st[g]["hh"] = hh
 
         def m1(g):
@@ -213,21 +218,34 @@ def tile_supervisedrefiner_pb_t_kernel(
             rstd = work.tile([P, GT], F32, name="rstd", tag="rstd", bufs=3)
             nc.gpsimd.tensor_tensor(out=rstd[:], in0=veps[:], in1=neghalf[:], op=ALU.pow)
             st[g]["rstd"] = rstd
+            if len(XH_ON_S) > 0:
+                nmr = work.tile([P, GT], F32, name="nmr", tag="nmr", bufs=3)
+                nc.gpsimd.tensor_tensor(out=nmr[:], in0=st[g]["negmean"][:], in1=rstd[:], op=ALU.mult)
+                st[g]["nmr"] = nmr
 
         def xh_tx(g):
             hh = st[g]["hh"]
-            xh = work.tile([P, GW], F32, name="xh", tag="xh")
+            xh = work.tile([P, GW], F32, name="xh", tag="xh", bufs=XH_BUFS)
             xtp = [xt.tile([P, D], F32, name="xtp%d" % j, tag="xtp%d" % j) for j in range(4)]
             for i in range(GT):
                 sl = slice(D * i, D * i + D)
-                nc.vector.tensor_scalar(
-                    out=xh[:, sl],
-                    in0=hh[:, sl],
-                    scalar1=st[g]["negmean"][:, i : i + 1],
-                    scalar2=st[g]["rstd"][:, i : i + 1],
-                    op0=ALU.add,
-                    op1=ALU.mult,
-                )
+                if i in XH_ON_S:
+                    nc.scalar.activation(
+                        out=xh[:, sl],
+                        in_=hh[:, sl],
+                        func=ACT.Identity,
+                        scale=st[g]["rstd"][:, i : i + 1],
+                        bias=st[g]["nmr"][:, i : i + 1],
+                    )
+                else:
+                    nc.vector.tensor_scalar(
+                        out=xh[:, sl],
+                        in0=hh[:, sl],
+                        scalar1=st[g]["negmean"][:, i : i + 1],
+                        scalar2=st[g]["rstd"][:, i : i + 1],
+                        op0=ALU.add,
+                        op1=ALU.mult,
+                    )
                 for j in range(4):
                     c0 = D * i + P * j
                     nc.tensor.transpose(xtp[j][:, P * i : P * i + P], xh[:, c0 : c0 + P], ident32[:])

@@ -22,10 +22,87 @@ LN_EPS = 1e-5
 
 FLOPS = 2 * 2 * TOKENS * D * D
 
-HB_ON_V = (2, 3)
-XH_ON_S = ()
-HH_BUFS = 4
-XH_BUFS = 3
+HB_V = frozenset((("HBG", 0, 0), ("HBG", 0, 1), ("HBG", 0, 2), ("HBG", 0, 3), ("HBG", 1, 0), ("HBG", 1, 1), ("HBG", 1, 2), ("HBG", 1, 3), ("HBG", 2, 0), ("HBG", 2, 1), ("HBG", 2, 2), ("HBG", 2, 3),))
+XH_G = frozenset((("XH", 0, 2), ("XH", 0, 3), ("XH", 1, 2), ("XH", 1, 3), ("XH", 2, 2), ("XH", 2, 3), ("XH", 3, 2), ("XH", 3, 3), ("XH", 4, 2), ("XH", 4, 3), ("XH", 5, 2), ("XH", 5, 3), ("XH", 6, 2), ("XH", 6, 3), ("XH", 7, 2), ("XH", 7, 3),))
+GB_V = frozenset(())
+P1_V = frozenset(())
+P1W_V = frozenset((("P1W", 1, -1),))
+
+ORDER = (
+    ("MEMS", -1, -1), ("IDENT", -1, -1), ("WARM", -1, -1), ("LDS", -1, -1), ("LDH", 0, -1), ("BOMM", -1, -1),
+    ("LDWO", -1, -1), ("BOBC", -1, -1), ("LDA", 0, -1), ("HBG", 0, 0), ("TAW", 0, -1), ("HBG", 0, 1),
+    ("LDH", 1, -1), ("HBG", 0, 2), ("TAW", 1, -1), ("P1W", 0, -1), ("HBG", 0, 3), ("TA", 0, 0),
+    ("LDH", 2, -1), ("P1W", 1, -1), ("TA", 0, 1), ("QWo", -1, -1), ("P1", 0, 0), ("LDA", 1, -1),
+    ("HBG", 1, 0), ("P1", 0, 1), ("HBG", 1, 1), ("LDW2", -1, -1), ("HBG", 1, 2), ("TA", 1, 0),
+    ("Q1", 0, -1), ("LDA", 2, -1), ("TA", 1, 1), ("HBG", 1, 3), ("P1", 1, 0), ("TW2", 0, -1),
+    ("LDH", 3, -1), ("HBG", 2, 0), ("P1", 1, 1), ("M1", 0, 0), ("HBG", 2, 1), ("M1", 0, 1),
+    ("W2C", 0, -1), ("M1", 0, 2), ("LDA", 3, -1), ("C", 0, 0), ("M1", 0, 3), ("TA", 2, 0),
+    ("HBG", 3, 0), ("C", 0, 1), ("LDH", 4, -1), ("TA", 2, 1), ("SQ", 0, 0), ("C", 0, 2),
+    ("TW2", 1, -1), ("SQ", 0, 1), ("C", 0, 3), ("HBG", 3, 1), ("LDA", 4, -1), ("SQ", 0, 2),
+    ("Q1", 1, -1), ("LDH", 5, -1), ("SQ", 0, 3), ("HBG", 2, 2), ("HBG", 3, 2), ("M1", 1, 0),
+    ("HBG", 2, 3), ("P1", 2, 0), ("M1", 1, 1), ("LDA", 5, -1), ("M1", 1, 2), ("P1", 2, 1),
+    ("C", 1, 0), ("M1", 1, 3), ("W2C", 1, -1), ("C", 1, 1), ("POW", 0, -1), ("LDH", 6, -1),
+    ("C", 1, 2), ("XH", 0, 2), ("SQ", 1, 0), ("C", 1, 3), ("LDA", 6, -1), ("SQ", 1, 1),
+    ("XH", 0, 3), ("XH", 0, 0), ("XH", 0, 1), ("SQ", 1, 2), ("LDH", 7, -1), ("Q1", 2, -1),
+    ("HBG", 3, 3), ("SQ", 1, 3), ("TX", 0, 0), ("QW2", -1, -1), ("LDA", 7, -1), ("TX", 0, 1),
+    ("POW", 1, -1), ("GB", 0, 0), ("M1", 2, 0), ("STH", 0, -1), ("M1", 2, 1), ("GB", 0, 1),
+    ("XH", 1, 2), ("M1", 2, 2), ("C", 2, 0), ("TA", 3, 0), ("XH", 1, 3), ("XH", 1, 0),
+    ("TA", 3, 1), ("XH", 1, 1), ("SQ", 2, 0), ("C", 2, 1), ("STH", 1, -1), ("M1", 2, 3),
+    ("P1", 3, 0), ("TX", 0, 2), ("C", 2, 2), ("HBG", 4, 0), ("P1", 3, 1), ("C", 2, 3),
+    ("TX", 0, 3), ("SQ", 2, 1), ("TX", 1, 0), ("Q1", 3, -1), ("HBG", 4, 1), ("SQ", 2, 2),
+    ("STH", 2, -1), ("TX", 1, 1), ("SQ", 2, 3), ("M1", 3, 0), ("GB", 1, 0), ("M1", 3, 1),
+    ("HBG", 4, 2), ("M1", 3, 2), ("C", 3, 0), ("GB", 1, 1), ("M1", 3, 3), ("TA", 4, 0),
+    ("C", 3, 1), ("GB", 0, 2), ("POW", 2, -1), ("GB", 0, 3), ("C", 3, 2), ("TA", 4, 1),
+    ("P1", 4, 0), ("C", 3, 3), ("TX", 1, 2), ("XH", 2, 2), ("P1", 4, 1), ("XH", 2, 0),
+    ("TX", 1, 3), ("XH", 2, 1), ("XH", 2, 3), ("STH", 3, -1), ("SQ", 3, 0), ("RG", 0, -1),
+    ("HBG", 4, 3), ("SQ", 3, 1), ("TX", 2, 0), ("Q1", 4, -1), ("SQ", 3, 2), ("TX", 2, 1),
+    ("Q2", 0, -1), ("SQ", 3, 3), ("HBG", 5, 0), ("M1", 4, 0), ("GB", 2, 0), ("M1", 4, 1),
+    ("M1", 4, 2), ("GB", 2, 1), ("C", 4, 0), ("M1", 4, 3), ("TA", 5, 0), ("POW", 3, -1),
+    ("GB", 1, 2), ("C", 4, 1), ("GB", 1, 3), ("TA", 5, 1), ("C", 4, 2), ("XH", 3, 2),
+    ("P1", 5, 0), ("M2", 0, 0), ("XH", 3, 0), ("M2", 0, 1), ("XH", 3, 3), ("XH", 3, 1),
+    ("P1", 5, 1), ("M2", 0, 2), ("C", 4, 3), ("TX", 2, 2), ("SQ", 4, 0), ("HBG", 5, 1),
+    ("HB", 0, 0), ("TX", 3, 0), ("SQ", 4, 1), ("STH", 4, -1), ("Q1", 5, -1), ("TX", 3, 1),
+    ("SQ", 4, 2), ("HB", 0, 1), ("HBG", 5, 2), ("HB", 0, 2), ("M2", 0, 3), ("GB", 3, 0),
+    ("TX", 2, 3), ("RG", 1, -1), ("GB", 3, 1), ("TA", 6, 0), ("SQ", 4, 3), ("HBG", 5, 3),
+    ("HB", 0, 3), ("TA", 6, 1), ("GB", 2, 2), ("Q2", 1, -1), ("P1", 6, 0), ("M1", 5, 0),
+    ("POW", 4, -1), ("M1", 5, 1), ("P1", 6, 1), ("M1", 5, 2), ("C", 5, 0), ("M1", 5, 3),
+    ("GB", 2, 3), ("TX", 3, 2), ("XH", 4, 2), ("C", 5, 1), ("GE", 0, 0), ("M2", 1, 0),
+    ("XH", 4, 3), ("C", 5, 2), ("TX", 3, 3), ("SQ", 5, 0), ("C", 5, 3), ("HBG", 6, 0),
+    ("GB", 3, 2), ("M2", 1, 1), ("M2", 1, 2), ("XH", 4, 0), ("GB", 3, 3), ("XH", 4, 1),
+    ("M2", 1, 3), ("STH", 5, -1), ("Q1", 6, -1), ("SQ", 5, 1), ("HBG", 6, 1), ("TX", 4, 0),
+    ("HB", 1, 0), ("SQ", 5, 2), ("HB", 1, 1), ("TX", 4, 1), ("SQ", 5, 3), ("HB", 1, 2),
+    ("M1", 6, 0), ("HBG", 6, 2), ("GB", 4, 0), ("M1", 6, 1), ("HB", 1, 3), ("TX", 4, 2),
+    ("GB", 4, 1), ("RG", 2, -1), ("M1", 6, 2), ("GE", 0, 1), ("M1", 6, 3), ("HBG", 6, 3),
+    ("TA", 7, 0), ("GE", 0, 2), ("C", 6, 0), ("GE", 0, 3), ("TA", 7, 1), ("C", 6, 1),
+    ("P1", 7, 0), ("POW", 5, -1), ("TX", 4, 3), ("C", 6, 2), ("STA", 0, -1), ("P1", 7, 1),
+    ("C", 6, 3), ("HBG", 7, 0), ("GB", 4, 2), ("Q2", 2, -1), ("GB", 4, 3), ("Q1", 7, -1),
+    ("SQ", 6, 0), ("M2", 2, 0), ("HBG", 7, 1), ("STH", 6, -1), ("XH", 5, 0), ("M2", 2, 1),
+    ("XH", 5, 1), ("SQ", 6, 1), ("M2", 2, 2), ("HB", 2, 0), ("M2", 2, 3), ("SQ", 6, 2),
+    ("HB", 2, 1), ("HBG", 7, 2), ("SQ", 6, 3), ("M1", 7, 0), ("HB", 2, 2), ("M1", 7, 1),
+    ("GE", 1, 0), ("HB", 2, 3), ("M1", 7, 2), ("GE", 1, 1), ("RG", 3, -1), ("HBG", 7, 3),
+    ("M1", 7, 3), ("GE", 1, 2), ("GE", 1, 3), ("C", 7, 0), ("XH", 5, 2), ("GE", 2, 0),
+    ("C", 7, 1), ("STA", 1, -1), ("SQ", 7, 0), ("C", 7, 2), ("XH", 5, 3), ("SQ", 7, 1),
+    ("C", 7, 3), ("POW", 6, -1), ("SQ", 7, 2), ("Q2", 3, -1), ("TX", 5, 0), ("XH", 6, 2),
+    ("SQ", 7, 3), ("RG", 4, -1), ("STH", 7, -1), ("TX", 5, 1), ("XH", 6, 3), ("GB", 5, 0),
+    ("TX", 5, 2), ("XH", 6, 0), ("XH", 6, 1), ("GB", 5, 1), ("POW", 7, -1), ("TX", 5, 3),
+    ("Q2", 4, -1), ("GB", 5, 2), ("M2", 3, 0), ("M2", 3, 1), ("GB", 5, 3), ("XH", 7, 2),
+    ("XH", 7, 0), ("M2", 3, 2), ("HB", 3, 0), ("M2", 3, 3), ("GE", 2, 1), ("TX", 6, 0),
+    ("XH", 7, 3), ("HB", 3, 1), ("GE", 2, 2), ("TX", 6, 1), ("HB", 3, 2), ("GE", 2, 3),
+    ("HB", 3, 3), ("TX", 6, 2), ("GB", 6, 0), ("RG", 5, -1), ("TX", 6, 3), ("STA", 2, -1),
+    ("GB", 6, 1), ("M2", 4, 0), ("GB", 6, 2), ("XH", 7, 1), ("M2", 4, 1), ("Q2", 5, -1),
+    ("M2", 4, 2), ("GB", 6, 3), ("M2", 4, 3), ("HB", 4, 0), ("TX", 7, 0), ("GE", 3, 0),
+    ("HB", 4, 1), ("GE", 3, 1), ("TX", 7, 1), ("HB", 4, 2), ("GE", 3, 2), ("TX", 7, 2),
+    ("HB", 4, 3), ("GE", 3, 3), ("TX", 7, 3), ("RG", 6, -1), ("GB", 7, 0), ("STA", 3, -1),
+    ("M2", 5, 0), ("GB", 7, 1), ("M2", 5, 1), ("Q2", 6, -1), ("M2", 5, 2), ("GB", 7, 2),
+    ("M2", 5, 3), ("HB", 5, 0), ("GB", 7, 3), ("HB", 5, 1), ("GE", 4, 0), ("M2", 6, 0),
+    ("HB", 5, 2), ("GE", 4, 1), ("M2", 6, 1), ("HB", 5, 3), ("GE", 4, 2), ("M2", 6, 2),
+    ("RG", 7, -1), ("GE", 4, 3), ("M2", 6, 3), ("GE", 5, 0), ("Q2", 7, -1), ("STA", 4, -1),
+    ("GE", 5, 1), ("HB", 6, 0), ("GE", 5, 2), ("HB", 6, 1), ("GE", 5, 3), ("M2", 7, 0),
+    ("HB", 6, 2), ("GE", 6, 0), ("M2", 7, 1), ("HB", 6, 3), ("STA", 5, -1), ("GE", 6, 1),
+    ("M2", 7, 2), ("HB", 7, 0), ("GE", 6, 2), ("M2", 7, 3), ("HB", 7, 1), ("GE", 6, 3),
+    ("HB", 7, 2), ("GE", 7, 0), ("HB", 7, 3), ("STA", 6, -1), ("GE", 7, 1), ("GE", 7, 2),
+    ("GE", 7, 3), ("STL", 7, 0), ("STL", 7, 1), ("STL", 7, 2), ("STL", 7, 3),
+)
 
 
 def tile_supervisedrefiner_pb_t_kernel(
@@ -38,343 +115,271 @@ def tile_supervisedrefiner_pb_t_kernel(
     o1_v = out_1.flatten_outer_dims().rearrange("(p t) d -> p (t d)", t=TILES)
 
     with ExitStack() as ctx:
+        ctx.enter_context(tc.manual_schedule())
         const = ctx.enter_context(tc.tile_pool(name="const", bufs=1))
         loads = ctx.enter_context(tc.tile_pool(name="loads", bufs=GROUPS))
         work = ctx.enter_context(tc.tile_pool(name="work", bufs=2))
         mm = ctx.enter_context(tc.psum_pool(name="mm", bufs=1))
         xt = ctx.enter_context(tc.psum_pool(name="xt", bufs=1))
 
-        wo_raw = const.tile([P, GW], BF16, name="wo_raw")
-        nc.sync.dma_start(
-            out=wo_raw[:].rearrange("p (r k) -> p r k", k=D),
-            in_=Wo.rearrange("(r p) k -> p r k", p=P),
-        )
-        att_sb = []
-        hid_sb = []
-        w2_raw = const.tile([P, GW], BF16, name="w2_raw")
-        for g in range(GROUPS):
-            a_t = loads.tile([P, GW], BF16, name="att_sb", tag="att")
-            nc.sync.dma_start(out=a_t[:], in_=att_v[:, g * GW : (g + 1) * GW])
-            att_sb.append(a_t)
-            if g == 1:
-                nc.sync.dma_start(
-                    out=w2_raw[:].rearrange("p (r k) -> p r k", k=D),
-                    in_=W_ff1.rearrange("(r p) k -> p r k", p=P),
-                )
-            h_t = loads.tile([P, GW], BF16, name="hid_sb", tag="hid")
-            nc.sync.dma_start(out=h_t[:], in_=hid_v[:, g * GW : (g + 1) * GW])
-            hid_sb.append(h_t)
-
         rows = const.tile([P, 2 * D], BF16, name="rows")
-        nc.vector.memset(rows[:], 0.0)
-        nc.scalar.dma_start(out=rows[0:1, 0:D], in_=bo.unsqueeze(0))
-        nc.scalar.dma_start(out=rows[0:1, D : 2 * D], in_=b_ff1.unsqueeze(0))
         lnrows = const.tile([P, P], BF16, name="lnrows")
-        nc.vector.memset(lnrows[:], 0.0)
-        nc.scalar.dma_start(out=lnrows[0:4, :], in_=ln2_g.rearrange("(j c) -> j c", c=P))
-        nc.scalar.dma_start(out=lnrows[4:8, :], in_=ln2_b.rearrange("(j c) -> j c", c=P))
+        wo_raw = const.tile([P, GW], BF16, name="wo_raw")
+        w2_raw = const.tile([P, GW], BF16, name="w2_raw")
+        att_sb = [loads.tile([P, GW], BF16, name="att_sb", tag="att") for g in range(GROUPS)]
+        hid_sb = [loads.tile([P, GW], BF16, name="hid_sb", tag="hid") for g in range(GROUPS)]
         zero1 = const.tile([P, 1], F32, name="zero1")
-        nc.vector.memset(zero1[:], 0.0)
         warm = const.tile([P, 1], F32, name="warm")
-        nc.scalar.activation(out=warm[:], in_=zero1[:], func=ACT.Gelu)
-
         ident32 = const.tile([P, P], F32, name="ident32")
-        make_identity(nc, ident32[:])
         ident16 = const.tile([P, P], BF16, name="ident16")
-        make_identity(nc, ident16[:])
         ones16 = const.tile([P, P], BF16, name="ones16")
-        nc.vector.memset(ones16[:], 1.0)
         neghalf = const.tile([P, GT], F32, name="neghalf")
-        nc.vector.memset(neghalf[:], -0.5)
-
         bo_bc = const.tile([P, D], BF16, name="bo_bc")
         bff_bc = const.tile([P, D], F32, name="bff_bc")
         gb8 = const.tile([P, 8], F32, name="gb8")
-        bo_ps = mm.tile([P, D], F32, name="bo_ps", tag="mm0")
-        nc.tensor.matmul(out=bo_ps[:], lhsT=ones16[:], rhs=rows[:, 0:D], start=True, stop=True)
-        nc.vector.tensor_copy(out=bo_bc[:], in_=bo_ps[:])
-        bff_ps = mm.tile([P, D], F32, name="bff_ps", tag="mm1")
-        nc.tensor.matmul(out=bff_ps[:], lhsT=ones16[:], rhs=rows[:, D : 2 * D], start=True, stop=True)
-        ln_ps = mm.tile([P, P], BF16, name="ln_ps", tag="mm2")
-        nc.tensor.transpose(ln_ps[:], lnrows[:], ident16[:])
-        nc.vector.tensor_copy(out=bff_bc[:], in_=bff_ps[:])
-        nc.vector.tensor_copy(out=gb8[:], in_=ln_ps[:, 0:8])
+        wo_cod = const.tile([P, D], U32, name="wo_cod", align_bytes=64)
+        wo_scl = const.tile([P, D], U8, name="wo_scl", align_bytes=64)
+        w2_cod = const.tile([P, D], U32, name="w2_cod", align_bytes=64)
+        w2_scl = const.tile([P, D], U8, name="w2_scl", align_bytes=64)
+        w2_gr = const.tile([P, GW], BF16, name="w2_gr", align_bytes=64)
+        wo_gr = const.tile([P, GW], BF16, name="wo_gr", align_bytes=64)
 
         st = {}
-        for g in range(GROUPS):
-            st[g] = {}
 
-        def words_to_psum(src, banks):
+        def slot(key, make):
+            if key not in st:
+                st[key] = make()
+            return st[key]
+
+        def load_w(dst, src):
+            nc.sync.dma_start(
+                out=dst[:].rearrange("p (r k) -> p r k", k=D), in_=src.rearrange("(r p) k -> p r k", p=P)
+            )
+
+        def words_to_psum(src, h, bank, key):
             src32 = src[:].bitcast(F32)
-            out = []
-            for h in range(2):
-                ps = xt.tile([P, 2, 2 * P], F32, name="at_ps", tag="xtp%d" % banks[h])
-                for i2 in range(2):
-                    for u in range(2):
-                        c0 = 256 * (2 * h + i2) + P * u
-                        nc.tensor.transpose(
-                            ps[:, u, P * i2 : P * i2 + P], src32[:, c0 : c0 + P], ident32[:]
-                        )
-                out.append(ps)
-            return out
+            ps = xt.tile([P, 2, 2 * P], F32, name="at_ps", tag="xtp%d" % bank)
+            for i2 in range(2):
+                for u in range(2):
+                    c0 = 256 * (2 * h + i2) + P * u
+                    nc.tensor.transpose(ps[:, u, P * i2 : P * i2 + P], src32[:, c0 : c0 + P], ident32[:])
+            st[key] = ps
 
-        def words_out(banks_ps, engines):
-            grouped = work.tile([P, GW], BF16, name="agr", tag="agr", align_bytes=64)
+        def words_out(grouped, h, key, on_v):
             g32 = grouped[:].bitcast(F32).rearrange("p (r u) -> p r u", u=2)
-            for h in range(2):
-                src_ap = banks_ps[h][:].rearrange("p u r -> p r u")
-                dst_ap = g32[:, 256 * h : 256 * h + 256, :]
-                if engines[h] == "s":
-                    nc.scalar.copy(out=dst_ap, in_=src_ap)
-                else:
-                    nc.vector.tensor_copy(out=dst_ap, in_=src_ap)
-            return grouped
+            src_ap = st[key][:].rearrange("p u r -> p r u")
+            dst_ap = g32[:, 256 * h : 256 * h + 256, :]
+            if on_v:
+                nc.vector.tensor_copy(out=dst_ap, in_=src_ap)
+            else:
+                nc.scalar.copy(out=dst_ap, in_=src_ap)
 
-        def ta(g, banks):
-            st[g]["at_ps"] = words_to_psum(att_sb[g], banks)
-
-        def p1(g, engines):
-            st[g]["agr"] = words_out(st[g]["at_ps"], engines)
-
-        def q1(g):
-            acod = work.tile([P, D], U32, name="acod", tag="acod", bufs=3, align_bytes=64)
-            ascl = work.tile([P, D], U8, name="ascl", tag="ascl", bufs=3, align_bytes=64)
-            nc.vector.quantize_mx(out=acod[:].bitcast(FP8X4), scales=ascl[:], in_=st[g]["agr"][:])
-            st[g]["acod"] = acod
-            st[g]["ascl"] = ascl
-
-        def hbg(g):
-            hh = work.tile([P, GW], F32, name="hh", tag="hh", bufs=HH_BUFS)
-            for i in range(GT):
-                sl = slice(D * i, D * i + D)
-                eng = nc.vector if i in HB_ON_V else nc.gpsimd
+        def emit(k, g, i):
+            name = (k, g, i)
+            sl = slice(D * i, D * i + D)
+            cs = slice(P * i, P * i + P)
+            if k == "LDS":
+                nc.sync.dma_start(out=rows[0:1, 0:D], in_=bo.unsqueeze(0))
+                nc.sync.dma_start(out=rows[0:1, D : 2 * D], in_=b_ff1.unsqueeze(0))
+                nc.sync.dma_start(out=lnrows[0:4, :], in_=ln2_g.rearrange("(j c) -> j c", c=P))
+                nc.sync.dma_start(out=lnrows[4:8, :], in_=ln2_b.rearrange("(j c) -> j c", c=P))
+            elif k == "LDWO":
+                load_w(wo_raw, Wo)
+            elif k == "LDW2":
+                load_w(w2_raw, W_ff1)
+            elif k == "LDA":
+                nc.sync.dma_start(out=att_sb[g][:], in_=att_v[:, g * GW : (g + 1) * GW])
+            elif k == "LDH":
+                nc.sync.dma_start(out=hid_sb[g][:], in_=hid_v[:, g * GW : (g + 1) * GW])
+            elif k == "IDENT":
+                make_identity(nc, ident32[:])
+                make_identity(nc, ident16[:])
+            elif k == "WARM":
+                nc.scalar.activation(out=warm[:], in_=zero1[:], func=ACT.Gelu)
+            elif k == "BOMM":
+                st["bo_ps"] = mm.tile([P, D], F32, name="bo_ps", tag="mm0")
+                nc.tensor.matmul(out=st["bo_ps"][:], lhsT=ones16[:], rhs=rows[:, 0:D], start=True, stop=True)
+                st["bff_ps"] = mm.tile([P, D], F32, name="bff_ps", tag="mm1")
+                nc.tensor.matmul(
+                    out=st["bff_ps"][:], lhsT=ones16[:], rhs=rows[:, D : 2 * D], start=True, stop=True
+                )
+                st["ln_ps"] = mm.tile([P, P], BF16, name="ln_ps", tag="mm2")
+                nc.tensor.transpose(st["ln_ps"][:], lnrows[:], ident16[:])
+            elif k == "BOBC":
+                nc.vector.tensor_copy(out=bo_bc[:], in_=st["bo_ps"][:])
+                nc.vector.tensor_copy(out=bff_bc[:], in_=st["bff_ps"][:])
+                nc.vector.tensor_copy(out=gb8[:], in_=st["ln_ps"][:, 0:8])
+            elif k == "TAW":
+                words_to_psum(wo_raw, g, g, name)
+            elif k == "P1W":
+                words_out(wo_gr, g, ("TAW", g, -1), name in P1W_V)
+            elif k == "QWo":
+                nc.vector.quantize_mx(out=wo_cod[:].bitcast(FP8X4), scales=wo_scl[:], in_=wo_gr[:])
+            elif k == "TW2":
+                ps = xt.tile([P, 4, 2 * P], BF16, name="w2_ps", tag="xtp%d" % (2 + g))
+                for r2 in range(2):
+                    for j in range(4):
+                        c0 = D * (2 * g + r2) + P * j
+                        nc.tensor.transpose(ps[:, j, P * r2 : P * r2 + P], w2_raw[:, c0 : c0 + P], ident16[:])
+                st[name] = ps
+            elif k == "W2C":
+                w2_g3 = w2_gr[:].rearrange("p (f j) -> p f j", j=4)
+                nc.scalar.copy(
+                    out=w2_g3[:, 256 * g : 256 * g + 256, :],
+                    in_=st[("TW2", g, -1)][:].rearrange("p j f -> p f j"),
+                )
+            elif k == "QW2":
+                nc.vector.quantize_mx(out=w2_cod[:].bitcast(FP8X4), scales=w2_scl[:], in_=w2_gr[:])
+            elif k == "HBG":
+                hh = slot(("hh", g), lambda: work.tile([P, GW], F32, name="hh", tag="hh", bufs=4))
+                eng = nc.vector if name in HB_V else nc.gpsimd
                 eng.tensor_tensor(out=hh[:, sl], in0=hid_sb[g][:, sl], in1=bo_bc[:], op=ALU.add)
-            st[g]["hh"] = hh
-
-        def m1(g):
-            st[g]["s1"] = []
-            for i in range(GT):
-                cs = slice(P * i, P * i + P)
+            elif k == "TA":
+                words_to_psum(att_sb[g], i, (2 + i) if g == 0 else i, name)
+            elif k == "P1":
+                agr = slot(
+                    ("agr", g),
+                    lambda: work.tile([P, GW], BF16, name="agr", tag="agr", bufs=2, align_bytes=64),
+                )
+                words_out(agr, i, ("TA", g, i), name in P1_V)
+            elif k == "Q1":
+                acod = work.tile([P, D], U32, name="acod", tag="acod", bufs=3, align_bytes=64)
+                ascl = work.tile([P, D], U8, name="ascl", tag="ascl", bufs=3, align_bytes=64)
+                nc.vector.quantize_mx(out=acod[:].bitcast(FP8X4), scales=ascl[:], in_=st[("agr", g)][:])
+                st[("acod", g)] = acod
+                st[("ascl", g)] = ascl
+            elif k == "M1":
                 s1 = mm.tile([P, D], F32, name="s1", tag="mm%d" % i)
                 nc.tensor.matmul_mx(
                     out=s1[:],
-                    lhsT=st[g]["acod"][:, cs].bitcast(FP8X4),
-                    lhsT_scale=st[g]["ascl"][:, cs],
+                    lhsT=st[("acod", g)][:, cs].bitcast(FP8X4),
+                    lhsT_scale=st[("ascl", g)][:, cs],
                     rhs=wo_cod[:].bitcast(FP8X4),
                     rhs_scale=wo_scl[:],
                     start=True,
                     stop=True,
                 )
-                st[g]["s1"].append(s1)
-
-        def c4(g):
-            hh = st[g]["hh"]
-            hsum = work.tile([P, GT], F32, name="hsum", tag="hsum", bufs=3)
-            for i in range(GT):
-                sl = slice(D * i, D * i + D)
+                st[("s1", g, i)] = s1
+            elif k == "C":
+                hsum = slot(("hsum", g), lambda: work.tile([P, GT], F32, name="hsum", tag="hsum", bufs=4))
+                hh = st[("hh", g)]
                 nc.vector.scalar_tensor_tensor(
                     out=hh[:, sl],
-                    in0=st[g]["s1"][i][:],
+                    in0=st[("s1", g, i)][:],
                     scalar=1.0,
                     in1=hh[:, sl],
                     op0=ALU.mult,
                     op1=ALU.add,
                     accum_out=hsum[:, i : i + 1],
                 )
-            st[g]["hsum"] = hsum
-            nc.sync.dma_start(out=o0_v[:, g * GW : (g + 1) * GW], in_=hh[:])
-
-        def sq4(g):
-            hh = st[g]["hh"]
-            negmean = work.tile([P, GT], F32, name="negmean", tag="negmean", bufs=3)
-            ssq = work.tile([P, GT], F32, name="ssq", tag="ssq", bufs=3)
-            for i in range(GT):
-                sl = slice(D * i, D * i + D)
-                nc.scalar.mul(
-                    out=negmean[:, i : i + 1], in_=st[g]["hsum"][:, i : i + 1], mul=-1.0 / D
+            elif k == "STH":
+                nc.sync.dma_start(out=o0_v[:, g * GW : (g + 1) * GW], in_=st[("hh", g)][:])
+            elif k == "SQ":
+                negmean = slot(
+                    ("negmean", g), lambda: work.tile([P, GT], F32, name="negmean", tag="negmean", bufs=4)
                 )
+                ssq = slot(("ssq", g), lambda: work.tile([P, GT], F32, name="ssq", tag="ssq", bufs=4))
+                nc.scalar.mul(out=negmean[:, i : i + 1], in_=st[("hsum", g)][:, i : i + 1], mul=-1.0 / D)
                 junk = work.tile([P, D], BF16, name="junk", tag="junk")
                 nc.scalar.activation(
                     out=junk[:],
-                    in_=hh[:, sl],
+                    in_=st[("hh", g)][:, sl],
                     func=ACT.Square,
                     bias=negmean[:, i : i + 1],
                     scale=1.0,
                     accum_out=ssq[:, i : i + 1],
                 )
-            st[g]["negmean"] = negmean
-            st[g]["ssq"] = ssq
-
-        def powg(g):
-            veps = work.tile([P, GT], F32, name="veps", tag="veps", bufs=3)
-            nc.gpsimd.tensor_scalar(
-                out=veps[:],
-                in0=st[g]["ssq"][:],
-                scalar1=1.0 / D,
-                scalar2=LN_EPS,
-                op0=ALU.mult,
-                op1=ALU.add,
-            )
-            rstd = work.tile([P, GT], F32, name="rstd", tag="rstd", bufs=3)
-            nc.gpsimd.tensor_tensor(out=rstd[:], in0=veps[:], in1=neghalf[:], op=ALU.pow)
-            st[g]["rstd"] = rstd
-            if len(XH_ON_S) > 0:
-                nmr = work.tile([P, GT], F32, name="nmr", tag="nmr", bufs=3)
-                nc.gpsimd.tensor_tensor(out=nmr[:], in0=st[g]["negmean"][:], in1=rstd[:], op=ALU.mult)
-                st[g]["nmr"] = nmr
-
-        def xh_tx(g):
-            hh = st[g]["hh"]
-            xh = work.tile([P, GW], F32, name="xh", tag="xh", bufs=XH_BUFS)
-            xtp = [xt.tile([P, D], F32, name="xtp%d" % j, tag="xtp%d" % j) for j in range(4)]
-            for i in range(GT):
-                sl = slice(D * i, D * i + D)
-                if i in XH_ON_S:
-                    nc.scalar.activation(
-                        out=xh[:, sl],
-                        in_=hh[:, sl],
-                        func=ACT.Identity,
-                        scale=st[g]["rstd"][:, i : i + 1],
-                        bias=st[g]["nmr"][:, i : i + 1],
+            elif k == "POW":
+                veps = work.tile([P, GT], F32, name="veps", tag="veps", bufs=4)
+                nc.gpsimd.tensor_scalar(
+                    out=veps[:],
+                    in0=st[("ssq", g)][:],
+                    scalar1=1.0 / D,
+                    scalar2=LN_EPS,
+                    op0=ALU.mult,
+                    op1=ALU.add,
+                )
+                rstd = work.tile([P, GT], F32, name="rstd", tag="rstd", bufs=4)
+                nc.gpsimd.tensor_tensor(out=rstd[:], in0=veps[:], in1=neghalf[:], op=ALU.pow)
+                st[("rstd", g)] = rstd
+            elif k == "XH":
+                xh = slot(("xh", g), lambda: work.tile([P, GW], F32, name="xh", tag="xh", bufs=2))
+                eng = nc.gpsimd if name in XH_G else nc.vector
+                eng.tensor_scalar(
+                    out=xh[:, sl],
+                    in0=st[("hh", g)][:, sl],
+                    scalar1=st[("negmean", g)][:, i : i + 1],
+                    scalar2=st[("rstd", g)][:, i : i + 1],
+                    op0=ALU.add,
+                    op1=ALU.mult,
+                )
+            elif k == "TX":
+                xtp = xt.tile([P, D], F32, name="xtp", tag="xtp%d" % i)
+                for t in range(GT):
+                    c0 = D * t + P * i
+                    nc.tensor.transpose(xtp[:, P * t : P * t + P], st[("xh", g)][:, c0 : c0 + P], ident32[:])
+                st[("xtp", g, i)] = xtp
+            elif k == "GB":
+                n_t = slot(("n_t", g), lambda: work.tile([P, 4, D], BF16, name="n_t", tag="n_t", bufs=3))
+                if name in GB_V:
+                    nc.vector.tensor_scalar(
+                        out=n_t[:, i, :],
+                        in0=st[("xtp", g, i)][:],
+                        scalar1=gb8[:, i : i + 1],
+                        scalar2=gb8[:, 4 + i : 5 + i],
+                        op0=ALU.mult,
+                        op1=ALU.add,
                     )
                 else:
-                    nc.vector.tensor_scalar(
-                        out=xh[:, sl],
-                        in0=hh[:, sl],
-                        scalar1=st[g]["negmean"][:, i : i + 1],
-                        scalar2=st[g]["rstd"][:, i : i + 1],
-                        op0=ALU.add,
-                        op1=ALU.mult,
+                    nc.scalar.activation(
+                        out=n_t[:, i, :],
+                        in_=st[("xtp", g, i)][:],
+                        func=ACT.Identity,
+                        scale=gb8[:, i : i + 1],
+                        bias=gb8[:, 4 + i : 5 + i],
                     )
-                for j in range(4):
-                    c0 = D * i + P * j
-                    nc.tensor.transpose(xtp[j][:, P * i : P * i + P], xh[:, c0 : c0 + P], ident32[:])
-            st[g]["xtp"] = xtp
-
-        def gbs(g):
-            n_t = work.tile([P, 4, D], BF16, name="n_t", tag="n_t")
-            for j in range(4):
-                nc.scalar.activation(
-                    out=n_t[:, j, :],
-                    in_=st[g]["xtp"][j][:],
-                    func=ACT.Identity,
-                    scale=gb8[:, j : j + 1],
-                    bias=gb8[:, 4 + j : 5 + j],
+            elif k == "RG":
+                ngr = work.tile([P, GW], BF16, name="ngr", tag="ngr", bufs=2, align_bytes=64)
+                nc.vector.tensor_copy(
+                    out=ngr[:].rearrange("p (c i t) -> p c t i", i=4, t=4),
+                    in_=st[("n_t", g)][:].rearrange("p t (c i) -> p c t i", i=4),
                 )
-            st[g]["n_t"] = n_t
-
-        def rg_q2(g):
-            ngr = work.tile([P, GW], BF16, name="ngr", tag="ngr", align_bytes=64)
-            nc.vector.tensor_copy(
-                out=ngr[:].rearrange("p (c i t) -> p c t i", i=4, t=4),
-                in_=st[g]["n_t"][:].rearrange("p t (c i) -> p c t i", i=4),
-            )
-            ncod = work.tile([P, D], U32, name="ncod", tag="ncod", align_bytes=64)
-            nscl = work.tile([P, D], U8, name="nscl", tag="nscl", align_bytes=64)
-            nc.vector.quantize_mx(out=ncod[:].bitcast(FP8X4), scales=nscl[:], in_=ngr[:])
-            st[g]["ncod"] = ncod
-            st[g]["nscl"] = nscl
-
-        def m2(g):
-            st[g]["s2"] = []
-            for i in range(GT):
-                cs = slice(P * i, P * i + P)
+                st[("ngr", g)] = ngr
+            elif k == "Q2":
+                ncod = work.tile([P, D], U32, name="ncod", tag="ncod", bufs=3, align_bytes=64)
+                nscl = work.tile([P, D], U8, name="nscl", tag="nscl", bufs=3, align_bytes=64)
+                nc.vector.quantize_mx(out=ncod[:].bitcast(FP8X4), scales=nscl[:], in_=st[("ngr", g)][:])
+                st[("ncod", g)] = ncod
+                st[("nscl", g)] = nscl
+            elif k == "M2":
                 s2 = mm.tile([P, D], F32, name="s2", tag="mm%d" % i)
                 nc.tensor.matmul_mx(
                     out=s2[:],
-                    lhsT=st[g]["ncod"][:, cs].bitcast(FP8X4),
-                    lhsT_scale=st[g]["nscl"][:, cs],
+                    lhsT=st[("ncod", g)][:, cs].bitcast(FP8X4),
+                    lhsT_scale=st[("nscl", g)][:, cs],
                     rhs=w2_cod[:].bitcast(FP8X4),
                     rhs_scale=w2_scl[:],
                     start=True,
                     stop=True,
                 )
-                st[g]["s2"].append(s2)
-
-        def hb4(g):
-            aa = work.tile([P, GW], F32, name="aa", tag="aa", bufs=3)
-            for i in range(GT):
-                sl = slice(D * i, D * i + D)
-                nc.vector.tensor_tensor(out=aa[:, sl], in0=st[g]["s2"][i][:], in1=bff_bc[:], op=ALU.add)
-            st[g]["aa"] = aa
-
-        def ge4(g):
-            aa = st[g]["aa"]
-            for i in range(GT):
-                sl = slice(D * i, D * i + D)
+                st[("s2", g, i)] = s2
+            elif k == "HB":
+                aa = slot(("aa", g), lambda: work.tile([P, GW], F32, name="aa", tag="aa", bufs=3))
+                nc.vector.tensor_tensor(out=aa[:, sl], in0=st[("s2", g, i)][:], in1=bff_bc[:], op=ALU.add)
+            elif k == "GE":
+                aa = st[("aa", g)]
                 nc.scalar.activation(out=aa[:, sl], in_=aa[:, sl], func=ACT.Gelu)
-                if g == GROUPS - 1:
-                    nc.sync.dma_start(out=o1_v[:, g * GW + D * i : g * GW + D * i + D], in_=aa[:, sl])
-            if g < GROUPS - 1:
-                nc.sync.dma_start(out=o1_v[:, g * GW : (g + 1) * GW], in_=aa[:])
+            elif k == "STA":
+                nc.sync.dma_start(out=o1_v[:, g * GW : (g + 1) * GW], in_=st[("aa", g)][:])
+            elif k == "STL":
+                nc.sync.dma_start(out=o1_v[:, g * GW + D * i : g * GW + D * i + D], in_=st[("aa", g)][:, sl])
+            else:
+                assert k == "MEMS"
+                nc.vector.memset(rows[:], 0.0)
+                nc.vector.memset(lnrows[:], 0.0)
+                nc.vector.memset(zero1[:], 0.0)
+                nc.vector.memset(ones16[:], 1.0)
+                nc.vector.memset(neghalf[:], -0.5)
 
-        wo_cod = const.tile([P, D], U32, name="wo_cod", align_bytes=64)
-        wo_scl = const.tile([P, D], U8, name="wo_scl", align_bytes=64)
-        w2_cod = const.tile([P, D], U32, name="w2_cod", align_bytes=64)
-        w2_scl = const.tile([P, D], U8, name="w2_scl", align_bytes=64)
-        w2_gr = const.tile([P, GW], BF16, name="w2_gr", align_bytes=64)
-
-        wo_ps = words_to_psum(wo_raw, (0, 1))
-        ta(0, (2, 3))
-        wo_gr = words_out(wo_ps, "sv")
-        p1(0, "sv")
-        nc.vector.quantize_mx(out=wo_cod[:].bitcast(FP8X4), scales=wo_scl[:], in_=wo_gr[:])
-        q1(0)
-        hbg(0)
-        hbg(1)
-        m1(0)
-
-        def has(g):
-            return 0 <= g < GROUPS
-
-        for p in range(GROUPS + 3):
-            x, w, y, z, e = p, p + 1, p - 1, p - 2, p - 3
-            if has(x):
-                c4(x)
-            if has(z):
-                gbs(z)
-            if has(w):
-                ta(w, (0, 1))
-                p1(w, "ss")
-            if p == 0:
-                w2_ps = []
-                for h in range(2):
-                    ps = xt.tile([P, 4, 2 * P], BF16, name="w2_ps", tag="xtp%d" % (2 + h))
-                    for r2 in range(2):
-                        for j in range(4):
-                            c0 = D * (2 * h + r2) + P * j
-                            nc.tensor.transpose(
-                                ps[:, j, P * r2 : P * r2 + P], w2_raw[:, c0 : c0 + P], ident16[:]
-                            )
-                    w2_ps.append(ps)
-            if has(z):
-                rg_q2(z)
-            if has(w):
-                q1(w)
-            if p == 1:
-                nc.vector.quantize_mx(out=w2_cod[:].bitcast(FP8X4), scales=w2_scl[:], in_=w2_gr[:])
-            if has(z):
-                m2(z)
-            if not has(z) and has(x + 1):
-                m1(x + 1)
-            if has(y):
-                xh_tx(y)
-            if has(x):
-                sq4(x)
-            if p == 0:
-                w2_g3 = w2_gr[:].rearrange("p (f j) -> p f j", j=4)
-                for h in range(2):
-                    nc.scalar.copy(
-                        out=w2_g3[:, 256 * h : 256 * h + 256, :],
-                        in_=w2_ps[h][:].rearrange("p j f -> p f j"),
-                    )
-            if has(e):
-                ge4(e)
-            if has(z):
-                hb4(z)
-            if has(z) and has(x + 1):
-                m1(x + 1)
-            if has(x):
-                powg(x)
-            if has(p + 2):
-                hbg(p + 2)
+        for k, g, i in ORDER:
+            emit(k, g, i)

@@ -22,87 +22,12 @@ LN_EPS = 1e-5
 
 FLOPS = 2 * 2 * TOKENS * D * D
 
-HB_V = frozenset((("HBG", 0, 0), ("HBG", 0, 1), ("HBG", 0, 2), ("HBG", 0, 3), ("HBG", 1, 0), ("HBG", 1, 1), ("HBG", 1, 2), ("HBG", 1, 3), ("HBG", 2, 0), ("HBG", 2, 1), ("HBG", 2, 2), ("HBG", 2, 3),))
-XH_G = frozenset((("XH", 0, 2), ("XH", 0, 3), ("XH", 1, 2), ("XH", 1, 3), ("XH", 2, 2), ("XH", 2, 3), ("XH", 3, 2), ("XH", 3, 3), ("XH", 4, 2), ("XH", 4, 3), ("XH", 5, 2), ("XH", 5, 3), ("XH", 6, 2), ("XH", 6, 3), ("XH", 7, 2), ("XH", 7, 3),))
-GB_V = frozenset(())
-P1_V = frozenset(())
-P1W_V = frozenset((("P1W", 1, -1),))
-
-ORDER = (
-    ("MEMS", -1, -1), ("IDENT", -1, -1), ("WARM", -1, -1), ("LDS", -1, -1), ("LDH", 0, -1), ("BOMM", -1, -1),
-    ("LDWO", -1, -1), ("BOBC", -1, -1), ("LDA", 0, -1), ("HBG", 0, 0), ("TAW", 0, -1), ("HBG", 0, 1),
-    ("LDH", 1, -1), ("HBG", 0, 2), ("TAW", 1, -1), ("P1W", 0, -1), ("HBG", 0, 3), ("TA", 0, 0),
-    ("LDH", 2, -1), ("P1W", 1, -1), ("TA", 0, 1), ("QWo", -1, -1), ("P1", 0, 0), ("LDA", 1, -1),
-    ("HBG", 1, 0), ("P1", 0, 1), ("HBG", 1, 1), ("LDW2", -1, -1), ("HBG", 1, 2), ("TA", 1, 0),
-    ("Q1", 0, -1), ("LDA", 2, -1), ("TA", 1, 1), ("HBG", 1, 3), ("P1", 1, 0), ("TW2", 0, -1),
-    ("LDH", 3, -1), ("HBG", 2, 0), ("P1", 1, 1), ("M1", 0, 0), ("HBG", 2, 1), ("M1", 0, 1),
-    ("W2C", 0, -1), ("M1", 0, 2), ("LDA", 3, -1), ("C", 0, 0), ("M1", 0, 3), ("TA", 2, 0),
-    ("HBG", 3, 0), ("C", 0, 1), ("LDH", 4, -1), ("TA", 2, 1), ("SQ", 0, 0), ("C", 0, 2),
-    ("TW2", 1, -1), ("SQ", 0, 1), ("C", 0, 3), ("HBG", 3, 1), ("LDA", 4, -1), ("SQ", 0, 2),
-    ("Q1", 1, -1), ("LDH", 5, -1), ("SQ", 0, 3), ("HBG", 2, 2), ("HBG", 3, 2), ("M1", 1, 0),
-    ("HBG", 2, 3), ("P1", 2, 0), ("M1", 1, 1), ("LDA", 5, -1), ("M1", 1, 2), ("P1", 2, 1),
-    ("C", 1, 0), ("M1", 1, 3), ("W2C", 1, -1), ("C", 1, 1), ("POW", 0, -1), ("LDH", 6, -1),
-    ("C", 1, 2), ("XH", 0, 2), ("SQ", 1, 0), ("C", 1, 3), ("LDA", 6, -1), ("SQ", 1, 1),
-    ("XH", 0, 3), ("XH", 0, 0), ("XH", 0, 1), ("SQ", 1, 2), ("LDH", 7, -1), ("Q1", 2, -1),
-    ("HBG", 3, 3), ("SQ", 1, 3), ("TX", 0, 0), ("QW2", -1, -1), ("LDA", 7, -1), ("TX", 0, 1),
-    ("POW", 1, -1), ("GB", 0, 0), ("M1", 2, 0), ("STH", 0, -1), ("M1", 2, 1), ("GB", 0, 1),
-    ("XH", 1, 2), ("M1", 2, 2), ("C", 2, 0), ("TA", 3, 0), ("XH", 1, 3), ("XH", 1, 0),
-    ("TA", 3, 1), ("XH", 1, 1), ("SQ", 2, 0), ("C", 2, 1), ("STH", 1, -1), ("M1", 2, 3),
-    ("P1", 3, 0), ("TX", 0, 2), ("C", 2, 2), ("HBG", 4, 0), ("P1", 3, 1), ("C", 2, 3),
-    ("TX", 0, 3), ("SQ", 2, 1), ("TX", 1, 0), ("Q1", 3, -1), ("HBG", 4, 1), ("SQ", 2, 2),
-    ("STH", 2, -1), ("TX", 1, 1), ("SQ", 2, 3), ("M1", 3, 0), ("GB", 1, 0), ("M1", 3, 1),
-    ("HBG", 4, 2), ("M1", 3, 2), ("C", 3, 0), ("GB", 1, 1), ("M1", 3, 3), ("TA", 4, 0),
-    ("C", 3, 1), ("GB", 0, 2), ("POW", 2, -1), ("GB", 0, 3), ("C", 3, 2), ("TA", 4, 1),
-    ("P1", 4, 0), ("C", 3, 3), ("TX", 1, 2), ("XH", 2, 2), ("P1", 4, 1), ("XH", 2, 0),
-    ("TX", 1, 3), ("XH", 2, 1), ("XH", 2, 3), ("STH", 3, -1), ("SQ", 3, 0), ("RG", 0, -1),
-    ("HBG", 4, 3), ("SQ", 3, 1), ("TX", 2, 0), ("Q1", 4, -1), ("SQ", 3, 2), ("TX", 2, 1),
-    ("Q2", 0, -1), ("SQ", 3, 3), ("HBG", 5, 0), ("M1", 4, 0), ("GB", 2, 0), ("M1", 4, 1),
-    ("M1", 4, 2), ("GB", 2, 1), ("C", 4, 0), ("M1", 4, 3), ("TA", 5, 0), ("POW", 3, -1),
-    ("GB", 1, 2), ("C", 4, 1), ("GB", 1, 3), ("TA", 5, 1), ("C", 4, 2), ("XH", 3, 2),
-    ("P1", 5, 0), ("M2", 0, 0), ("XH", 3, 0), ("M2", 0, 1), ("XH", 3, 3), ("XH", 3, 1),
-    ("P1", 5, 1), ("M2", 0, 2), ("C", 4, 3), ("TX", 2, 2), ("SQ", 4, 0), ("HBG", 5, 1),
-    ("HB", 0, 0), ("TX", 3, 0), ("SQ", 4, 1), ("STH", 4, -1), ("Q1", 5, -1), ("TX", 3, 1),
-    ("SQ", 4, 2), ("HB", 0, 1), ("HBG", 5, 2), ("HB", 0, 2), ("M2", 0, 3), ("GB", 3, 0),
-    ("TX", 2, 3), ("RG", 1, -1), ("GB", 3, 1), ("TA", 6, 0), ("SQ", 4, 3), ("HBG", 5, 3),
-    ("HB", 0, 3), ("TA", 6, 1), ("GB", 2, 2), ("Q2", 1, -1), ("P1", 6, 0), ("M1", 5, 0),
-    ("POW", 4, -1), ("M1", 5, 1), ("P1", 6, 1), ("M1", 5, 2), ("C", 5, 0), ("M1", 5, 3),
-    ("GB", 2, 3), ("TX", 3, 2), ("XH", 4, 2), ("C", 5, 1), ("GE", 0, 0), ("M2", 1, 0),
-    ("XH", 4, 3), ("C", 5, 2), ("TX", 3, 3), ("SQ", 5, 0), ("C", 5, 3), ("HBG", 6, 0),
-    ("GB", 3, 2), ("M2", 1, 1), ("M2", 1, 2), ("XH", 4, 0), ("GB", 3, 3), ("XH", 4, 1),
-    ("M2", 1, 3), ("STH", 5, -1), ("Q1", 6, -1), ("SQ", 5, 1), ("HBG", 6, 1), ("TX", 4, 0),
-    ("HB", 1, 0), ("SQ", 5, 2), ("HB", 1, 1), ("TX", 4, 1), ("SQ", 5, 3), ("HB", 1, 2),
-    ("M1", 6, 0), ("HBG", 6, 2), ("GB", 4, 0), ("M1", 6, 1), ("HB", 1, 3), ("TX", 4, 2),
-    ("GB", 4, 1), ("RG", 2, -1), ("M1", 6, 2), ("GE", 0, 1), ("M1", 6, 3), ("HBG", 6, 3),
-    ("TA", 7, 0), ("GE", 0, 2), ("C", 6, 0), ("GE", 0, 3), ("TA", 7, 1), ("C", 6, 1),
-    ("P1", 7, 0), ("POW", 5, -1), ("TX", 4, 3), ("C", 6, 2), ("STA", 0, -1), ("P1", 7, 1),
-    ("C", 6, 3), ("HBG", 7, 0), ("GB", 4, 2), ("Q2", 2, -1), ("GB", 4, 3), ("Q1", 7, -1),
-    ("SQ", 6, 0), ("M2", 2, 0), ("HBG", 7, 1), ("STH", 6, -1), ("XH", 5, 0), ("M2", 2, 1),
-    ("XH", 5, 1), ("SQ", 6, 1), ("M2", 2, 2), ("HB", 2, 0), ("M2", 2, 3), ("SQ", 6, 2),
-    ("HB", 2, 1), ("HBG", 7, 2), ("SQ", 6, 3), ("M1", 7, 0), ("HB", 2, 2), ("M1", 7, 1),
-    ("GE", 1, 0), ("HB", 2, 3), ("M1", 7, 2), ("GE", 1, 1), ("RG", 3, -1), ("HBG", 7, 3),
-    ("M1", 7, 3), ("GE", 1, 2), ("GE", 1, 3), ("C", 7, 0), ("XH", 5, 2), ("GE", 2, 0),
-    ("C", 7, 1), ("STA", 1, -1), ("SQ", 7, 0), ("C", 7, 2), ("XH", 5, 3), ("SQ", 7, 1),
-    ("C", 7, 3), ("POW", 6, -1), ("SQ", 7, 2), ("Q2", 3, -1), ("TX", 5, 0), ("XH", 6, 2),
-    ("SQ", 7, 3), ("RG", 4, -1), ("STH", 7, -1), ("TX", 5, 1), ("XH", 6, 3), ("GB", 5, 0),
-    ("TX", 5, 2), ("XH", 6, 0), ("XH", 6, 1), ("GB", 5, 1), ("POW", 7, -1), ("TX", 5, 3),
-    ("Q2", 4, -1), ("GB", 5, 2), ("M2", 3, 0), ("M2", 3, 1), ("GB", 5, 3), ("XH", 7, 2),
-    ("XH", 7, 0), ("M2", 3, 2), ("HB", 3, 0), ("M2", 3, 3), ("GE", 2, 1), ("TX", 6, 0),
-    ("XH", 7, 3), ("HB", 3, 1), ("GE", 2, 2), ("TX", 6, 1), ("HB", 3, 2), ("GE", 2, 3),
-    ("HB", 3, 3), ("TX", 6, 2), ("GB", 6, 0), ("RG", 5, -1), ("TX", 6, 3), ("STA", 2, -1),
-    ("GB", 6, 1), ("M2", 4, 0), ("GB", 6, 2), ("XH", 7, 1), ("M2", 4, 1), ("Q2", 5, -1),
-    ("M2", 4, 2), ("GB", 6, 3), ("M2", 4, 3), ("HB", 4, 0), ("TX", 7, 0), ("GE", 3, 0),
-    ("HB", 4, 1), ("GE", 3, 1), ("TX", 7, 1), ("HB", 4, 2), ("GE", 3, 2), ("TX", 7, 2),
-    ("HB", 4, 3), ("GE", 3, 3), ("TX", 7, 3), ("RG", 6, -1), ("GB", 7, 0), ("STA", 3, -1),
-    ("M2", 5, 0), ("GB", 7, 1), ("M2", 5, 1), ("Q2", 6, -1), ("M2", 5, 2), ("GB", 7, 2),
-    ("M2", 5, 3), ("HB", 5, 0), ("GB", 7, 3), ("HB", 5, 1), ("GE", 4, 0), ("M2", 6, 0),
-    ("HB", 5, 2), ("GE", 4, 1), ("M2", 6, 1), ("HB", 5, 3), ("GE", 4, 2), ("M2", 6, 2),
-    ("RG", 7, -1), ("GE", 4, 3), ("M2", 6, 3), ("GE", 5, 0), ("Q2", 7, -1), ("STA", 4, -1),
-    ("GE", 5, 1), ("HB", 6, 0), ("GE", 5, 2), ("HB", 6, 1), ("GE", 5, 3), ("M2", 7, 0),
-    ("HB", 6, 2), ("GE", 6, 0), ("M2", 7, 1), ("HB", 6, 3), ("STA", 5, -1), ("GE", 6, 1),
-    ("M2", 7, 2), ("HB", 7, 0), ("GE", 6, 2), ("M2", 7, 3), ("HB", 7, 1), ("GE", 6, 3),
-    ("HB", 7, 2), ("GE", 7, 0), ("HB", 7, 3), ("STA", 6, -1), ("GE", 7, 1), ("GE", 7, 2),
-    ("GE", 7, 3), ("STL", 7, 0), ("STL", 7, 1), ("STL", 7, 2), ("STL", 7, 3),
-)
+HB_ON_V = (0, 1, 2, 3)
+HB_HEAD = 3
+XH_ON_S = (2, 3)
+HH_BUFS = 5
+LAG2 = 2
+XH_BUFS = 3
 
 
 def tile_supervisedrefiner_pb_t_kernel(
@@ -115,7 +40,6 @@ def tile_supervisedrefiner_pb_t_kernel(
     o1_v = out_1.flatten_outer_dims().rearrange("(p t) d -> p (t d)", t=TILES)
 
     with ExitStack() as ctx:
-        ctx.enter_context(tc.manual_schedule())
         const = ctx.enter_context(tc.tile_pool(name="const", bufs=1))
         loads = ctx.enter_context(tc.tile_pool(name="loads", bufs=GROUPS))
         work = ctx.enter_context(tc.tile_pool(name="work", bufs=2))
@@ -123,263 +47,353 @@ def tile_supervisedrefiner_pb_t_kernel(
         xt = ctx.enter_context(tc.psum_pool(name="xt", bufs=1))
 
         rows = const.tile([P, 2 * D], BF16, name="rows")
+        nc.vector.memset(rows[:], 0.0)
         lnrows = const.tile([P, P], BF16, name="lnrows")
+        nc.vector.memset(lnrows[:], 0.0)
+        nc.sync.dma_start(out=rows[0:1, 0:D], in_=bo.unsqueeze(0))
+        nc.sync.dma_start(out=rows[0:1, D : 2 * D], in_=b_ff1.unsqueeze(0))
+        nc.sync.dma_start(out=lnrows[0:4, :], in_=ln2_g.rearrange("(j c) -> j c", c=P))
+        nc.sync.dma_start(out=lnrows[4:8, :], in_=ln2_b.rearrange("(j c) -> j c", c=P))
+
         wo_raw = const.tile([P, GW], BF16, name="wo_raw")
         w2_raw = const.tile([P, GW], BF16, name="w2_raw")
         att_sb = [loads.tile([P, GW], BF16, name="att_sb", tag="att") for g in range(GROUPS)]
         hid_sb = [loads.tile([P, GW], BF16, name="hid_sb", tag="hid") for g in range(GROUPS)]
+
+        def load_w(dst, src, halves):
+            step = 4 // halves
+            for h in range(halves):
+                nc.sync.dma_start(
+                    out=dst[:, h * step * D : (h + 1) * step * D].rearrange("p (r k) -> p r k", k=D),
+                    in_=src[h * step * P : (h + 1) * step * P, :].rearrange("(r p) k -> p r k", p=P),
+                )
+
+        def load_t(dst, src_v, g, halves):
+            step = GW // halves
+            for h in range(halves):
+                nc.sync.dma_start(
+                    out=dst[g][:, h * step : (h + 1) * step],
+                    in_=src_v[:, g * GW + h * step : g * GW + (h + 1) * step],
+                )
+
+        load_t(hid_sb, hid_v, 0, 1)
+        load_w(wo_raw, Wo, 2)
+        load_t(att_sb, att_v, 0, 2)
+        load_t(hid_sb, hid_v, 1, 1)
+        load_t(hid_sb, hid_v, 2, 1)
+        load_t(att_sb, att_v, 1, 1)
+        load_w(w2_raw, W_ff1, 1)
+        load_t(att_sb, att_v, 2, 1)
+        for g in range(3, GROUPS):
+            load_t(hid_sb, hid_v, g, 1)
+            load_t(att_sb, att_v, g, 1)
+
         zero1 = const.tile([P, 1], F32, name="zero1")
+        nc.vector.memset(zero1[:], 0.0)
         warm = const.tile([P, 1], F32, name="warm")
+        nc.scalar.activation(out=warm[:], in_=zero1[:], func=ACT.Gelu)
+
         ident32 = const.tile([P, P], F32, name="ident32")
+        make_identity(nc, ident32[:])
         ident16 = const.tile([P, P], BF16, name="ident16")
+        make_identity(nc, ident16[:])
         ones16 = const.tile([P, P], BF16, name="ones16")
+        nc.vector.memset(ones16[:], 1.0)
         neghalf = const.tile([P, GT], F32, name="neghalf")
+        nc.vector.memset(neghalf[:], -0.5)
+
         bo_bc = const.tile([P, D], BF16, name="bo_bc")
         bff_bc = const.tile([P, D], F32, name="bff_bc")
         gb8 = const.tile([P, 8], F32, name="gb8")
-        wo_cod = const.tile([P, D], U32, name="wo_cod", align_bytes=64)
-        wo_scl = const.tile([P, D], U8, name="wo_scl", align_bytes=64)
-        w2_cod = const.tile([P, D], U32, name="w2_cod", align_bytes=64)
-        w2_scl = const.tile([P, D], U8, name="w2_scl", align_bytes=64)
-        w2_gr = const.tile([P, GW], BF16, name="w2_gr", align_bytes=64)
-        wo_gr = const.tile([P, GW], BF16, name="wo_gr", align_bytes=64)
+        bo_ps = mm.tile([P, D], F32, name="bo_ps", tag="mm0")
+        nc.tensor.matmul(out=bo_ps[:], lhsT=ones16[:], rhs=rows[:, 0:D], start=True, stop=True)
+        nc.vector.tensor_copy(out=bo_bc[:], in_=bo_ps[:])
+        bff_ps = mm.tile([P, D], F32, name="bff_ps", tag="mm1")
+        nc.tensor.matmul(out=bff_ps[:], lhsT=ones16[:], rhs=rows[:, D : 2 * D], start=True, stop=True)
+        ln_ps = mm.tile([P, P], BF16, name="ln_ps", tag="mm2")
+        nc.tensor.transpose(ln_ps[:], lnrows[:], ident16[:])
+        nc.vector.tensor_copy(out=bff_bc[:], in_=bff_ps[:])
+        nc.vector.tensor_copy(out=gb8[:], in_=ln_ps[:, 0:8])
 
         st = {}
+        for g in range(GROUPS):
+            st[g] = {}
 
-        def slot(key, make):
-            if key not in st:
-                st[key] = make()
-            return st[key]
-
-        def load_w(dst, src):
-            nc.sync.dma_start(
-                out=dst[:].rearrange("p (r k) -> p r k", k=D), in_=src.rearrange("(r p) k -> p r k", p=P)
-            )
-
-        def words_to_psum(src, h, bank, key):
+        def words_to_psum(src, banks):
             src32 = src[:].bitcast(F32)
-            ps = xt.tile([P, 2, 2 * P], F32, name="at_ps", tag="xtp%d" % bank)
-            for i2 in range(2):
-                for u in range(2):
-                    c0 = 256 * (2 * h + i2) + P * u
-                    nc.tensor.transpose(ps[:, u, P * i2 : P * i2 + P], src32[:, c0 : c0 + P], ident32[:])
-            st[key] = ps
+            out = []
+            for h in range(2):
+                ps = xt.tile([P, 2, 2 * P], F32, name="at_ps", tag="xtp%d" % banks[h])
+                for i2 in range(2):
+                    for u in range(2):
+                        c0 = 256 * (2 * h + i2) + P * u
+                        nc.tensor.transpose(
+                            ps[:, u, P * i2 : P * i2 + P], src32[:, c0 : c0 + P], ident32[:]
+                        )
+                out.append(ps)
+            return out
 
-        def words_out(grouped, h, key, on_v):
+        def words_out(banks_ps, engines):
+            grouped = work.tile([P, GW], BF16, name="agr", tag="agr", align_bytes=64)
             g32 = grouped[:].bitcast(F32).rearrange("p (r u) -> p r u", u=2)
-            src_ap = st[key][:].rearrange("p u r -> p r u")
-            dst_ap = g32[:, 256 * h : 256 * h + 256, :]
-            if on_v:
-                nc.vector.tensor_copy(out=dst_ap, in_=src_ap)
-            else:
-                nc.scalar.copy(out=dst_ap, in_=src_ap)
+            for h in range(2):
+                src_ap = banks_ps[h][:].rearrange("p u r -> p r u")
+                dst_ap = g32[:, 256 * h : 256 * h + 256, :]
+                if engines[h] == "s":
+                    nc.scalar.copy(out=dst_ap, in_=src_ap)
+                else:
+                    nc.vector.tensor_copy(out=dst_ap, in_=src_ap)
+            return grouped
 
-        def emit(k, g, i):
-            name = (k, g, i)
-            sl = slice(D * i, D * i + D)
-            cs = slice(P * i, P * i + P)
-            if k == "LDS":
-                nc.sync.dma_start(out=rows[0:1, 0:D], in_=bo.unsqueeze(0))
-                nc.sync.dma_start(out=rows[0:1, D : 2 * D], in_=b_ff1.unsqueeze(0))
-                nc.sync.dma_start(out=lnrows[0:4, :], in_=ln2_g.rearrange("(j c) -> j c", c=P))
-                nc.sync.dma_start(out=lnrows[4:8, :], in_=ln2_b.rearrange("(j c) -> j c", c=P))
-            elif k == "LDWO":
-                load_w(wo_raw, Wo)
-            elif k == "LDW2":
-                load_w(w2_raw, W_ff1)
-            elif k == "LDA":
-                nc.sync.dma_start(out=att_sb[g][:], in_=att_v[:, g * GW : (g + 1) * GW])
-            elif k == "LDH":
-                nc.sync.dma_start(out=hid_sb[g][:], in_=hid_v[:, g * GW : (g + 1) * GW])
-            elif k == "IDENT":
-                make_identity(nc, ident32[:])
-                make_identity(nc, ident16[:])
-            elif k == "WARM":
-                nc.scalar.activation(out=warm[:], in_=zero1[:], func=ACT.Gelu)
-            elif k == "BOMM":
-                st["bo_ps"] = mm.tile([P, D], F32, name="bo_ps", tag="mm0")
-                nc.tensor.matmul(out=st["bo_ps"][:], lhsT=ones16[:], rhs=rows[:, 0:D], start=True, stop=True)
-                st["bff_ps"] = mm.tile([P, D], F32, name="bff_ps", tag="mm1")
-                nc.tensor.matmul(
-                    out=st["bff_ps"][:], lhsT=ones16[:], rhs=rows[:, D : 2 * D], start=True, stop=True
-                )
-                st["ln_ps"] = mm.tile([P, P], BF16, name="ln_ps", tag="mm2")
-                nc.tensor.transpose(st["ln_ps"][:], lnrows[:], ident16[:])
-            elif k == "BOBC":
-                nc.vector.tensor_copy(out=bo_bc[:], in_=st["bo_ps"][:])
-                nc.vector.tensor_copy(out=bff_bc[:], in_=st["bff_ps"][:])
-                nc.vector.tensor_copy(out=gb8[:], in_=st["ln_ps"][:, 0:8])
-            elif k == "TAW":
-                words_to_psum(wo_raw, g, g, name)
-            elif k == "P1W":
-                words_out(wo_gr, g, ("TAW", g, -1), name in P1W_V)
-            elif k == "QWo":
-                nc.vector.quantize_mx(out=wo_cod[:].bitcast(FP8X4), scales=wo_scl[:], in_=wo_gr[:])
-            elif k == "TW2":
-                ps = xt.tile([P, 4, 2 * P], BF16, name="w2_ps", tag="xtp%d" % (2 + g))
-                for r2 in range(2):
-                    for j in range(4):
-                        c0 = D * (2 * g + r2) + P * j
-                        nc.tensor.transpose(ps[:, j, P * r2 : P * r2 + P], w2_raw[:, c0 : c0 + P], ident16[:])
-                st[name] = ps
-            elif k == "W2C":
-                w2_g3 = w2_gr[:].rearrange("p (f j) -> p f j", j=4)
-                nc.scalar.copy(
-                    out=w2_g3[:, 256 * g : 256 * g + 256, :],
-                    in_=st[("TW2", g, -1)][:].rearrange("p j f -> p f j"),
-                )
-            elif k == "QW2":
-                nc.vector.quantize_mx(out=w2_cod[:].bitcast(FP8X4), scales=w2_scl[:], in_=w2_gr[:])
-            elif k == "HBG":
-                hh = slot(("hh", g), lambda: work.tile([P, GW], F32, name="hh", tag="hh", bufs=4))
-                eng = nc.vector if name in HB_V else nc.gpsimd
+        def ta(g, banks):
+            st[g]["at_ps"] = words_to_psum(att_sb[g], banks)
+
+        def p1(g, engines):
+            st[g]["agr"] = words_out(st[g]["at_ps"], engines)
+
+        def q1(g):
+            acod = work.tile([P, D], U32, name="acod", tag="acod", bufs=3, align_bytes=64)
+            ascl = work.tile([P, D], U8, name="ascl", tag="ascl", bufs=3, align_bytes=64)
+            nc.vector.quantize_mx(out=acod[:].bitcast(FP8X4), scales=ascl[:], in_=st[g]["agr"][:])
+            st[g]["acod"] = acod
+            st[g]["ascl"] = ascl
+
+        def hbg(g):
+            hh = work.tile([P, GW], F32, name="hh", tag="hh", bufs=HH_BUFS)
+            for i in range(GT):
+                sl = slice(D * i, D * i + D)
+                eng = nc.vector if (g < HB_HEAD or i in HB_ON_V) else nc.gpsimd
                 eng.tensor_tensor(out=hh[:, sl], in0=hid_sb[g][:, sl], in1=bo_bc[:], op=ALU.add)
-            elif k == "TA":
-                words_to_psum(att_sb[g], i, (2 + i) if g == 0 else i, name)
-            elif k == "P1":
-                agr = slot(
-                    ("agr", g),
-                    lambda: work.tile([P, GW], BF16, name="agr", tag="agr", bufs=2, align_bytes=64),
-                )
-                words_out(agr, i, ("TA", g, i), name in P1_V)
-            elif k == "Q1":
-                acod = work.tile([P, D], U32, name="acod", tag="acod", bufs=3, align_bytes=64)
-                ascl = work.tile([P, D], U8, name="ascl", tag="ascl", bufs=3, align_bytes=64)
-                nc.vector.quantize_mx(out=acod[:].bitcast(FP8X4), scales=ascl[:], in_=st[("agr", g)][:])
-                st[("acod", g)] = acod
-                st[("ascl", g)] = ascl
-            elif k == "M1":
+            st[g]["hh"] = hh
+
+        def m1(g):
+            st[g]["s1"] = []
+            for i in range(GT):
+                cs = slice(P * i, P * i + P)
                 s1 = mm.tile([P, D], F32, name="s1", tag="mm%d" % i)
                 nc.tensor.matmul_mx(
                     out=s1[:],
-                    lhsT=st[("acod", g)][:, cs].bitcast(FP8X4),
-                    lhsT_scale=st[("ascl", g)][:, cs],
+                    lhsT=st[g]["acod"][:, cs].bitcast(FP8X4),
+                    lhsT_scale=st[g]["ascl"][:, cs],
                     rhs=wo_cod[:].bitcast(FP8X4),
                     rhs_scale=wo_scl[:],
                     start=True,
                     stop=True,
                 )
-                st[("s1", g, i)] = s1
-            elif k == "C":
-                hsum = slot(("hsum", g), lambda: work.tile([P, GT], F32, name="hsum", tag="hsum", bufs=4))
-                hh = st[("hh", g)]
+                st[g]["s1"].append(s1)
+
+        def c4(g):
+            hh = st[g]["hh"]
+            hsum = work.tile([P, GT], F32, name="hsum", tag="hsum", bufs=3)
+            for i in range(GT):
+                sl = slice(D * i, D * i + D)
                 nc.vector.scalar_tensor_tensor(
                     out=hh[:, sl],
-                    in0=st[("s1", g, i)][:],
+                    in0=st[g]["s1"][i][:],
                     scalar=1.0,
                     in1=hh[:, sl],
                     op0=ALU.mult,
                     op1=ALU.add,
                     accum_out=hsum[:, i : i + 1],
                 )
-            elif k == "STH":
-                nc.sync.dma_start(out=o0_v[:, g * GW : (g + 1) * GW], in_=st[("hh", g)][:])
-            elif k == "SQ":
-                negmean = slot(
-                    ("negmean", g), lambda: work.tile([P, GT], F32, name="negmean", tag="negmean", bufs=4)
+            st[g]["hsum"] = hsum
+            nc.sync.dma_start(out=o0_v[:, g * GW : (g + 1) * GW], in_=hh[:])
+
+        def sq4(g):
+            hh = st[g]["hh"]
+            negmean = work.tile([P, GT], F32, name="negmean", tag="negmean", bufs=3)
+            ssq = work.tile([P, GT], F32, name="ssq", tag="ssq", bufs=3)
+            for i in range(GT):
+                sl = slice(D * i, D * i + D)
+                nc.scalar.mul(
+                    out=negmean[:, i : i + 1], in_=st[g]["hsum"][:, i : i + 1], mul=-1.0 / D
                 )
-                ssq = slot(("ssq", g), lambda: work.tile([P, GT], F32, name="ssq", tag="ssq", bufs=4))
-                nc.scalar.mul(out=negmean[:, i : i + 1], in_=st[("hsum", g)][:, i : i + 1], mul=-1.0 / D)
                 junk = work.tile([P, D], BF16, name="junk", tag="junk")
                 nc.scalar.activation(
                     out=junk[:],
-                    in_=st[("hh", g)][:, sl],
+                    in_=hh[:, sl],
                     func=ACT.Square,
                     bias=negmean[:, i : i + 1],
                     scale=1.0,
                     accum_out=ssq[:, i : i + 1],
                 )
-            elif k == "POW":
-                veps = work.tile([P, GT], F32, name="veps", tag="veps", bufs=4)
-                nc.gpsimd.tensor_scalar(
-                    out=veps[:],
-                    in0=st[("ssq", g)][:],
-                    scalar1=1.0 / D,
-                    scalar2=LN_EPS,
-                    op0=ALU.mult,
-                    op1=ALU.add,
-                )
-                rstd = work.tile([P, GT], F32, name="rstd", tag="rstd", bufs=4)
-                nc.gpsimd.tensor_tensor(out=rstd[:], in0=veps[:], in1=neghalf[:], op=ALU.pow)
-                st[("rstd", g)] = rstd
-            elif k == "XH":
-                xh = slot(("xh", g), lambda: work.tile([P, GW], F32, name="xh", tag="xh", bufs=2))
-                eng = nc.gpsimd if name in XH_G else nc.vector
-                eng.tensor_scalar(
-                    out=xh[:, sl],
-                    in0=st[("hh", g)][:, sl],
-                    scalar1=st[("negmean", g)][:, i : i + 1],
-                    scalar2=st[("rstd", g)][:, i : i + 1],
-                    op0=ALU.add,
-                    op1=ALU.mult,
-                )
-            elif k == "TX":
-                xtp = xt.tile([P, D], F32, name="xtp", tag="xtp%d" % i)
-                for t in range(GT):
-                    c0 = D * t + P * i
-                    nc.tensor.transpose(xtp[:, P * t : P * t + P], st[("xh", g)][:, c0 : c0 + P], ident32[:])
-                st[("xtp", g, i)] = xtp
-            elif k == "GB":
-                n_t = slot(("n_t", g), lambda: work.tile([P, 4, D], BF16, name="n_t", tag="n_t", bufs=3))
-                if name in GB_V:
-                    nc.vector.tensor_scalar(
-                        out=n_t[:, i, :],
-                        in0=st[("xtp", g, i)][:],
-                        scalar1=gb8[:, i : i + 1],
-                        scalar2=gb8[:, 4 + i : 5 + i],
-                        op0=ALU.mult,
-                        op1=ALU.add,
+            st[g]["negmean"] = negmean
+            st[g]["ssq"] = ssq
+
+        def powg(g):
+            veps = work.tile([P, GT], F32, name="veps", tag="veps", bufs=3)
+            nc.gpsimd.tensor_scalar(
+                out=veps[:],
+                in0=st[g]["ssq"][:],
+                scalar1=1.0 / D,
+                scalar2=LN_EPS,
+                op0=ALU.mult,
+                op1=ALU.add,
+            )
+            rstd = work.tile([P, GT], F32, name="rstd", tag="rstd", bufs=3)
+            nc.gpsimd.tensor_tensor(out=rstd[:], in0=veps[:], in1=neghalf[:], op=ALU.pow)
+            st[g]["rstd"] = rstd
+            if len(XH_ON_S) > 0:
+                nmr = work.tile([P, GT], F32, name="nmr", tag="nmr", bufs=3)
+                nc.gpsimd.tensor_tensor(out=nmr[:], in0=st[g]["negmean"][:], in1=rstd[:], op=ALU.mult)
+                st[g]["nmr"] = nmr
+
+        def xh_tx(g):
+            hh = st[g]["hh"]
+            xh = work.tile([P, GW], F32, name="xh", tag="xh", bufs=XH_BUFS)
+            xtp = [xt.tile([P, D], F32, name="xtp%d" % j, tag="xtp%d" % j) for j in range(4)]
+            for i in range(GT):
+                sl = slice(D * i, D * i + D)
+                if i in XH_ON_S:
+                    nc.scalar.activation(
+                        out=xh[:, sl],
+                        in_=hh[:, sl],
+                        func=ACT.Identity,
+                        scale=st[g]["rstd"][:, i : i + 1],
+                        bias=st[g]["nmr"][:, i : i + 1],
                     )
                 else:
-                    nc.scalar.activation(
-                        out=n_t[:, i, :],
-                        in_=st[("xtp", g, i)][:],
-                        func=ACT.Identity,
-                        scale=gb8[:, i : i + 1],
-                        bias=gb8[:, 4 + i : 5 + i],
+                    nc.vector.tensor_scalar(
+                        out=xh[:, sl],
+                        in0=hh[:, sl],
+                        scalar1=st[g]["negmean"][:, i : i + 1],
+                        scalar2=st[g]["rstd"][:, i : i + 1],
+                        op0=ALU.add,
+                        op1=ALU.mult,
                     )
-            elif k == "RG":
-                ngr = work.tile([P, GW], BF16, name="ngr", tag="ngr", bufs=2, align_bytes=64)
-                nc.vector.tensor_copy(
-                    out=ngr[:].rearrange("p (c i t) -> p c t i", i=4, t=4),
-                    in_=st[("n_t", g)][:].rearrange("p t (c i) -> p c t i", i=4),
+            for j in range(4):
+                for i in range(GT):
+                    c0 = D * i + P * j
+                    nc.tensor.transpose(xtp[j][:, P * i : P * i + P], xh[:, c0 : c0 + P], ident32[:])
+            st[g]["xtp"] = xtp
+
+        def gbs(g):
+            n_t = work.tile([P, 4, D], BF16, name="n_t", tag="n_t", bufs=LAG2 + 2)
+            for j in range(4):
+                nc.scalar.activation(
+                    out=n_t[:, j, :],
+                    in_=st[g]["xtp"][j][:],
+                    func=ACT.Identity,
+                    scale=gb8[:, j : j + 1],
+                    bias=gb8[:, 4 + j : 5 + j],
                 )
-                st[("ngr", g)] = ngr
-            elif k == "Q2":
-                ncod = work.tile([P, D], U32, name="ncod", tag="ncod", bufs=3, align_bytes=64)
-                nscl = work.tile([P, D], U8, name="nscl", tag="nscl", bufs=3, align_bytes=64)
-                nc.vector.quantize_mx(out=ncod[:].bitcast(FP8X4), scales=nscl[:], in_=st[("ngr", g)][:])
-                st[("ncod", g)] = ncod
-                st[("nscl", g)] = nscl
-            elif k == "M2":
+            st[g]["n_t"] = n_t
+
+        def rg_q2(g):
+            ngr = work.tile([P, GW], BF16, name="ngr", tag="ngr", align_bytes=64)
+            nc.vector.tensor_copy(
+                out=ngr[:].rearrange("p (c i t) -> p c t i", i=4, t=4),
+                in_=st[g]["n_t"][:].rearrange("p t (c i) -> p c t i", i=4),
+            )
+            ncod = work.tile([P, D], U32, name="ncod", tag="ncod", align_bytes=64)
+            nscl = work.tile([P, D], U8, name="nscl", tag="nscl", align_bytes=64)
+            nc.vector.quantize_mx(out=ncod[:].bitcast(FP8X4), scales=nscl[:], in_=ngr[:])
+            st[g]["ncod"] = ncod
+            st[g]["nscl"] = nscl
+
+        def m2(g):
+            st[g]["s2"] = []
+            for i in range(GT):
+                cs = slice(P * i, P * i + P)
                 s2 = mm.tile([P, D], F32, name="s2", tag="mm%d" % i)
                 nc.tensor.matmul_mx(
                     out=s2[:],
-                    lhsT=st[("ncod", g)][:, cs].bitcast(FP8X4),
-                    lhsT_scale=st[("nscl", g)][:, cs],
+                    lhsT=st[g]["ncod"][:, cs].bitcast(FP8X4),
+                    lhsT_scale=st[g]["nscl"][:, cs],
                     rhs=w2_cod[:].bitcast(FP8X4),
                     rhs_scale=w2_scl[:],
                     start=True,
                     stop=True,
                 )
-                st[("s2", g, i)] = s2
-            elif k == "HB":
-                aa = slot(("aa", g), lambda: work.tile([P, GW], F32, name="aa", tag="aa", bufs=3))
-                nc.vector.tensor_tensor(out=aa[:, sl], in0=st[("s2", g, i)][:], in1=bff_bc[:], op=ALU.add)
-            elif k == "GE":
-                aa = st[("aa", g)]
-                nc.scalar.activation(out=aa[:, sl], in_=aa[:, sl], func=ACT.Gelu)
-            elif k == "STA":
-                nc.sync.dma_start(out=o1_v[:, g * GW : (g + 1) * GW], in_=st[("aa", g)][:])
-            elif k == "STL":
-                nc.sync.dma_start(out=o1_v[:, g * GW + D * i : g * GW + D * i + D], in_=st[("aa", g)][:, sl])
-            else:
-                assert k == "MEMS"
-                nc.vector.memset(rows[:], 0.0)
-                nc.vector.memset(lnrows[:], 0.0)
-                nc.vector.memset(zero1[:], 0.0)
-                nc.vector.memset(ones16[:], 1.0)
-                nc.vector.memset(neghalf[:], -0.5)
+                st[g]["s2"].append(s2)
 
-        for k, g, i in ORDER:
-            emit(k, g, i)
+        def hb4(g):
+            aa = work.tile([P, GW], F32, name="aa", tag="aa", bufs=3)
+            for i in range(GT):
+                sl = slice(D * i, D * i + D)
+                nc.vector.tensor_tensor(out=aa[:, sl], in0=st[g]["s2"][i][:], in1=bff_bc[:], op=ALU.add)
+            st[g]["aa"] = aa
+
+        def ge4(g):
+            aa = st[g]["aa"]
+            for i in range(GT):
+                sl = slice(D * i, D * i + D)
+                nc.scalar.activation(out=aa[:, sl], in_=aa[:, sl], func=ACT.Gelu)
+                if g == GROUPS - 1:
+                    nc.sync.dma_start(out=o1_v[:, g * GW + D * i : g * GW + D * i + D], in_=aa[:, sl])
+            if g < GROUPS - 1:
+                nc.sync.dma_start(out=o1_v[:, g * GW : (g + 1) * GW], in_=aa[:])
+
+        wo_cod = const.tile([P, D], U32, name="wo_cod", align_bytes=64)
+        wo_scl = const.tile([P, D], U8, name="wo_scl", align_bytes=64)
+        w2_cod = const.tile([P, D], U32, name="w2_cod", align_bytes=64)
+        w2_scl = const.tile([P, D], U8, name="w2_scl", align_bytes=64)
+        w2_gr = const.tile([P, GW], BF16, name="w2_gr", align_bytes=64)
+
+        hbg(0)
+        wo_ps = words_to_psum(wo_raw, (0, 1))
+        ta(0, (2, 3))
+        wo_gr = words_out(wo_ps, "sv")
+        p1(0, "sv")
+        nc.vector.quantize_mx(out=wo_cod[:].bitcast(FP8X4), scales=wo_scl[:], in_=wo_gr[:])
+        q1(0)
+        m1(0)
+        hbg(1)
+        hbg(2)
+
+        def has(g):
+            return 0 <= g < GROUPS
+
+        for p in range(GROUPS + 3 + LAG2):
+            x, w, y, z = p, p + 1, p - 1, p - 2
+            r = z - LAG2
+            e = r - 1
+            if has(x):
+                c4(x)
+            if has(z):
+                gbs(z)
+            if has(w):
+                ta(w, (0, 1))
+                p1(w, "ss")
+            if p == 0:
+                w2_ps = []
+                for h in range(2):
+                    ps = xt.tile([P, 4, 2 * P], BF16, name="w2_ps", tag="xtp%d" % (2 + h))
+                    for r2 in range(2):
+                        for j in range(4):
+                            c0 = D * (2 * h + r2) + P * j
+                            nc.tensor.transpose(
+                                ps[:, j, P * r2 : P * r2 + P], w2_raw[:, c0 : c0 + P], ident16[:]
+                            )
+                    w2_ps.append(ps)
+            if has(r):
+                rg_q2(r)
+            if has(w):
+                q1(w)
+            if p == 1:
+                nc.vector.quantize_mx(out=w2_cod[:].bitcast(FP8X4), scales=w2_scl[:], in_=w2_gr[:])
+            if has(r):
+                m2(r)
+            if not has(r) and has(x + 1):
+                m1(x + 1)
+            if has(y):
+                xh_tx(y)
+            if has(x):
+                sq4(x)
+            if p == 0:
+                w2_g3 = w2_gr[:].rearrange("p (f j) -> p f j", j=4)
+                for h in range(2):
+                    nc.scalar.copy(
+                        out=w2_g3[:, 256 * h : 256 * h + 256, :],
+                        in_=w2_ps[h][:].rearrange("p j f -> p f j"),
+                    )
+            if has(e):
+                ge4(e)
+            if has(r):
+                hb4(r)
+            if has(r) and has(x + 1):
+                m1(x + 1)
+            if has(x):
+                powg(x)
+            if has(p + 3):
+                hbg(p + 3)

@@ -21,13 +21,7 @@ GW = GT * D
 LN_EPS = 1e-5
 
 FLOPS = 2 * 2 * TOKENS * D * D
-
-HB_ON_V = (0, 1, 2, 3)
-HB_HEAD = 3
-XH_ON_S = (2, 3)
-HH_BUFS = 5
-LAG2 = 2
-XH_BUFS = 3
+WARM_PASSES = 4
 
 
 def tile_supervisedrefiner_pb_t_kernel(
@@ -40,54 +34,42 @@ def tile_supervisedrefiner_pb_t_kernel(
     o1_v = out_1.flatten_outer_dims().rearrange("(p t) d -> p (t d)", t=TILES)
 
     with ExitStack() as ctx:
+        ctx.enter_context(tc.manual_schedule())
         const = ctx.enter_context(tc.tile_pool(name="const", bufs=1))
         loads = ctx.enter_context(tc.tile_pool(name="loads", bufs=GROUPS))
         work = ctx.enter_context(tc.tile_pool(name="work", bufs=2))
         mm = ctx.enter_context(tc.psum_pool(name="mm", bufs=1))
         xt = ctx.enter_context(tc.psum_pool(name="xt", bufs=1))
 
+        wo_raw = const.tile([P, GW], BF16, name="wo_raw")
+        nc.sync.dma_start(
+            out=wo_raw[:].rearrange("p (r k) -> p r k", k=D),
+            in_=Wo.rearrange("(r p) k -> p r k", p=P),
+        )
+        att_sb = []
+        hid_sb = []
+        w2_raw = const.tile([P, GW], BF16, name="w2_raw")
+        for g in range(GROUPS):
+            a_t = loads.tile([P, GW], BF16, name="att_sb", tag="att")
+            nc.sync.dma_start(out=a_t[:], in_=att_v[:, g * GW : (g + 1) * GW])
+            att_sb.append(a_t)
+            if g == 1:
+                nc.sync.dma_start(
+                    out=w2_raw[:].rearrange("p (r k) -> p r k", k=D),
+                    in_=W_ff1.rearrange("(r p) k -> p r k", p=P),
+                )
+            h_t = loads.tile([P, GW], BF16, name="hid_sb", tag="hid")
+            nc.sync.dma_start(out=h_t[:], in_=hid_v[:, g * GW : (g + 1) * GW])
+            hid_sb.append(h_t)
+
         rows = const.tile([P, 2 * D], BF16, name="rows")
         nc.vector.memset(rows[:], 0.0)
+        nc.scalar.dma_start(out=rows[0:1, 0:D], in_=bo.unsqueeze(0))
+        nc.scalar.dma_start(out=rows[0:1, D : 2 * D], in_=b_ff1.unsqueeze(0))
         lnrows = const.tile([P, P], BF16, name="lnrows")
         nc.vector.memset(lnrows[:], 0.0)
-        nc.sync.dma_start(out=rows[0:1, 0:D], in_=bo.unsqueeze(0))
-        nc.sync.dma_start(out=rows[0:1, D : 2 * D], in_=b_ff1.unsqueeze(0))
-        nc.sync.dma_start(out=lnrows[0:4, :], in_=ln2_g.rearrange("(j c) -> j c", c=P))
-        nc.sync.dma_start(out=lnrows[4:8, :], in_=ln2_b.rearrange("(j c) -> j c", c=P))
-
-        wo_raw = const.tile([P, GW], BF16, name="wo_raw")
-        w2_raw = const.tile([P, GW], BF16, name="w2_raw")
-        att_sb = [loads.tile([P, GW], BF16, name="att_sb", tag="att") for g in range(GROUPS)]
-        hid_sb = [loads.tile([P, GW], BF16, name="hid_sb", tag="hid") for g in range(GROUPS)]
-
-        def load_w(dst, src, halves):
-            step = 4 // halves
-            for h in range(halves):
-                nc.sync.dma_start(
-                    out=dst[:, h * step * D : (h + 1) * step * D].rearrange("p (r k) -> p r k", k=D),
-                    in_=src[h * step * P : (h + 1) * step * P, :].rearrange("(r p) k -> p r k", p=P),
-                )
-
-        def load_t(dst, src_v, g, halves):
-            step = GW // halves
-            for h in range(halves):
-                nc.sync.dma_start(
-                    out=dst[g][:, h * step : (h + 1) * step],
-                    in_=src_v[:, g * GW + h * step : g * GW + (h + 1) * step],
-                )
-
-        load_t(hid_sb, hid_v, 0, 1)
-        load_w(wo_raw, Wo, 2)
-        load_t(att_sb, att_v, 0, 2)
-        load_t(hid_sb, hid_v, 1, 1)
-        load_t(hid_sb, hid_v, 2, 1)
-        load_t(att_sb, att_v, 1, 1)
-        load_w(w2_raw, W_ff1, 1)
-        load_t(att_sb, att_v, 2, 1)
-        for g in range(3, GROUPS):
-            load_t(hid_sb, hid_v, g, 1)
-            load_t(att_sb, att_v, g, 1)
-
+        nc.scalar.dma_start(out=lnrows[0:4, :], in_=ln2_g.rearrange("(j c) -> j c", c=P))
+        nc.scalar.dma_start(out=lnrows[4:8, :], in_=ln2_b.rearrange("(j c) -> j c", c=P))
         zero1 = const.tile([P, 1], F32, name="zero1")
         nc.vector.memset(zero1[:], 0.0)
         warm = const.tile([P, 1], F32, name="warm")
@@ -101,6 +83,19 @@ def tile_supervisedrefiner_pb_t_kernel(
         nc.vector.memset(ones16[:], 1.0)
         neghalf = const.tile([P, GT], F32, name="neghalf")
         nc.vector.memset(neghalf[:], -0.5)
+
+        def dummy(pool, tag, n):
+            ps = pool.tile([P, D], F32, name="dum", tag=tag)
+            for rep in range(n):
+                nc.tensor.matmul_mx(
+                    out=ps[:],
+                    lhsT=wo_cod[:, 0:P].bitcast(FP8X4),
+                    lhsT_scale=wo_scl[:, 0:P],
+                    rhs=wo_cod[:].bitcast(FP8X4),
+                    rhs_scale=wo_scl[:],
+                    start=True,
+                    stop=True,
+                )
 
         bo_bc = const.tile([P, D], BF16, name="bo_bc")
         bff_bc = const.tile([P, D], F32, name="bff_bc")
@@ -159,11 +154,10 @@ def tile_supervisedrefiner_pb_t_kernel(
             st[g]["ascl"] = ascl
 
         def hbg(g):
-            hh = work.tile([P, GW], F32, name="hh", tag="hh", bufs=HH_BUFS)
+            hh = work.tile([P, GW], F32, name="hh", tag="hh", bufs=3)
             for i in range(GT):
                 sl = slice(D * i, D * i + D)
-                eng = nc.vector if (g < HB_HEAD or i in HB_ON_V) else nc.gpsimd
-                eng.tensor_tensor(out=hh[:, sl], in0=hid_sb[g][:, sl], in1=bo_bc[:], op=ALU.add)
+                nc.gpsimd.tensor_tensor(out=hh[:, sl], in0=hid_sb[g][:, sl], in1=bo_bc[:], op=ALU.add)
             st[g]["hh"] = hh
 
         def m1(g):
@@ -233,42 +227,28 @@ def tile_supervisedrefiner_pb_t_kernel(
             rstd = work.tile([P, GT], F32, name="rstd", tag="rstd", bufs=3)
             nc.gpsimd.tensor_tensor(out=rstd[:], in0=veps[:], in1=neghalf[:], op=ALU.pow)
             st[g]["rstd"] = rstd
-            if len(XH_ON_S) > 0:
-                nmr = work.tile([P, GT], F32, name="nmr", tag="nmr", bufs=3)
-                nc.gpsimd.tensor_tensor(out=nmr[:], in0=st[g]["negmean"][:], in1=rstd[:], op=ALU.mult)
-                st[g]["nmr"] = nmr
 
         def xh_tx(g):
             hh = st[g]["hh"]
-            xh = work.tile([P, GW], F32, name="xh", tag="xh", bufs=XH_BUFS)
+            xh = work.tile([P, GW], F32, name="xh", tag="xh")
             xtp = [xt.tile([P, D], F32, name="xtp%d" % j, tag="xtp%d" % j) for j in range(4)]
             for i in range(GT):
                 sl = slice(D * i, D * i + D)
-                if i in XH_ON_S:
-                    nc.scalar.activation(
-                        out=xh[:, sl],
-                        in_=hh[:, sl],
-                        func=ACT.Identity,
-                        scale=st[g]["rstd"][:, i : i + 1],
-                        bias=st[g]["nmr"][:, i : i + 1],
-                    )
-                else:
-                    nc.vector.tensor_scalar(
-                        out=xh[:, sl],
-                        in0=hh[:, sl],
-                        scalar1=st[g]["negmean"][:, i : i + 1],
-                        scalar2=st[g]["rstd"][:, i : i + 1],
-                        op0=ALU.add,
-                        op1=ALU.mult,
-                    )
-            for j in range(4):
-                for i in range(GT):
+                nc.vector.tensor_scalar(
+                    out=xh[:, sl],
+                    in0=hh[:, sl],
+                    scalar1=st[g]["negmean"][:, i : i + 1],
+                    scalar2=st[g]["rstd"][:, i : i + 1],
+                    op0=ALU.add,
+                    op1=ALU.mult,
+                )
+                for j in range(4):
                     c0 = D * i + P * j
                     nc.tensor.transpose(xtp[j][:, P * i : P * i + P], xh[:, c0 : c0 + P], ident32[:])
             st[g]["xtp"] = xtp
 
         def gbs(g):
-            n_t = work.tile([P, 4, D], BF16, name="n_t", tag="n_t", bufs=LAG2 + 2)
+            n_t = work.tile([P, 4, D], BF16, name="n_t", tag="n_t")
             for j in range(4):
                 nc.scalar.activation(
                     out=n_t[:, j, :],
@@ -330,31 +310,36 @@ def tile_supervisedrefiner_pb_t_kernel(
         w2_scl = const.tile([P, D], U8, name="w2_scl", align_bytes=64)
         w2_gr = const.tile([P, GW], BF16, name="w2_gr", align_bytes=64)
 
-        hbg(0)
         wo_ps = words_to_psum(wo_raw, (0, 1))
         ta(0, (2, 3))
         wo_gr = words_out(wo_ps, "sv")
         p1(0, "sv")
         nc.vector.quantize_mx(out=wo_cod[:].bitcast(FP8X4), scales=wo_scl[:], in_=wo_gr[:])
         q1(0)
-        m1(0)
+        hbg(0)
         hbg(1)
-        hbg(2)
+        dummy(mm, "mm3", WARM_PASSES)
+        m1(0)
 
         def has(g):
             return 0 <= g < GROUPS
 
-        for p in range(GROUPS + 3 + LAG2):
-            x, w, y, z = p, p + 1, p - 1, p - 2
-            r = z - LAG2
-            e = r - 1
+        for p in range(GROUPS + 3):
+            x, w, y, z, e = p, p + 1, p - 1, p - 2, p - 3
             if has(x):
                 c4(x)
             if has(z):
                 gbs(z)
+            dummy(mm, "mm0", 1)
+            dummy(mm, "mm1", 1)
             if has(w):
                 ta(w, (0, 1))
                 p1(w, "ss")
+            dummy(mm, "mm2", 1)
+            dummy(mm, "mm3", 1)
+            if p > 0:
+                dummy(xt, "xtp0", 1)
+                dummy(xt, "xtp1", 1)
             if p == 0:
                 w2_ps = []
                 for h in range(2):
@@ -366,15 +351,15 @@ def tile_supervisedrefiner_pb_t_kernel(
                                 ps[:, j, P * r2 : P * r2 + P], w2_raw[:, c0 : c0 + P], ident16[:]
                             )
                     w2_ps.append(ps)
-            if has(r):
-                rg_q2(r)
+            if has(z):
+                rg_q2(z)
             if has(w):
                 q1(w)
             if p == 1:
                 nc.vector.quantize_mx(out=w2_cod[:].bitcast(FP8X4), scales=w2_scl[:], in_=w2_gr[:])
-            if has(r):
-                m2(r)
-            if not has(r) and has(x + 1):
+            if has(z):
+                m2(z)
+            if not has(z) and has(x + 1):
                 m1(x + 1)
             if has(y):
                 xh_tx(y)
@@ -389,11 +374,11 @@ def tile_supervisedrefiner_pb_t_kernel(
                     )
             if has(e):
                 ge4(e)
-            if has(r):
-                hb4(r)
-            if has(r) and has(x + 1):
+            if has(z):
+                hb4(z)
+            if has(z) and has(x + 1):
                 m1(x + 1)
             if has(x):
                 powg(x)
-            if has(p + 3):
-                hbg(p + 3)
+            if has(p + 2):
+                hbg(p + 2)

@@ -23,6 +23,11 @@ LN_EPS = 1e-5
 FLOPS = 2 * 2 * TOKENS * D * D
 WARM_PASSES = 4
 
+HB_ON_V = (2, 3)
+XH_ON_S = ()
+HH_BUFS = 4
+XH_BUFS = 3
+
 
 def tile_supervisedrefiner_pb_t_kernel(
     tc, attended, hidden, Wo, bo, ln2_g, ln2_b, W_ff1, b_ff1, out_0, out_1
@@ -34,7 +39,6 @@ def tile_supervisedrefiner_pb_t_kernel(
     o1_v = out_1.flatten_outer_dims().rearrange("(p t) d -> p (t d)", t=TILES)
 
     with ExitStack() as ctx:
-        ctx.enter_context(tc.manual_schedule())
         const = ctx.enter_context(tc.tile_pool(name="const", bufs=1))
         loads = ctx.enter_context(tc.tile_pool(name="loads", bufs=GROUPS))
         work = ctx.enter_context(tc.tile_pool(name="work", bufs=2))
@@ -154,10 +158,11 @@ def tile_supervisedrefiner_pb_t_kernel(
             st[g]["ascl"] = ascl
 
         def hbg(g):
-            hh = work.tile([P, GW], F32, name="hh", tag="hh", bufs=3)
+            hh = work.tile([P, GW], F32, name="hh", tag="hh", bufs=HH_BUFS)
             for i in range(GT):
                 sl = slice(D * i, D * i + D)
-                nc.gpsimd.tensor_tensor(out=hh[:, sl], in0=hid_sb[g][:, sl], in1=bo_bc[:], op=ALU.add)
+                eng = nc.vector if i in HB_ON_V else nc.gpsimd
+                eng.tensor_tensor(out=hh[:, sl], in0=hid_sb[g][:, sl], in1=bo_bc[:], op=ALU.add)
             st[g]["hh"] = hh
 
         def m1(g):
@@ -227,21 +232,34 @@ def tile_supervisedrefiner_pb_t_kernel(
             rstd = work.tile([P, GT], F32, name="rstd", tag="rstd", bufs=3)
             nc.gpsimd.tensor_tensor(out=rstd[:], in0=veps[:], in1=neghalf[:], op=ALU.pow)
             st[g]["rstd"] = rstd
+            if len(XH_ON_S) > 0:
+                nmr = work.tile([P, GT], F32, name="nmr", tag="nmr", bufs=3)
+                nc.gpsimd.tensor_tensor(out=nmr[:], in0=st[g]["negmean"][:], in1=rstd[:], op=ALU.mult)
+                st[g]["nmr"] = nmr
 
         def xh_tx(g):
             hh = st[g]["hh"]
-            xh = work.tile([P, GW], F32, name="xh", tag="xh")
+            xh = work.tile([P, GW], F32, name="xh", tag="xh", bufs=XH_BUFS)
             xtp = [xt.tile([P, D], F32, name="xtp%d" % j, tag="xtp%d" % j) for j in range(4)]
             for i in range(GT):
                 sl = slice(D * i, D * i + D)
-                nc.vector.tensor_scalar(
-                    out=xh[:, sl],
-                    in0=hh[:, sl],
-                    scalar1=st[g]["negmean"][:, i : i + 1],
-                    scalar2=st[g]["rstd"][:, i : i + 1],
-                    op0=ALU.add,
-                    op1=ALU.mult,
-                )
+                if i in XH_ON_S:
+                    nc.scalar.activation(
+                        out=xh[:, sl],
+                        in_=hh[:, sl],
+                        func=ACT.Identity,
+                        scale=st[g]["rstd"][:, i : i + 1],
+                        bias=st[g]["nmr"][:, i : i + 1],
+                    )
+                else:
+                    nc.vector.tensor_scalar(
+                        out=xh[:, sl],
+                        in0=hh[:, sl],
+                        scalar1=st[g]["negmean"][:, i : i + 1],
+                        scalar2=st[g]["rstd"][:, i : i + 1],
+                        op0=ALU.add,
+                        op1=ALU.mult,
+                    )
                 for j in range(4):
                     c0 = D * i + P * j
                     nc.tensor.transpose(xtp[j][:, P * i : P * i + P], xh[:, c0 : c0 + P], ident32[:])

@@ -15,18 +15,13 @@ P = 128
 D = 512
 TOKENS = 4096
 TILES = TOKENS // P
-GT = 4
-GROUPS = TILES // GT
+GT = 2
+PAIRS = TILES // GT
 GW = GT * D
 LN_EPS = 1e-5
+HB_AHEAD = 4
 
 FLOPS = 2 * 2 * TOKENS * D * D
-WARM_PASSES = 4
-
-HB_ON_V = (2, 3)
-XH_ON_S = ()
-HH_BUFS = 4
-XH_BUFS = 3
 
 
 def tile_supervisedrefiner_pb_t_kernel(
@@ -39,58 +34,101 @@ def tile_supervisedrefiner_pb_t_kernel(
     o1_v = out_1.flatten_outer_dims().rearrange("(p t) d -> p (t d)", t=TILES)
 
     with ExitStack() as ctx:
+        ctx.enter_context(tc.manual_schedule())
         const = ctx.enter_context(tc.tile_pool(name="const", bufs=1))
-        loads = ctx.enter_context(tc.tile_pool(name="loads", bufs=GROUPS))
         work = ctx.enter_context(tc.tile_pool(name="work", bufs=2))
-        mm = ctx.enter_context(tc.psum_pool(name="mm", bufs=1))
-        xt = ctx.enter_context(tc.psum_pool(name="xt", bufs=1))
+        psum = ctx.enter_context(tc.psum_pool(name="psum", bufs=1))
 
-        wo_raw = const.tile([P, GW], BF16, name="wo_raw")
-        nc.sync.dma_start(
-            out=wo_raw[:].rearrange("p (r k) -> p r k", k=D),
-            in_=Wo.rearrange("(r p) k -> p r k", p=P),
-        )
-        att_sb = []
-        hid_sb = []
-        w2_raw = const.tile([P, GW], BF16, name="w2_raw")
-        for g in range(GROUPS):
-            a_t = loads.tile([P, GW], BF16, name="att_sb", tag="att")
-            nc.sync.dma_start(out=a_t[:], in_=att_v[:, g * GW : (g + 1) * GW])
-            att_sb.append(a_t)
-            if g == 1:
-                nc.sync.dma_start(
-                    out=w2_raw[:].rearrange("p (r k) -> p r k", k=D),
-                    in_=W_ff1.rearrange("(r p) k -> p r k", p=P),
-                )
-            h_t = loads.tile([P, GW], BF16, name="hid_sb", tag="hid")
-            nc.sync.dma_start(out=h_t[:], in_=hid_v[:, g * GW : (g + 1) * GW])
-            hid_sb.append(h_t)
+        wo_raw = const.tile([P, 4 * D], BF16, name="wo_raw")
+        w2_raw = const.tile([P, 4 * D], BF16, name="w2_raw")
+        att = {}
+        hid = {}
 
-        rows = const.tile([P, 2 * D], BF16, name="rows")
-        nc.vector.memset(rows[:], 0.0)
-        nc.scalar.dma_start(out=rows[0:1, 0:D], in_=bo.unsqueeze(0))
-        nc.scalar.dma_start(out=rows[0:1, D : 2 * D], in_=b_ff1.unsqueeze(0))
+        def load_w(dst, src, r0, r1):
+            nc.sync.dma_start(
+                out=dst[:, D * r0 : D * r1].rearrange("p (r k) -> p r k", k=D),
+                in_=src[P * r0 : P * r1, :].rearrange("(r p) k -> p r k", p=P),
+            )
+
+        def load_x(dst, name, src, g0, n):
+            t = const.tile([P, n * GW], BF16, name="%s%d" % (name, g0))
+            nc.sync.dma_start(out=t[:], in_=src[:, g0 * GW : (g0 + n) * GW])
+            for k in range(n):
+                dst[g0 + k] = t[:, k * GW : (k + 1) * GW]
+
+        load_w(wo_raw, Wo, 0, 2)
+        load_w(wo_raw, Wo, 2, 4)
+        load_x(att, "att", att_v, 0, 1)
+        load_x(hid, "hid", hid_v, 0, 1)
+        load_x(att, "att", att_v, 1, 1)
+        load_x(hid, "hid", hid_v, 1, 1)
+        load_x(att, "att", att_v, 2, 2)
+        load_x(hid, "hid", hid_v, 2, 2)
+        load_w(w2_raw, W_ff1, 0, 4)
+        for g in range(4, PAIRS, 2):
+            load_x(att, "att", att_v, g, 2)
+            load_x(hid, "hid", hid_v, g, 2)
+
+        bo_row = const.tile([P, D], BF16, name="bo_row")
+        nc.vector.memset(bo_row[:], 0.0)
+        nc.scalar.dma_start(out=bo_row[0:1, :], in_=bo.unsqueeze(0))
         lnrows = const.tile([P, P], BF16, name="lnrows")
         nc.vector.memset(lnrows[:], 0.0)
         nc.scalar.dma_start(out=lnrows[0:4, :], in_=ln2_g.rearrange("(j c) -> j c", c=P))
         nc.scalar.dma_start(out=lnrows[4:8, :], in_=ln2_b.rearrange("(j c) -> j c", c=P))
         zero1 = const.tile([P, 1], F32, name="zero1")
         nc.vector.memset(zero1[:], 0.0)
+        bff_row = const.tile([P, D], BF16, name="bff_row")
+        nc.vector.memset(bff_row[:], 0.0)
+        nc.scalar.dma_start(out=bff_row[0:1, :], in_=b_ff1.unsqueeze(0))
         warm = const.tile([P, 1], F32, name="warm")
         nc.scalar.activation(out=warm[:], in_=zero1[:], func=ACT.Gelu)
-
-        ident32 = const.tile([P, P], F32, name="ident32")
-        make_identity(nc, ident32[:])
-        ident16 = const.tile([P, P], BF16, name="ident16")
-        make_identity(nc, ident16[:])
         ones16 = const.tile([P, P], BF16, name="ones16")
         nc.vector.memset(ones16[:], 1.0)
         neghalf = const.tile([P, GT], F32, name="neghalf")
         nc.vector.memset(neghalf[:], -0.5)
+        ident32 = const.tile([P, P], F32, name="ident32")
+        make_identity(nc, ident32[:])
+        ident16 = const.tile([P, P], BF16, name="ident16")
+        make_identity(nc, ident16[:])
 
-        def dummy(pool, tag, n):
-            ps = pool.tile([P, D], F32, name="dum", tag=tag)
+        bo_bc = const.tile([P, D], BF16, name="bo_bc")
+        bff_bc = const.tile([P, D], F32, name="bff_bc")
+        gb8 = const.tile([P, 8], F32, name="gb8")
+        wo_cod = const.tile([P, D], U32, name="wo_cod", align_bytes=64)
+        wo_scl = const.tile([P, D], U8, name="wo_scl", align_bytes=64)
+        w2_cod = const.tile([P, D], U32, name="w2_cod", align_bytes=64)
+        w2_scl = const.tile([P, D], U8, name="w2_scl", align_bytes=64)
+        wo_gr = const.tile([P, 4 * D], BF16, name="wo_gr", align_bytes=64)
+        w2_gr = const.tile([P, 4 * D], BF16, name="w2_gr", align_bytes=64)
+
+        st = {}
+        for g in range(PAIRS):
+            st[g] = {}
+
+        def has(g):
+            return 0 <= g < PAIRS
+
+        def words_t(src, tag):
+            src32 = src.bitcast(F32)
+            ps = psum.tile([P, 2, 2 * P], F32, name="words_ps", tag=tag)
+            for i in range(2):
+                for u in range(2):
+                    c0 = 256 * i + P * u
+                    nc.tensor.transpose(ps[:, u, P * i : P * i + P], src32[:, c0 : c0 + P], ident32[:])
+            return ps
+
+        def words_copy(eng, dst, ps):
+            out = dst.bitcast(F32).rearrange("p (r u) -> p r u", u=2)
+            src = ps[:].rearrange("p u r -> p r u")
+            if eng == "s":
+                nc.scalar.copy(out=out, in_=src)
+            else:
+                nc.vector.tensor_copy(out=out, in_=src)
+
+        def dummy(n):
             for rep in range(n):
+                ps = psum.tile([P, D], F32, name="dum", tag="D1")
                 nc.tensor.matmul_mx(
                     out=ps[:],
                     lhsT=wo_cod[:, 0:P].bitcast(FP8X4),
@@ -101,302 +139,236 @@ def tile_supervisedrefiner_pb_t_kernel(
                     stop=True,
                 )
 
-        bo_bc = const.tile([P, D], BF16, name="bo_bc")
-        bff_bc = const.tile([P, D], F32, name="bff_bc")
-        gb8 = const.tile([P, 8], F32, name="gb8")
-        bo_ps = mm.tile([P, D], F32, name="bo_ps", tag="mm0")
-        nc.tensor.matmul(out=bo_ps[:], lhsT=ones16[:], rhs=rows[:, 0:D], start=True, stop=True)
-        nc.vector.tensor_copy(out=bo_bc[:], in_=bo_ps[:])
-        bff_ps = mm.tile([P, D], F32, name="bff_ps", tag="mm1")
-        nc.tensor.matmul(out=bff_ps[:], lhsT=ones16[:], rhs=rows[:, D : 2 * D], start=True, stop=True)
-        ln_ps = mm.tile([P, P], BF16, name="ln_ps", tag="mm2")
-        nc.tensor.transpose(ln_ps[:], lnrows[:], ident16[:])
-        nc.vector.tensor_copy(out=bff_bc[:], in_=bff_ps[:])
-        nc.vector.tensor_copy(out=gb8[:], in_=ln_ps[:, 0:8])
+        def at(g):
+            st[g]["at"] = words_t(att[g], "D0")
 
-        st = {}
-        for g in range(GROUPS):
-            st[g] = {}
-
-        def words_to_psum(src, banks):
-            src32 = src[:].bitcast(F32)
-            out = []
-            for h in range(2):
-                ps = xt.tile([P, 2, 2 * P], F32, name="at_ps", tag="xtp%d" % banks[h])
-                for i2 in range(2):
-                    for u in range(2):
-                        c0 = 256 * (2 * h + i2) + P * u
-                        nc.tensor.transpose(
-                            ps[:, u, P * i2 : P * i2 + P], src32[:, c0 : c0 + P], ident32[:]
-                        )
-                out.append(ps)
-            return out
-
-        def words_out(banks_ps, engines):
-            grouped = work.tile([P, GW], BF16, name="agr", tag="agr", align_bytes=64)
-            g32 = grouped[:].bitcast(F32).rearrange("p (r u) -> p r u", u=2)
-            for h in range(2):
-                src_ap = banks_ps[h][:].rearrange("p u r -> p r u")
-                dst_ap = g32[:, 256 * h : 256 * h + 256, :]
-                if engines[h] == "s":
-                    nc.scalar.copy(out=dst_ap, in_=src_ap)
-                else:
-                    nc.vector.tensor_copy(out=dst_ap, in_=src_ap)
-            return grouped
-
-        def ta(g, banks):
-            st[g]["at_ps"] = words_to_psum(att_sb[g], banks)
-
-        def p1(g, engines):
-            st[g]["agr"] = words_out(st[g]["at_ps"], engines)
+        def p1(g):
+            agr = work.tile([P, GW], BF16, name="agr", tag="agr", align_bytes=64)
+            words_copy("s", agr[:], st[g]["at"])
+            st[g]["agr"] = agr
 
         def q1(g):
-            acod = work.tile([P, D], U32, name="acod", tag="acod", bufs=3, align_bytes=64)
-            ascl = work.tile([P, D], U8, name="ascl", tag="ascl", bufs=3, align_bytes=64)
+            acod = work.tile([P, GW // 4], U32, name="acod", tag="acod", bufs=3, align_bytes=64)
+            ascl = work.tile([P, GW // 4], U8, name="ascl", tag="ascl", bufs=3, align_bytes=64)
             nc.vector.quantize_mx(out=acod[:].bitcast(FP8X4), scales=ascl[:], in_=st[g]["agr"][:])
             st[g]["acod"] = acod
             st[g]["ascl"] = ascl
 
-        def hbg(g):
-            hh = work.tile([P, GW], F32, name="hh", tag="hh", bufs=HH_BUFS)
+        def hb(g):
+            st[g]["hb"] = []
             for i in range(GT):
-                sl = slice(D * i, D * i + D)
-                eng = nc.vector if i in HB_ON_V else nc.gpsimd
-                eng.tensor_tensor(out=hh[:, sl], in0=hid_sb[g][:, sl], in1=bo_bc[:], op=ALU.add)
-            st[g]["hh"] = hh
+                eng = nc.vector if g < 2 or i == 1 else nc.gpsimd
+                t = work.tile([P, D], F32, name="hb", tag="hb", bufs=GT * HB_AHEAD)
+                eng.tensor_tensor(out=t[:], in0=hid[g][:, D * i : D * i + D], in1=bo_bc[:], op=ALU.add)
+                st[g]["hb"].append(t)
 
-        def m1(g):
-            st[g]["s1"] = []
+        def mx2(g, cod, scl, w_cod, w_scl, tag):
+            out = []
             for i in range(GT):
                 cs = slice(P * i, P * i + P)
-                s1 = mm.tile([P, D], F32, name="s1", tag="mm%d" % i)
+                ps = psum.tile([P, D], F32, name="mx_ps", tag="%s%d" % (tag, i))
                 nc.tensor.matmul_mx(
-                    out=s1[:],
-                    lhsT=st[g]["acod"][:, cs].bitcast(FP8X4),
-                    lhsT_scale=st[g]["ascl"][:, cs],
-                    rhs=wo_cod[:].bitcast(FP8X4),
-                    rhs_scale=wo_scl[:],
+                    out=ps[:],
+                    lhsT=st[g][cod][:, cs].bitcast(FP8X4),
+                    lhsT_scale=st[g][scl][:, cs],
+                    rhs=w_cod[:].bitcast(FP8X4),
+                    rhs_scale=w_scl[:],
                     start=True,
                     stop=True,
                 )
-                st[g]["s1"].append(s1)
+                out.append(ps)
+            return out
+
+        def m1(g):
+            st[g]["s1"] = mx2(g, "acod", "ascl", wo_cod, wo_scl, "A")
+
+        def m2(g):
+            st[g]["s2"] = mx2(g, "ncod", "nscl", w2_cod, w2_scl, "B")
 
         def c4(g):
-            hh = st[g]["hh"]
-            hsum = work.tile([P, GT], F32, name="hsum", tag="hsum", bufs=3)
+            h = work.tile([P, GW], F32, name="h", tag="h", bufs=4)
+            hsum = work.tile([P, GT], F32, name="hsum", tag="hsum", bufs=4)
             for i in range(GT):
-                sl = slice(D * i, D * i + D)
                 nc.vector.scalar_tensor_tensor(
-                    out=hh[:, sl],
+                    out=h[:, D * i : D * i + D],
                     in0=st[g]["s1"][i][:],
                     scalar=1.0,
-                    in1=hh[:, sl],
+                    in1=st[g]["hb"][i][:],
                     op0=ALU.mult,
                     op1=ALU.add,
                     accum_out=hsum[:, i : i + 1],
                 )
+            st[g]["h"] = h
             st[g]["hsum"] = hsum
-            nc.sync.dma_start(out=o0_v[:, g * GW : (g + 1) * GW], in_=hh[:])
+            nc.sync.dma_start(out=o0_v[:, g * GW : (g + 1) * GW], in_=h[:])
 
-        def sq4(g):
-            hh = st[g]["hh"]
-            negmean = work.tile([P, GT], F32, name="negmean", tag="negmean", bufs=3)
-            ssq = work.tile([P, GT], F32, name="ssq", tag="ssq", bufs=3)
+        def sq(g):
+            ssq = work.tile([P, GT], F32, name="ssq", tag="ssq", bufs=4)
             for i in range(GT):
-                sl = slice(D * i, D * i + D)
-                nc.scalar.mul(
-                    out=negmean[:, i : i + 1], in_=st[g]["hsum"][:, i : i + 1], mul=-1.0 / D
-                )
                 junk = work.tile([P, D], BF16, name="junk", tag="junk")
                 nc.scalar.activation(
                     out=junk[:],
-                    in_=hh[:, sl],
+                    in_=st[g]["h"][:, D * i : D * i + D],
                     func=ACT.Square,
-                    bias=negmean[:, i : i + 1],
-                    scale=1.0,
+                    bias=st[g]["hsum"][:, i : i + 1],
+                    scale=-float(D),
                     accum_out=ssq[:, i : i + 1],
                 )
-            st[g]["negmean"] = negmean
             st[g]["ssq"] = ssq
 
-        def powg(g):
-            veps = work.tile([P, GT], F32, name="veps", tag="veps", bufs=3)
+        def stats(g):
+            negmean = work.tile([P, GT], F32, name="negmean", tag="negmean", bufs=4)
             nc.gpsimd.tensor_scalar(
-                out=veps[:],
-                in0=st[g]["ssq"][:],
-                scalar1=1.0 / D,
-                scalar2=LN_EPS,
-                op0=ALU.mult,
-                op1=ALU.add,
+                out=negmean[:], in0=st[g]["hsum"][:], scalar1=-1.0 / D, scalar2=0.0, op0=ALU.mult, op1=ALU.add
             )
-            rstd = work.tile([P, GT], F32, name="rstd", tag="rstd", bufs=3)
+            veps = work.tile([P, GT], F32, name="veps", tag="veps", bufs=4)
+            nc.gpsimd.tensor_scalar(
+                out=veps[:], in0=st[g]["ssq"][:], scalar1=1.0 / D**3, scalar2=LN_EPS, op0=ALU.mult, op1=ALU.add
+            )
+            rstd = work.tile([P, GT], F32, name="rstd", tag="rstd", bufs=4)
             nc.gpsimd.tensor_tensor(out=rstd[:], in0=veps[:], in1=neghalf[:], op=ALU.pow)
+            st[g]["negmean"] = negmean
             st[g]["rstd"] = rstd
-            if len(XH_ON_S) > 0:
-                nmr = work.tile([P, GT], F32, name="nmr", tag="nmr", bufs=3)
-                nc.gpsimd.tensor_tensor(out=nmr[:], in0=st[g]["negmean"][:], in1=rstd[:], op=ALU.mult)
-                st[g]["nmr"] = nmr
 
-        def xh_tx(g):
-            hh = st[g]["hh"]
-            xh = work.tile([P, GW], F32, name="xh", tag="xh", bufs=XH_BUFS)
-            xtp = [xt.tile([P, D], F32, name="xtp%d" % j, tag="xtp%d" % j) for j in range(4)]
+        def xh(g):
+            x = work.tile([P, GW], F32, name="xh", tag="xh")
             for i in range(GT):
-                sl = slice(D * i, D * i + D)
-                if i in XH_ON_S:
-                    nc.scalar.activation(
-                        out=xh[:, sl],
-                        in_=hh[:, sl],
-                        func=ACT.Identity,
-                        scale=st[g]["rstd"][:, i : i + 1],
-                        bias=st[g]["nmr"][:, i : i + 1],
-                    )
-                else:
-                    nc.vector.tensor_scalar(
-                        out=xh[:, sl],
-                        in0=hh[:, sl],
-                        scalar1=st[g]["negmean"][:, i : i + 1],
-                        scalar2=st[g]["rstd"][:, i : i + 1],
-                        op0=ALU.add,
-                        op1=ALU.mult,
-                    )
-                for j in range(4):
-                    c0 = D * i + P * j
-                    nc.tensor.transpose(xtp[j][:, P * i : P * i + P], xh[:, c0 : c0 + P], ident32[:])
-            st[g]["xtp"] = xtp
+                nc.vector.tensor_scalar(
+                    out=x[:, D * i : D * i + D],
+                    in0=st[g]["h"][:, D * i : D * i + D],
+                    scalar1=st[g]["negmean"][:, i : i + 1],
+                    scalar2=st[g]["rstd"][:, i : i + 1],
+                    op0=ALU.add,
+                    op1=ALU.mult,
+                )
+            st[g]["xh"] = x
+
+        def xt(g):
+            st[g]["xt"] = []
+            for b in range(2):
+                ps = psum.tile([P, 2, GT * P], F32, name="xt_ps", tag="C%d" % b)
+                for j2 in range(2):
+                    for i in range(GT):
+                        c0 = D * i + P * (2 * b + j2)
+                        nc.tensor.transpose(ps[:, j2, P * i : P * i + P], st[g]["xh"][:, c0 : c0 + P], ident32[:])
+                st[g]["xt"].append(ps)
 
         def gbs(g):
-            n_t = work.tile([P, 4, D], BF16, name="n_t", tag="n_t")
+            n_t = work.tile([P, 4, GT * P], BF16, name="n_t", tag="n_t", bufs=3)
             for j in range(4):
                 nc.scalar.activation(
                     out=n_t[:, j, :],
-                    in_=st[g]["xtp"][j][:],
+                    in_=st[g]["xt"][j // 2][:, j % 2, :],
                     func=ACT.Identity,
                     scale=gb8[:, j : j + 1],
                     bias=gb8[:, 4 + j : 5 + j],
                 )
             st[g]["n_t"] = n_t
 
-        def rg_q2(g):
+        def rg(g):
             ngr = work.tile([P, GW], BF16, name="ngr", tag="ngr", align_bytes=64)
             nc.vector.tensor_copy(
                 out=ngr[:].rearrange("p (c i t) -> p c t i", i=4, t=4),
                 in_=st[g]["n_t"][:].rearrange("p t (c i) -> p c t i", i=4),
             )
-            ncod = work.tile([P, D], U32, name="ncod", tag="ncod", align_bytes=64)
-            nscl = work.tile([P, D], U8, name="nscl", tag="nscl", align_bytes=64)
-            nc.vector.quantize_mx(out=ncod[:].bitcast(FP8X4), scales=nscl[:], in_=ngr[:])
+            st[g]["ngr"] = ngr
+
+        def q2(g):
+            ncod = work.tile([P, GW // 4], U32, name="ncod", tag="ncod", align_bytes=64)
+            nscl = work.tile([P, GW // 4], U8, name="nscl", tag="nscl", align_bytes=64)
+            nc.vector.quantize_mx(out=ncod[:].bitcast(FP8X4), scales=nscl[:], in_=st[g]["ngr"][:])
             st[g]["ncod"] = ncod
             st[g]["nscl"] = nscl
 
-        def m2(g):
-            st[g]["s2"] = []
-            for i in range(GT):
-                cs = slice(P * i, P * i + P)
-                s2 = mm.tile([P, D], F32, name="s2", tag="mm%d" % i)
-                nc.tensor.matmul_mx(
-                    out=s2[:],
-                    lhsT=st[g]["ncod"][:, cs].bitcast(FP8X4),
-                    lhsT_scale=st[g]["nscl"][:, cs],
-                    rhs=w2_cod[:].bitcast(FP8X4),
-                    rhs_scale=w2_scl[:],
-                    start=True,
-                    stop=True,
-                )
-                st[g]["s2"].append(s2)
-
         def hb4(g):
-            aa = work.tile([P, GW], F32, name="aa", tag="aa", bufs=3)
+            aa = work.tile([P, GW], F32, name="aa", tag="aa", bufs=4)
             for i in range(GT):
-                sl = slice(D * i, D * i + D)
-                nc.vector.tensor_tensor(out=aa[:, sl], in0=st[g]["s2"][i][:], in1=bff_bc[:], op=ALU.add)
+                nc.vector.tensor_tensor(
+                    out=aa[:, D * i : D * i + D], in0=st[g]["s2"][i][:], in1=bff_bc[:], op=ALU.add
+                )
             st[g]["aa"] = aa
 
-        def ge4(g):
+        def ge(g):
             aa = st[g]["aa"]
             for i in range(GT):
                 sl = slice(D * i, D * i + D)
                 nc.scalar.activation(out=aa[:, sl], in_=aa[:, sl], func=ACT.Gelu)
-                if g == GROUPS - 1:
+                if g == PAIRS - 1:
                     nc.sync.dma_start(out=o1_v[:, g * GW + D * i : g * GW + D * i + D], in_=aa[:, sl])
-            if g < GROUPS - 1:
+            if g < PAIRS - 1:
                 nc.sync.dma_start(out=o1_v[:, g * GW : (g + 1) * GW], in_=aa[:])
 
-        wo_cod = const.tile([P, D], U32, name="wo_cod", align_bytes=64)
-        wo_scl = const.tile([P, D], U8, name="wo_scl", align_bytes=64)
-        w2_cod = const.tile([P, D], U32, name="w2_cod", align_bytes=64)
-        w2_scl = const.tile([P, D], U8, name="w2_scl", align_bytes=64)
-        w2_gr = const.tile([P, GW], BF16, name="w2_gr", align_bytes=64)
-
-        wo_ps = words_to_psum(wo_raw, (0, 1))
-        ta(0, (2, 3))
-        wo_gr = words_out(wo_ps, "sv")
-        p1(0, "sv")
+        wo_ps = [words_t(wo_raw[:, 0:GW], "A0"), words_t(wo_raw[:, GW : 2 * GW], "A1")]
+        words_copy("s", wo_gr[:, 0:GW], wo_ps[0])
+        words_copy("v", wo_gr[:, GW : 2 * GW], wo_ps[1])
+        at(0)
+        bo_ps = psum.tile([P, D], F32, name="bo_ps", tag="B0")
+        nc.tensor.matmul(out=bo_ps[:], lhsT=ones16[:], rhs=bo_row[:], start=True, stop=True)
+        p1(0)
+        nc.vector.tensor_copy(out=bo_bc[:], in_=bo_ps[:])
         nc.vector.quantize_mx(out=wo_cod[:].bitcast(FP8X4), scales=wo_scl[:], in_=wo_gr[:])
+        at(1)
         q1(0)
-        hbg(0)
-        hbg(1)
-        dummy(mm, "mm3", WARM_PASSES)
+        p1(1)
+        hb(0)
+        bff_ps = psum.tile([P, D], F32, name="bff_ps", tag="B1")
+        nc.tensor.matmul(out=bff_ps[:], lhsT=ones16[:], rhs=bff_row[:], start=True, stop=True)
+        ln_ps = psum.tile([P, P], BF16, name="ln_ps", tag="C0")
+        nc.tensor.transpose(ln_ps[:], lnrows[:], ident16[:])
+        dummy(4)
         m1(0)
+        nc.scalar.copy(out=bff_bc[:], in_=bff_ps[:])
+        nc.scalar.copy(out=gb8[:], in_=ln_ps[:, 0:8])
+        at(2)
+        for g in range(1, HB_AHEAD):
+            hb(g)
+        q1(1)
 
-        def has(g):
-            return 0 <= g < GROUPS
-
-        for p in range(GROUPS + 3):
-            x, w, y, z, e = p, p + 1, p - 1, p - 2, p - 3
-            if has(x):
-                c4(x)
-            if has(z):
-                gbs(z)
-            dummy(mm, "mm0", 1)
-            dummy(mm, "mm1", 1)
-            if has(w):
-                ta(w, (0, 1))
-                p1(w, "ss")
-            dummy(mm, "mm2", 1)
-            dummy(mm, "mm3", 1)
-            if p > 0:
-                dummy(xt, "xtp0", 1)
-                dummy(xt, "xtp1", 1)
-            if p == 0:
-                w2_ps = []
-                for h in range(2):
-                    ps = xt.tile([P, 4, 2 * P], BF16, name="w2_ps", tag="xtp%d" % (2 + h))
-                    for r2 in range(2):
-                        for j in range(4):
-                            c0 = D * (2 * h + r2) + P * j
-                            nc.tensor.transpose(
-                                ps[:, j, P * r2 : P * r2 + P], w2_raw[:, c0 : c0 + P], ident16[:]
-                            )
-                    w2_ps.append(ps)
-            if has(z):
-                rg_q2(z)
-            if has(w):
-                q1(w)
-            if p == 1:
-                nc.vector.quantize_mx(out=w2_cod[:].bitcast(FP8X4), scales=w2_scl[:], in_=w2_gr[:])
-            if has(z):
-                m2(z)
-            if not has(z) and has(x + 1):
-                m1(x + 1)
-            if has(y):
-                xh_tx(y)
-            if has(x):
-                sq4(x)
-            if p == 0:
+        for p in range(PAIRS + 4):
+            if has(p - 3):
+                m2(p - 3)
+            if has(p - 2):
+                gbs(p - 2)
+            if has(p):
+                c4(p)
+            if has(p + HB_AHEAD):
+                hb(p + HB_AHEAD)
+            if has(p + 1):
+                m1(p + 1)
+            dummy(2)
+            if p == 0 or p == 1:
+                w2_ps = psum.tile([P, 4, 2 * P], BF16, name="w2_ps", tag="B%d" % p)
+                for r2 in range(2):
+                    for j in range(4):
+                        c0 = D * (2 * p + r2) + P * j
+                        nc.tensor.transpose(w2_ps[:, j, P * r2 : P * r2 + P], w2_raw[:, c0 : c0 + P], ident16[:])
+            if has(p - 3):
+                hb4(p - 3)
+            if has(p):
+                sq(p)
+                stats(p)
+            if p == 0 or p == 1:
                 w2_g3 = w2_gr[:].rearrange("p (f j) -> p f j", j=4)
-                for h in range(2):
-                    nc.scalar.copy(
-                        out=w2_g3[:, 256 * h : 256 * h + 256, :],
-                        in_=w2_ps[h][:].rearrange("p j f -> p f j"),
-                    )
-            if has(e):
-                ge4(e)
-            if has(z):
-                hb4(z)
-            if has(z) and has(x + 1):
-                m1(x + 1)
-            if has(x):
-                powg(x)
+                nc.scalar.copy(
+                    out=w2_g3[:, 256 * p : 256 * p + 256, :], in_=w2_ps[:].rearrange("p j f -> p f j")
+                )
+            if has(p - 1):
+                xh(p - 1)
             if has(p + 2):
-                hbg(p + 2)
+                p1(p + 2)
+            if has(p - 1):
+                xt(p - 1)
+            dummy(1)
+            if has(p + 3):
+                at(p + 3)
+                dummy(1)
+            if has(p - 2):
+                rg(p - 2)
+            if p == 2:
+                nc.vector.quantize_mx(out=w2_cod[:].bitcast(FP8X4), scales=w2_scl[:], in_=w2_gr[:])
+            if has(p + 2):
+                q1(p + 2)
+            if has(p - 2):
+                q2(p - 2)
+            if has(p - 3):
+                ge(p - 3)

@@ -19,7 +19,8 @@ GT = 2
 PAIRS = TILES // GT
 GW = GT * D
 LN_EPS = 1e-5
-HB_AHEAD = 4
+H_BUFS = 5
+HB_AHEAD = 3
 
 FLOPS = 2 * 2 * TOKENS * D * D
 
@@ -155,12 +156,12 @@ def tile_supervisedrefiner_pb_t_kernel(
             st[g]["ascl"] = ascl
 
         def hb(g):
-            st[g]["hb"] = []
+            h = work.tile([P, GW], F32, name="h", tag="h", bufs=H_BUFS)
             for i in range(GT):
-                eng = nc.vector if g < 2 or i == 1 else nc.gpsimd
-                t = work.tile([P, D], F32, name="hb", tag="hb", bufs=GT * HB_AHEAD)
-                eng.tensor_tensor(out=t[:], in0=hid[g][:, D * i : D * i + D], in1=bo_bc[:], op=ALU.add)
-                st[g]["hb"].append(t)
+                sl = slice(D * i, D * i + D)
+                eng = nc.vector if g < 2 or i else nc.gpsimd
+                eng.tensor_tensor(out=h[:, sl], in0=hid[g][:, sl], in1=bo_bc[:], op=ALU.add)
+            st[g]["h"] = h
 
         def mx2(g, cod, scl, w_cod, w_scl, tag):
             out = []
@@ -186,24 +187,23 @@ def tile_supervisedrefiner_pb_t_kernel(
             st[g]["s2"] = mx2(g, "ncod", "nscl", w2_cod, w2_scl, "B")
 
         def c4(g):
-            h = work.tile([P, GW], F32, name="h", tag="h", bufs=4)
-            hsum = work.tile([P, GT], F32, name="hsum", tag="hsum", bufs=4)
+            h = st[g]["h"]
+            hsum = work.tile([P, GT], F32, name="hsum", tag="hsum", bufs=10)
             for i in range(GT):
                 nc.vector.scalar_tensor_tensor(
                     out=h[:, D * i : D * i + D],
                     in0=st[g]["s1"][i][:],
                     scalar=1.0,
-                    in1=st[g]["hb"][i][:],
+                    in1=h[:, D * i : D * i + D],
                     op0=ALU.mult,
                     op1=ALU.add,
                     accum_out=hsum[:, i : i + 1],
                 )
-            st[g]["h"] = h
             st[g]["hsum"] = hsum
             nc.sync.dma_start(out=o0_v[:, g * GW : (g + 1) * GW], in_=h[:])
 
         def sq(g):
-            ssq = work.tile([P, GT], F32, name="ssq", tag="ssq", bufs=4)
+            ssq = work.tile([P, GT], F32, name="ssq", tag="ssq", bufs=10)
             for i in range(GT):
                 junk = work.tile([P, D], BF16, name="junk", tag="junk")
                 nc.scalar.activation(
@@ -217,21 +217,21 @@ def tile_supervisedrefiner_pb_t_kernel(
             st[g]["ssq"] = ssq
 
         def stats(g):
-            negmean = work.tile([P, GT], F32, name="negmean", tag="negmean", bufs=4)
+            negmean = work.tile([P, GT], F32, name="negmean", tag="negmean", bufs=10)
             nc.gpsimd.tensor_scalar(
                 out=negmean[:], in0=st[g]["hsum"][:], scalar1=-1.0 / D, scalar2=0.0, op0=ALU.mult, op1=ALU.add
             )
-            veps = work.tile([P, GT], F32, name="veps", tag="veps", bufs=4)
+            veps = work.tile([P, GT], F32, name="veps", tag="veps", bufs=10)
             nc.gpsimd.tensor_scalar(
                 out=veps[:], in0=st[g]["ssq"][:], scalar1=1.0 / D**3, scalar2=LN_EPS, op0=ALU.mult, op1=ALU.add
             )
-            rstd = work.tile([P, GT], F32, name="rstd", tag="rstd", bufs=4)
+            rstd = work.tile([P, GT], F32, name="rstd", tag="rstd", bufs=10)
             nc.gpsimd.tensor_tensor(out=rstd[:], in0=veps[:], in1=neghalf[:], op=ALU.pow)
             st[g]["negmean"] = negmean
             st[g]["rstd"] = rstd
 
         def xh(g):
-            x = work.tile([P, GW], F32, name="xh", tag="xh")
+            x = work.tile([P, GW], F32, name="xh", tag="xh", bufs=3)
             for i in range(GT):
                 nc.vector.tensor_scalar(
                     out=x[:, D * i : D * i + D],
@@ -307,9 +307,7 @@ def tile_supervisedrefiner_pb_t_kernel(
         p1(0)
         nc.vector.tensor_copy(out=bo_bc[:], in_=bo_ps[:])
         nc.vector.quantize_mx(out=wo_cod[:].bitcast(FP8X4), scales=wo_scl[:], in_=wo_gr[:])
-        at(1)
         q1(0)
-        p1(1)
         hb(0)
         bff_ps = psum.tile([P, D], F32, name="bff_ps", tag="B1")
         nc.tensor.matmul(out=bff_ps[:], lhsT=ones16[:], rhs=bff_row[:], start=True, stop=True)
@@ -319,56 +317,59 @@ def tile_supervisedrefiner_pb_t_kernel(
         m1(0)
         nc.scalar.copy(out=bff_bc[:], in_=bff_ps[:])
         nc.scalar.copy(out=gb8[:], in_=ln_ps[:, 0:8])
-        at(2)
         for g in range(1, HB_AHEAD):
             hb(g)
+        at(1)
+        p1(1)
         q1(1)
+        at(2)
+        p1(2)
 
-        for p in range(PAIRS + 4):
+        for p in range(PAIRS + 6):
+            if has(p - 5):
+                m2(p - 5)
+            dummy(1)
             if has(p - 3):
-                m2(p - 3)
-            if has(p - 2):
-                gbs(p - 2)
+                xh(p - 3)
+            if has(p - 6):
+                ge(p - 6)
             if has(p):
                 c4(p)
-            if has(p + HB_AHEAD):
-                hb(p + HB_AHEAD)
+            if 3 <= p + 2 < PAIRS:
+                hb(p + 2)
+            if has(p - 3):
+                xt(p - 3)
             if has(p + 1):
                 m1(p + 1)
-            dummy(2)
+            dummy(1)
+            if has(p + 3):
+                at(p + 3)
             if p == 0 or p == 1:
                 w2_ps = psum.tile([P, 4, 2 * P], BF16, name="w2_ps", tag="B%d" % p)
                 for r2 in range(2):
                     for j in range(4):
                         c0 = D * (2 * p + r2) + P * j
                         nc.tensor.transpose(w2_ps[:, j, P * r2 : P * r2 + P], w2_raw[:, c0 : c0 + P], ident16[:])
+            if has(p - 5):
+                hb4(p - 5)
             if has(p - 3):
-                hb4(p - 3)
+                gbs(p - 3)
             if has(p):
                 sq(p)
+            if has(p):
                 stats(p)
             if p == 0 or p == 1:
                 w2_g3 = w2_gr[:].rearrange("p (f j) -> p f j", j=4)
                 nc.scalar.copy(
                     out=w2_g3[:, 256 * p : 256 * p + 256, :], in_=w2_ps[:].rearrange("p j f -> p f j")
                 )
-            if has(p - 1):
-                xh(p - 1)
-            if has(p + 2):
-                p1(p + 2)
-            if has(p - 1):
-                xt(p - 1)
-            dummy(1)
             if has(p + 3):
-                at(p + 3)
-                dummy(1)
-            if has(p - 2):
-                rg(p - 2)
-            if p == 2:
+                p1(p + 3)
+            if has(p - 4):
+                rg(p - 4)
+            if p == 1:
                 nc.vector.quantize_mx(out=w2_cod[:].bitcast(FP8X4), scales=w2_scl[:], in_=w2_gr[:])
             if has(p + 2):
                 q1(p + 2)
-            if has(p - 2):
-                q2(p - 2)
-            if has(p - 3):
-                ge(p - 3)
+            if has(p - 4):
+                q2(p - 4)

@@ -20,6 +20,7 @@ PAIRS = TILES // GT
 GW = GT * D
 LN_EPS = 1e-5
 H_BUFS = 5
+ON_PE = tuple(range(3, 14))
 HB_AHEAD = 3
 
 FLOPS = 2 * 2 * TOKENS * D * D
@@ -157,11 +158,24 @@ def tile_supervisedrefiner_pb_t_kernel(
 
         def hb(g):
             h = work.tile([P, GW], F32, name="h", tag="h", bufs=H_BUFS)
+            st[g]["h"] = h
             for i in range(GT):
+                if i == 1 and g in ON_PE:
+                    continue
                 sl = slice(D * i, D * i + D)
                 eng = nc.vector if g < 2 or i else nc.gpsimd
                 eng.tensor_tensor(out=h[:, sl], in0=hid[g][:, sl], in1=bo_bc[:], op=ALU.add)
-            st[g]["h"] = h
+
+        def hm(g):
+            if g in ON_PE:
+                ps = psum.tile([P, D], F32, name="hb_ps", tag="D1")
+                nc.tensor.matmul(out=ps[:], lhsT=ident16[:], rhs=hid[g][:, D : 2 * D], start=True, stop=False)
+                nc.tensor.matmul(out=ps[:], lhsT=ones16[:], rhs=bo_row[:], start=False, stop=True)
+                st[g]["hb_ps"] = ps
+
+        def hs(g):
+            if g in ON_PE:
+                nc.scalar.copy(out=st[g]["h"][:, D : 2 * D], in_=st[g]["hb_ps"][:])
 
         def mx2(g, cod, scl, w_cod, w_scl, tag):
             out = []
@@ -328,7 +342,6 @@ def tile_supervisedrefiner_pb_t_kernel(
         for p in range(PAIRS + 6):
             if has(p - 5):
                 m2(p - 5)
-            dummy(1)
             if has(p - 3):
                 xh(p - 3)
             if has(p - 6):
@@ -341,7 +354,8 @@ def tile_supervisedrefiner_pb_t_kernel(
                 xt(p - 3)
             if has(p + 1):
                 m1(p + 1)
-            dummy(1)
+            if has(p + 2):
+                hm(p + 2)
             if has(p + 3):
                 at(p + 3)
             if p == 0 or p == 1:
@@ -350,8 +364,6 @@ def tile_supervisedrefiner_pb_t_kernel(
                     for j in range(4):
                         c0 = D * (2 * p + r2) + P * j
                         nc.tensor.transpose(w2_ps[:, j, P * r2 : P * r2 + P], w2_raw[:, c0 : c0 + P], ident16[:])
-            if has(p - 5):
-                hb4(p - 5)
             if has(p - 3):
                 gbs(p - 3)
             if has(p):
@@ -365,8 +377,12 @@ def tile_supervisedrefiner_pb_t_kernel(
                 )
             if has(p + 3):
                 p1(p + 3)
+            if has(p + 2):
+                hs(p + 2)
             if has(p - 4):
                 rg(p - 4)
+            if has(p - 5):
+                hb4(p - 5)
             if p == 1:
                 nc.vector.quantize_mx(out=w2_cod[:].bitcast(FP8X4), scales=w2_scl[:], in_=w2_gr[:])
             if has(p + 2):

@@ -128,21 +128,8 @@ def tile_supervisedrefiner_pb_t_kernel(
             else:
                 nc.vector.tensor_copy(out=out, in_=src)
 
-        def dummy(n):
-            for rep in range(n):
-                ps = psum.tile([P, D], F32, name="dum", tag="D1")
-                nc.tensor.matmul_mx(
-                    out=ps[:],
-                    lhsT=wo_cod[:, 0:P].bitcast(FP8X4),
-                    lhsT_scale=wo_scl[:, 0:P],
-                    rhs=wo_cod[:].bitcast(FP8X4),
-                    rhs_scale=wo_scl[:],
-                    start=True,
-                    stop=True,
-                )
-
-        def at(g):
-            st[g]["at"] = words_t(att[g], "D0")
+        def at(g, tag="D0"):
+            st[g]["at"] = words_t(att[g], tag)
 
         def p1(g):
             agr = work.tile([P, GW], BF16, name="agr", tag="agr", align_bytes=64)
@@ -315,29 +302,28 @@ def tile_supervisedrefiner_pb_t_kernel(
         wo_ps = [words_t(wo_raw[:, 0:GW], "A0"), words_t(wo_raw[:, GW : 2 * GW], "A1")]
         words_copy("s", wo_gr[:, 0:GW], wo_ps[0])
         words_copy("v", wo_gr[:, GW : 2 * GW], wo_ps[1])
-        at(0)
+        at(0, "D0")
+        p1(0)
         bo_ps = psum.tile([P, D], F32, name="bo_ps", tag="B0")
         nc.tensor.matmul(out=bo_ps[:], lhsT=ones16[:], rhs=bo_row[:], start=True, stop=True)
-        p1(0)
-        nc.vector.tensor_copy(out=bo_bc[:], in_=bo_ps[:])
+        at(1, "D1")
+        p1(1)
         nc.vector.quantize_mx(out=wo_cod[:].bitcast(FP8X4), scales=wo_scl[:], in_=wo_gr[:])
+        nc.vector.tensor_copy(out=bo_bc[:], in_=bo_ps[:])
         q1(0)
-        hb(0)
+        m1(0)
         bff_ps = psum.tile([P, D], F32, name="bff_ps", tag="B1")
         nc.tensor.matmul(out=bff_ps[:], lhsT=ones16[:], rhs=bff_row[:], start=True, stop=True)
         ln_ps = psum.tile([P, P], BF16, name="ln_ps", tag="C0")
         nc.tensor.transpose(ln_ps[:], lnrows[:], ident16[:])
-        dummy(4)
-        m1(0)
+        at(2, "D0")
+        for g in range(HB_AHEAD):
+            hb(g)
+            if g == 0:
+                q1(1)
+        p1(2)
         nc.scalar.copy(out=bff_bc[:], in_=bff_ps[:])
         nc.scalar.copy(out=gb8[:], in_=ln_ps[:, 0:8])
-        for g in range(1, HB_AHEAD):
-            hb(g)
-        at(1)
-        p1(1)
-        q1(1)
-        at(2)
-        p1(2)
 
         for p in range(PAIRS + 6):
             if has(p - 5):
@@ -358,11 +344,11 @@ def tile_supervisedrefiner_pb_t_kernel(
                 hm(p + 2)
             if has(p + 3):
                 at(p + 3)
-            if p == 0 or p == 1:
-                w2_ps = psum.tile([P, 4, 2 * P], BF16, name="w2_ps", tag="B%d" % p)
+            if 1 <= p <= 2:
+                w2_ps = psum.tile([P, 4, 2 * P], BF16, name="w2_ps", tag="B%d" % (p - 1))
                 for r2 in range(2):
                     for j in range(4):
-                        c0 = D * (2 * p + r2) + P * j
+                        c0 = D * (2 * (p - 1) + r2) + P * j
                         nc.tensor.transpose(w2_ps[:, j, P * r2 : P * r2 + P], w2_raw[:, c0 : c0 + P], ident16[:])
             if has(p - 3):
                 gbs(p - 3)
@@ -370,20 +356,20 @@ def tile_supervisedrefiner_pb_t_kernel(
                 sq(p)
             if has(p):
                 stats(p)
-            if p == 0 or p == 1:
-                w2_g3 = w2_gr[:].rearrange("p (f j) -> p f j", j=4)
-                nc.scalar.copy(
-                    out=w2_g3[:, 256 * p : 256 * p + 256, :], in_=w2_ps[:].rearrange("p j f -> p f j")
-                )
             if has(p + 3):
                 p1(p + 3)
             if has(p + 2):
                 hs(p + 2)
+            if 1 <= p <= 2:
+                w2_g3 = w2_gr[:].rearrange("p (f j) -> p f j", j=4)
+                nc.scalar.copy(
+                    out=w2_g3[:, 256 * (p - 1) : 256 * p, :], in_=w2_ps[:].rearrange("p j f -> p f j")
+                )
             if has(p - 4):
                 rg(p - 4)
             if has(p - 5):
                 hb4(p - 5)
-            if p == 1:
+            if p == 4:
                 nc.vector.quantize_mx(out=w2_cod[:].bitcast(FP8X4), scales=w2_scl[:], in_=w2_gr[:])
             if has(p + 2):
                 q1(p + 2)

@@ -19,8 +19,8 @@ GT = 2
 PAIRS = TILES // GT
 GW = GT * D
 LN_EPS = 1e-5
-H_BUFS = 5
-ON_PE = tuple(range(3, 14))
+H_BUFS = 6
+ON_PE = tuple(range(3, 13))
 HB_AHEAD = 3
 
 FLOPS = 2 * 2 * TOKENS * D * D
@@ -61,10 +61,10 @@ def tile_supervisedrefiner_pb_t_kernel(
         load_w(wo_raw, Wo, 0, 2)
         load_w(wo_raw, Wo, 2, 4)
         load_x(att, "att", att_v, 0, 1)
-        load_x(hid, "hid", hid_v, 0, 1)
         load_x(att, "att", att_v, 1, 1)
-        load_x(hid, "hid", hid_v, 1, 1)
+        load_x(hid, "hid", hid_v, 0, 1)
         load_x(att, "att", att_v, 2, 2)
+        load_x(hid, "hid", hid_v, 1, 1)
         load_x(hid, "hid", hid_v, 2, 2)
         load_w(w2_raw, W_ff1, 0, 4)
         for g in range(4, PAIRS, 2):
@@ -307,23 +307,23 @@ def tile_supervisedrefiner_pb_t_kernel(
         bo_ps = psum.tile([P, D], F32, name="bo_ps", tag="B0")
         nc.tensor.matmul(out=bo_ps[:], lhsT=ones16[:], rhs=bo_row[:], start=True, stop=True)
         at(1, "D1")
+        nc.scalar.copy(out=bo_bc[:], in_=bo_ps[:])
         p1(1)
-        nc.vector.quantize_mx(out=wo_cod[:].bitcast(FP8X4), scales=wo_scl[:], in_=wo_gr[:])
-        nc.vector.tensor_copy(out=bo_bc[:], in_=bo_ps[:])
+        for k in range(2):
+            half = slice(2 * P * k, 2 * P * (k + 1))
+            nc.vector.quantize_mx(
+                out=wo_cod[:, half].bitcast(FP8X4), scales=wo_scl[:, half], in_=wo_gr[:, GW * k : GW * (k + 1)]
+            )
         q1(0)
         m1(0)
+        at(2, "D0")
+        hb(0)
+        q1(1)
+        p1(2)
         bff_ps = psum.tile([P, D], F32, name="bff_ps", tag="B1")
         nc.tensor.matmul(out=bff_ps[:], lhsT=ones16[:], rhs=bff_row[:], start=True, stop=True)
         ln_ps = psum.tile([P, P], BF16, name="ln_ps", tag="C0")
         nc.tensor.transpose(ln_ps[:], lnrows[:], ident16[:])
-        at(2, "D0")
-        for g in range(HB_AHEAD):
-            hb(g)
-            if g == 0:
-                q1(1)
-        p1(2)
-        nc.scalar.copy(out=bff_bc[:], in_=bff_ps[:])
-        nc.scalar.copy(out=gb8[:], in_=ln_ps[:, 0:8])
 
         for p in range(PAIRS + 6):
             if has(p - 5):
@@ -334,8 +334,9 @@ def tile_supervisedrefiner_pb_t_kernel(
                 ge(p - 6)
             if has(p):
                 c4(p)
-            if 3 <= p + 2 < PAIRS:
-                hb(p + 2)
+            for g in (1, 2) if p == 0 else (p + 2,):
+                if has(g):
+                    hb(g)
             if has(p - 3):
                 xt(p - 3)
             if has(p + 1):
@@ -344,6 +345,9 @@ def tile_supervisedrefiner_pb_t_kernel(
                 hm(p + 2)
             if has(p + 3):
                 at(p + 3)
+            if p == 1:
+                nc.scalar.copy(out=bff_bc[:], in_=bff_ps[:])
+                nc.scalar.copy(out=gb8[:], in_=ln_ps[:, 0:8])
             if 1 <= p <= 2:
                 w2_ps = psum.tile([P, 4, 2 * P], BF16, name="w2_ps", tag="B%d" % (p - 1))
                 for r2 in range(2):

@@ -20,7 +20,7 @@ PAIRS = TILES // GT
 GW = GT * D
 LN_EPS = 1e-5
 H_BUFS = 6
-ON_PE = tuple(range(3, 13))
+ON_PE = tuple(range(3, 14))
 HB_AHEAD = 3
 
 FLOPS = 2 * 2 * TOKENS * D * D
@@ -80,9 +80,6 @@ def tile_supervisedrefiner_pb_t_kernel(
         nc.scalar.dma_start(out=lnrows[4:8, :], in_=ln2_b.rearrange("(j c) -> j c", c=P))
         zero1 = const.tile([P, 1], F32, name="zero1")
         nc.vector.memset(zero1[:], 0.0)
-        bff_row = const.tile([P, D], BF16, name="bff_row")
-        nc.vector.memset(bff_row[:], 0.0)
-        nc.scalar.dma_start(out=bff_row[0:1, :], in_=b_ff1.unsqueeze(0))
         warm = const.tile([P, 1], F32, name="warm")
         nc.scalar.activation(out=warm[:], in_=zero1[:], func=ACT.Gelu)
         ones16 = const.tile([P, P], BF16, name="ones16")
@@ -95,7 +92,8 @@ def tile_supervisedrefiner_pb_t_kernel(
         make_identity(nc, ident16[:])
 
         bo_bc = const.tile([P, D], BF16, name="bo_bc")
-        bff_bc = const.tile([P, D], F32, name="bff_bc")
+        bff_bc = const.tile([P, D], BF16, name="bff_bc")
+        nc.sync.dma_start(out=bff_bc[:], in_=b_ff1.partition_broadcast(P))
         gb8 = const.tile([P, 8], F32, name="gb8")
         wo_cod = const.tile([P, D], U32, name="wo_cod", align_bytes=64)
         wo_scl = const.tile([P, D], U8, name="wo_scl", align_bytes=64)
@@ -127,6 +125,19 @@ def tile_supervisedrefiner_pb_t_kernel(
                 nc.scalar.copy(out=out, in_=src)
             else:
                 nc.vector.tensor_copy(out=out, in_=src)
+
+        def dummy(n):
+            for rep in range(n):
+                ps = psum.tile([P, D], F32, name="dum", tag="D1")
+                nc.tensor.matmul_mx(
+                    out=ps[:],
+                    lhsT=wo_cod[:, 0:P].bitcast(FP8X4),
+                    lhsT_scale=wo_scl[:, 0:P],
+                    rhs=wo_cod[:].bitcast(FP8X4),
+                    rhs_scale=wo_scl[:],
+                    start=True,
+                    stop=True,
+                )
 
         def at(g, tag="D0"):
             st[g]["at"] = words_t(att[g], tag)
@@ -291,13 +302,11 @@ def tile_supervisedrefiner_pb_t_kernel(
 
         def ge(g):
             aa = st[g]["aa"]
-            for i in range(GT):
-                sl = slice(D * i, D * i + D)
-                nc.scalar.activation(out=aa[:, sl], in_=aa[:, sl], func=ACT.Gelu)
-                if g == PAIRS - 1:
-                    nc.sync.dma_start(out=o1_v[:, g * GW + D * i : g * GW + D * i + D], in_=aa[:, sl])
-            if g < PAIRS - 1:
-                nc.sync.dma_start(out=o1_v[:, g * GW : (g + 1) * GW], in_=aa[:])
+            n = GT if g == PAIRS - 1 else 1
+            w = GW // n
+            for k in range(n):
+                nc.scalar.activation(out=aa[:, w * k : w * k + w], in_=aa[:, w * k : w * k + w], func=ACT.Gelu)
+                nc.sync.dma_start(out=o1_v[:, g * GW + w * k : g * GW + w * k + w], in_=aa[:, w * k : w * k + w])
 
         wo_ps = [words_t(wo_raw[:, 0:GW], "A0"), words_t(wo_raw[:, GW : 2 * GW], "A1")]
         words_copy("s", wo_gr[:, 0:GW], wo_ps[0])
@@ -320,8 +329,6 @@ def tile_supervisedrefiner_pb_t_kernel(
         hb(0)
         q1(1)
         p1(2)
-        bff_ps = psum.tile([P, D], F32, name="bff_ps", tag="B1")
-        nc.tensor.matmul(out=bff_ps[:], lhsT=ones16[:], rhs=bff_row[:], start=True, stop=True)
         ln_ps = psum.tile([P, P], BF16, name="ln_ps", tag="C0")
         nc.tensor.transpose(ln_ps[:], lnrows[:], ident16[:])
 
@@ -330,8 +337,6 @@ def tile_supervisedrefiner_pb_t_kernel(
                 m2(p - 5)
             if has(p - 3):
                 xh(p - 3)
-            if has(p - 6):
-                ge(p - 6)
             if has(p):
                 c4(p)
             for g in (1, 2) if p == 0 else (p + 2,):
@@ -339,14 +344,15 @@ def tile_supervisedrefiner_pb_t_kernel(
                     hb(g)
             if has(p - 3):
                 xt(p - 3)
+            if p >= PAIRS:
+                dummy(2)
+            if has(p + 3):
+                at(p + 3)
             if has(p + 1):
                 m1(p + 1)
             if has(p + 2):
                 hm(p + 2)
-            if has(p + 3):
-                at(p + 3)
             if p == 1:
-                nc.scalar.copy(out=bff_bc[:], in_=bff_ps[:])
                 nc.scalar.copy(out=gb8[:], in_=ln_ps[:, 0:8])
             if 1 <= p <= 2:
                 w2_ps = psum.tile([P, 4, 2 * P], BF16, name="w2_ps", tag="B%d" % (p - 1))
@@ -369,6 +375,8 @@ def tile_supervisedrefiner_pb_t_kernel(
                 nc.scalar.copy(
                     out=w2_g3[:, 256 * (p - 1) : 256 * p, :], in_=w2_ps[:].rearrange("p j f -> p f j")
                 )
+            if has(p - 6):
+                ge(p - 6)
             if has(p - 4):
                 rg(p - 4)
             if has(p - 5):

@@ -126,9 +126,9 @@ def tile_supervisedrefiner_pb_t_kernel(
             else:
                 nc.vector.tensor_copy(out=out, in_=src)
 
-        def dummy(n):
+        def dummy(n, tag):
             for rep in range(n):
-                ps = psum.tile([P, D], F32, name="dum", tag="D1")
+                ps = psum.tile([P, D], F32, name="dum", tag=tag)
                 nc.tensor.matmul_mx(
                     out=ps[:],
                     lhsT=wo_cod[:, 0:P].bitcast(FP8X4),
@@ -308,6 +308,9 @@ def tile_supervisedrefiner_pb_t_kernel(
                 nc.scalar.activation(out=aa[:, w * k : w * k + w], in_=aa[:, w * k : w * k + w], func=ACT.Gelu)
                 nc.sync.dma_start(out=o1_v[:, g * GW + w * k : g * GW + w * k + w], in_=aa[:, w * k : w * k + w])
 
+        for rep in range(8):
+            ones_ps = psum.tile([P, P], F32, name="ones_ps", tag="C1")
+            nc.tensor.matmul(out=ones_ps[:], lhsT=ones16[:], rhs=ones16[:], start=True, stop=True)
         wo_ps = [words_t(wo_raw[:, 0:GW], "A0"), words_t(wo_raw[:, GW : 2 * GW], "A1")]
         words_copy("s", wo_gr[:, 0:GW], wo_ps[0])
         words_copy("v", wo_gr[:, GW : 2 * GW], wo_ps[1])
@@ -345,7 +348,7 @@ def tile_supervisedrefiner_pb_t_kernel(
             if has(p - 3):
                 xt(p - 3)
             if p >= PAIRS:
-                dummy(2)
+                dummy(2, "D1")
             if has(p + 3):
                 at(p + 3)
             if has(p + 1):
@@ -360,6 +363,8 @@ def tile_supervisedrefiner_pb_t_kernel(
                     for j in range(4):
                         c0 = D * (2 * (p - 1) + r2) + P * j
                         nc.tensor.transpose(w2_ps[:, j, P * r2 : P * r2 + P], w2_raw[:, c0 : c0 + P], ident16[:])
+            if p < 3:
+                dummy(2, "C1")
             if has(p - 3):
                 gbs(p - 3)
             if has(p):

from contextlib import ExitStack

import concourse.mybir as mybir
from concourse.masks import make_identity

F32 = mybir.dt.float32
BF16 = mybir.dt.bfloat16
U32 = mybir.dt.uint32
U8 = mybir.dt.uint8
FP8X4 = mybir.dt.float8_e4m3fn_x4
ALU = mybir.AluOpType
ACT = mybir.ActivationFunctionType

P = 128
D = 512
TOKENS = 4096
TILES = TOKENS // P
GT = 2
PAIRS = TILES // GT
GW = GT * D
LN_EPS = 1e-5
H_BUFS = 6
ON_PE = tuple(range(3, 14))
HB_AHEAD = 3

FLOPS = 2 * 2 * TOKENS * D * D


def tile_supervisedrefiner_pb_t_kernel(
    tc, attended, hidden, Wo, bo, ln2_g, ln2_b, W_ff1, b_ff1, out_0, out_1
):
    nc = tc.nc
    att_v = attended.flatten_outer_dims().rearrange("(p t) d -> p (t d)", t=TILES)
    hid_v = hidden.flatten_outer_dims().rearrange("(p t) d -> p (t d)", t=TILES)
    o0_v = out_0.flatten_outer_dims().rearrange("(p t) d -> p (t d)", t=TILES)
    o1_v = out_1.flatten_outer_dims().rearrange("(p t) d -> p (t d)", t=TILES)

    with ExitStack() as ctx:
        ctx.enter_context(tc.manual_schedule())
        const = ctx.enter_context(tc.tile_pool(name="const", bufs=1))
        work = ctx.enter_context(tc.tile_pool(name="work", bufs=2))
        psum = ctx.enter_context(tc.psum_pool(name="psum", bufs=1))

        wo_raw = const.tile([P, 4 * D], BF16, name="wo_raw")
        w2_raw = const.tile([P, 4 * D], BF16, name="w2_raw")
        att = {}
        hid = {}

        def load_w(dst, src, r0, r1):
            nc.sync.dma_start(
                out=dst[:, D * r0 : D * r1].rearrange("p (r k) -> p r k", k=D),
                in_=src[P * r0 : P * r1, :].rearrange("(r p) k -> p r k", p=P),
            )

        def load_x(dst, name, src, g0, n):
            t = const.tile([P, n * GW], BF16, name="%s%d" % (name, g0))
            nc.sync.dma_start(out=t[:], in_=src[:, g0 * GW : (g0 + n) * GW])
            for k in range(n):
                dst[g0 + k] = t[:, k * GW : (k + 1) * GW]

        load_w(wo_raw, Wo, 0, 2)
        load_w(wo_raw, Wo, 2, 4)
        load_x(att, "att", att_v, 0, 1)
        load_x(att, "att", att_v, 1, 1)
        load_x(hid, "hid", hid_v, 0, 1)
        load_x(att, "att", att_v, 2, 2)
        load_x(hid, "hid", hid_v, 1, 1)
        load_x(hid, "hid", hid_v, 2, 2)
        load_w(w2_raw, W_ff1, 0, 4)
        for g in range(4, PAIRS, 2):
            load_x(att, "att", att_v, g, 2)
            load_x(hid, "hid", hid_v, g, 2)

        bo_row = const.tile([P, D], BF16, name="bo_row")
        nc.vector.memset(bo_row[:], 0.0)
        nc.scalar.dma_start(out=bo_row[0:1, :], in_=bo.unsqueeze(0))
        lnrows = const.tile([P, P], BF16, name="lnrows")
        nc.vector.memset(lnrows[:], 0.0)
        nc.scalar.dma_start(out=lnrows[0:4, :], in_=ln2_g.rearrange("(j c) -> j c", c=P))
        nc.scalar.dma_start(out=lnrows[4:8, :], in_=ln2_b.rearrange("(j c) -> j c", c=P))
        zero1 = const.tile([P, 1], F32, name="zero1")
        nc.vector.memset(zero1[:], 0.0)
        warm = const.tile([P, 1], F32, name="warm")
        nc.scalar.activation(out=warm[:], in_=zero1[:], func=ACT.Gelu)
        ones16 = const.tile([P, P], BF16, name="ones16")
        nc.vector.memset(ones16[:], 1.0)
        neghalf = const.tile([P, GT], F32, name="neghalf")
        nc.vector.memset(neghalf[:], -0.5)
        ident32 = const.tile([P, P], F32, name="ident32")
        make_identity(nc, ident32[:])
        ident16 = const.tile([P, P], BF16, name="ident16")
        make_identity(nc, ident16[:])

        bo_bc = const.tile([P, D], BF16, name="bo_bc")
        bff_bc = const.tile([P, D], BF16, name="bff_bc")
        nc.sync.dma_start(out=bff_bc[:], in_=b_ff1.partition_broadcast(P))
        gb8 = const.tile([P, 8], F32, name="gb8")
        wo_cod = const.tile([P, D], U32, name="wo_cod", align_bytes=64)
        wo_scl = const.tile([P, D], U8, name="wo_scl", align_bytes=64)
        w2_cod = const.tile([P, D], U32, name="w2_cod", align_bytes=64)
        w2_scl = const.tile([P, D], U8, name="w2_scl", align_bytes=64)
        wo_gr = const.tile([P, 4 * D], BF16, name="wo_gr", align_bytes=64)
        w2_gr = const.tile([P, 4 * D], BF16, name="w2_gr", align_bytes=64)

        st = {}
        for g in range(PAIRS):
            st[g] = {}

        def has(g):
            return 0 <= g < PAIRS

        def words_t(src, tag):
            src32 = src.bitcast(F32)
            ps = psum.tile([P, 2, 2 * P], F32, name="words_ps", tag=tag)
            for i in range(2):
                for u in range(2):
                    c0 = 256 * i + P * u
                    nc.tensor.transpose(ps[:, u, P * i : P * i + P], src32[:, c0 : c0 + P], ident32[:])
            return ps

        def words_copy(eng, dst, ps):
            out = dst.bitcast(F32).rearrange("p (r u) -> p r u", u=2)
            src = ps[:].rearrange("p u r -> p r u")
            if eng == "s":
                nc.scalar.copy(out=out, in_=src)
            else:
                nc.vector.tensor_copy(out=out, in_=src)

        def dummy(n, tag):
            for rep in range(n):
                ps = psum.tile([P, D], F32, name="dum", tag=tag)
                nc.tensor.matmul_mx(
                    out=ps[:],
                    lhsT=wo_cod[:, 0:P].bitcast(FP8X4),
                    lhsT_scale=wo_scl[:, 0:P],
                    rhs=wo_cod[:].bitcast(FP8X4),
                    rhs_scale=wo_scl[:],
                    start=True,
                    stop=True,
                )

        def at(g, tag="D0"):
            st[g]["at"] = words_t(att[g], tag)

        def p1(g):
            agr = work.tile([P, GW], BF16, name="agr", tag="agr", align_bytes=64)
            words_copy("s", agr[:], st[g]["at"])
            st[g]["agr"] = agr

        def q1(g):
            acod = work.tile([P, GW // 4], U32, name="acod", tag="acod", bufs=3, align_bytes=64)
            ascl = work.tile([P, GW // 4], U8, name="ascl", tag="ascl", bufs=3, align_bytes=64)
            nc.vector.quantize_mx(out=acod[:].bitcast(FP8X4), scales=ascl[:], in_=st[g]["agr"][:])
            st[g]["acod"] = acod
            st[g]["ascl"] = ascl

        def hb(g):
            h = work.tile([P, GW], F32, name="h", tag="h", bufs=H_BUFS)
            st[g]["h"] = h
            for i in range(GT):
                if i == 1 and g in ON_PE:
                    continue
                sl = slice(D * i, D * i + D)
                eng = nc.vector if g < 2 or i else nc.gpsimd
                eng.tensor_tensor(out=h[:, sl], in0=hid[g][:, sl], in1=bo_bc[:], op=ALU.add)

        def hm(g):
            if g in ON_PE:
                ps = psum.tile([P, D], F32, name="hb_ps", tag="D1")
                nc.tensor.matmul(out=ps[:], lhsT=ident16[:], rhs=hid[g][:, D : 2 * D], start=True, stop=False)
                nc.tensor.matmul(out=ps[:], lhsT=ones16[:], rhs=bo_row[:], start=False, stop=True)
                st[g]["hb_ps"] = ps

        def hs(g):
            if g in ON_PE:
                nc.scalar.copy(out=st[g]["h"][:, D : 2 * D], in_=st[g]["hb_ps"][:])

        def mx2(g, cod, scl, w_cod, w_scl, tag):
            out = []
            for i in range(GT):
                cs = slice(P * i, P * i + P)
                ps = psum.tile([P, D], F32, name="mx_ps", tag="%s%d" % (tag, i))
                nc.tensor.matmul_mx(
                    out=ps[:],
                    lhsT=st[g][cod][:, cs].bitcast(FP8X4),
                    lhsT_scale=st[g][scl][:, cs],
                    rhs=w_cod[:].bitcast(FP8X4),
                    rhs_scale=w_scl[:],
                    start=True,
                    stop=True,
                )
                out.append(ps)
            return out

        def m1(g):
            st[g]["s1"] = mx2(g, "acod", "ascl", wo_cod, wo_scl, "A")

        def m2(g):
            st[g]["s2"] = mx2(g, "ncod", "nscl", w2_cod, w2_scl, "B")

        def c4(g):
            h = st[g]["h"]
            hsum = work.tile([P, GT], F32, name="hsum", tag="hsum", bufs=10)
            for i in range(GT):
                nc.vector.scalar_tensor_tensor(
                    out=h[:, D * i : D * i + D],
                    in0=st[g]["s1"][i][:],
                    scalar=1.0,
                    in1=h[:, D * i : D * i + D],
                    op0=ALU.mult,
                    op1=ALU.add,
                    accum_out=hsum[:, i : i + 1],
                )
            st[g]["hsum"] = hsum
            nc.sync.dma_start(out=o0_v[:, g * GW : (g + 1) * GW], in_=h[:])

        def sq(g):
            ssq = work.tile([P, GT], F32, name="ssq", tag="ssq", bufs=10)
            for i in range(GT):
                junk = work.tile([P, D], BF16, name="junk", tag="junk")
                nc.scalar.activation(
                    out=junk[:],
                    in_=st[g]["h"][:, D * i : D * i + D],
                    func=ACT.Square,
                    bias=st[g]["hsum"][:, i : i + 1],
                    scale=-float(D),
                    accum_out=ssq[:, i : i + 1],
                )
            st[g]["ssq"] = ssq

        def stats(g):
            negmean = work.tile([P, GT], F32, name="negmean", tag="negmean", bufs=10)
            nc.gpsimd.tensor_scalar(
                out=negmean[:], in0=st[g]["hsum"][:], scalar1=-1.0 / D, scalar2=0.0, op0=ALU.mult, op1=ALU.add
            )
            veps = work.tile([P, GT], F32, name="veps", tag="veps", bufs=10)
            nc.gpsimd.tensor_scalar(
                out=veps[:], in0=st[g]["ssq"][:], scalar1=1.0 / D**3, scalar2=LN_EPS, op0=ALU.mult, op1=ALU.add
            )
            rstd = work.tile([P, GT], F32, name="rstd", tag="rstd", bufs=10)
            nc.gpsimd.tensor_tensor(out=rstd[:], in0=veps[:], in1=neghalf[:], op=ALU.pow)
            st[g]["negmean"] = negmean
            st[g]["rstd"] = rstd

        def xh(g):
            x = work.tile([P, GW], F32, name="xh", tag="xh", bufs=3)
            for i in range(GT):
                nc.vector.tensor_scalar(
                    out=x[:, D * i : D * i + D],
                    in0=st[g]["h"][:, D * i : D * i + D],
                    scalar1=st[g]["negmean"][:, i : i + 1],
                    scalar2=st[g]["rstd"][:, i : i + 1],
                    op0=ALU.add,
                    op1=ALU.mult,
                )
            st[g]["xh"] = x

        def xt(g):
            st[g]["xt"] = []
            for b in range(2):
                ps = psum.tile([P, 2, GT * P], F32, name="xt_ps", tag="C%d" % b)
                for j2 in range(2):
                    for i in range(GT):
                        c0 = D * i + P * (2 * b + j2)
                        nc.tensor.transpose(ps[:, j2, P * i : P * i + P], st[g]["xh"][:, c0 : c0 + P], ident32[:])
                st[g]["xt"].append(ps)

        def gbs(g):
            n_t = work.tile([P, 4, GT * P], BF16, name="n_t", tag="n_t", bufs=3)
            for j in range(4):
                nc.scalar.activation(
                    out=n_t[:, j, :],
                    in_=st[g]["xt"][j // 2][:, j % 2, :],
                    func=ACT.Identity,
                    scale=gb8[:, j : j + 1],
                    bias=gb8[:, 4 + j : 5 + j],
                )
            st[g]["n_t"] = n_t

        def rg(g):
            ngr = work.tile([P, GW], BF16, name="ngr", tag="ngr", align_bytes=64)
            nc.vector.tensor_copy(
                out=ngr[:].rearrange("p (c i t) -> p c t i", i=4, t=4),
                in_=st[g]["n_t"][:].rearrange("p t (c i) -> p c t i", i=4),
            )
            st[g]["ngr"] = ngr

        def q2(g):
            ncod = work.tile([P, GW // 4], U32, name="ncod", tag="ncod", align_bytes=64)
            nscl = work.tile([P, GW // 4], U8, name="nscl", tag="nscl", align_bytes=64)
            nc.vector.quantize_mx(out=ncod[:].bitcast(FP8X4), scales=nscl[:], in_=st[g]["ngr"][:])
            st[g]["ncod"] = ncod
            st[g]["nscl"] = nscl

        def hb4(g):
            aa = work.tile([P, GW], F32, name="aa", tag="aa", bufs=4)
            for i in range(GT):
                nc.vector.tensor_tensor(
                    out=aa[:, D * i : D * i + D], in0=st[g]["s2"][i][:], in1=bff_bc[:], op=ALU.add
                )
            st[g]["aa"] = aa

        def ge(g):
            aa = st[g]["aa"]
            n = GT if g == PAIRS - 1 else 1
            w = GW // n
            for k in range(n):
                nc.scalar.activation(out=aa[:, w * k : w * k + w], in_=aa[:, w * k : w * k + w], func=ACT.Gelu)
                nc.sync.dma_start(out=o1_v[:, g * GW + w * k : g * GW + w * k + w], in_=aa[:, w * k : w * k + w])

        for rep in range(8):
            ones_ps = psum.tile([P, P], F32, name="ones_ps", tag="C1")
            nc.tensor.matmul(out=ones_ps[:], lhsT=ones16[:], rhs=ones16[:], start=True, stop=True)
        wo_ps = [words_t(wo_raw[:, 0:GW], "A0"), words_t(wo_raw[:, GW : 2 * GW], "A1")]
        words_copy("s", wo_gr[:, 0:GW], wo_ps[0])
        words_copy("v", wo_gr[:, GW : 2 * GW], wo_ps[1])
        at(0, "D0")
        p1(0)
        bo_ps = psum.tile([P, D], F32, name="bo_ps", tag="B0")
        nc.tensor.matmul(out=bo_ps[:], lhsT=ones16[:], rhs=bo_row[:], start=True, stop=True)
        at(1, "D1")
        nc.scalar.copy(out=bo_bc[:], in_=bo_ps[:])
        p1(1)
        for k in range(2):
            half = slice(2 * P * k, 2 * P * (k + 1))
            nc.vector.quantize_mx(
                out=wo_cod[:, half].bitcast(FP8X4), scales=wo_scl[:, half], in_=wo_gr[:, GW * k : GW * (k + 1)]
            )
        q1(0)
        m1(0)
        at(2, "D0")
        hb(0)
        q1(1)
        p1(2)
        ln_ps = psum.tile([P, P], BF16, name="ln_ps", tag="C0")
        nc.tensor.transpose(ln_ps[:], lnrows[:], ident16[:])

        for p in range(PAIRS + 6):
            if has(p - 5):
                m2(p - 5)
            if has(p - 3):
                xh(p - 3)
            if has(p):
                c4(p)
            for g in (1, 2) if p == 0 else (p + 2,):
                if has(g):
                    hb(g)
            if has(p - 3):
                xt(p - 3)
            if p >= PAIRS:
                dummy(2, "D1")
            if has(p + 3):
                at(p + 3)
            if has(p + 1):
                m1(p + 1)
            if has(p + 2):
                hm(p + 2)
            if p == 1:
                nc.scalar.copy(out=gb8[:], in_=ln_ps[:, 0:8])
            if 1 <= p <= 2:
                w2_ps = psum.tile([P, 4, 2 * P], BF16, name="w2_ps", tag="B%d" % (p - 1))
                for r2 in range(2):
                    for j in range(4):
                        c0 = D * (2 * (p - 1) + r2) + P * j
                        nc.tensor.transpose(w2_ps[:, j, P * r2 : P * r2 + P], w2_raw[:, c0 : c0 + P], ident16[:])
            if p < 3:
                dummy(2, "C1")
            if has(p - 3):
                gbs(p - 3)
            if has(p):
                sq(p)
            if has(p):
                stats(p)
            if has(p + 3):
                p1(p + 3)
            if has(p + 2):
                hs(p + 2)
            if 1 <= p <= 2:
                w2_g3 = w2_gr[:].rearrange("p (f j) -> p f j", j=4)
                nc.scalar.copy(
                    out=w2_g3[:, 256 * (p - 1) : 256 * p, :], in_=w2_ps[:].rearrange("p j f -> p f j")
                )
            if has(p - 6):
                ge(p - 6)
            if has(p - 4):
                rg(p - 4)
            if has(p - 5):
                hb4(p - 5)
            if p == 4:
                nc.vector.quantize_mx(out=w2_cod[:].bitcast(FP8X4), scales=w2_scl[:], in_=w2_gr[:])
            if has(p + 2):
                q1(p + 2)
            if has(p - 4):
                q2(p - 4)
